import numpy as np
import ml_dtypes


def mxq(x, axis, fmt="e4m3"):
    dtype, down = {"e4m3": (ml_dtypes.float8_e4m3fn, 7), "e5m2": (ml_dtypes.float8_e5m2, 14)}[fmt]
    v = np.moveaxis(np.asarray(x, np.float32).astype(ml_dtypes.bfloat16).astype(np.float64), axis, -1)
    blocks = v.reshape(v.shape[:-1] + (-1, 32))
    amax = np.abs(blocks).max(-1, keepdims=True)
    byte = np.maximum(np.where(amax > 0, np.frexp(amax)[1] - 1 + 127, 0) - down, 1)
    scale = np.exp2(byte - 127.0)
    codes = (blocks / scale).astype(np.float32).astype(dtype).astype(np.float64)
    return np.moveaxis((codes * scale).reshape(v.shape), -1, axis)


WIDE = False


def mx_kscale(k):
    if not WIDE:
        return np.ones(k)
    levels = np.array([10, -10, 5, -5, 0])
    a = np.random.permutation(np.resize(levels, k // 512 * 4)).reshape(k // 512, 4)
    idx = np.arange(k)
    return np.exp2(a[idx // 512, idx % 128 // 32])


BF16 = ml_dtypes.bfloat16


def bf(x):
    return np.asarray(x, np.float32).astype(BF16)


def f64(x):
    return np.asarray(x).astype(np.float64)


E2M1 = np.array([0.0, 0.5, 1.0, 1.5, 2.0, 3.0, 4.0, 6.0, -0.0, -0.5, -1.0, -1.5, -2.0, -3.0, -4.0, -6.0])


def pack_weight(w, fmt):
    k, n = w.shape
    w = f64(bf(w)).reshape(k // 32, 32, n)
    amax = np.abs(w).max(1)
    if fmt == "e4m3":
        byte = np.frexp(amax)[1] - 1 + 127 - 7
    else:
        mant, ex = np.frexp(amax / 6.0)
        byte = np.where(mant > 0.5, ex, ex - 1) + 127
    byte = np.clip(np.where(amax > 0, byte, 1), 1, 254)
    scaled = (w * np.exp2(127.0 - byte)[:, None, :]).reshape(k, n).astype(np.float32)
    by_word = np.ascontiguousarray(scaled.reshape(k // 512, 128, 4, n).transpose(0, 1, 3, 2))
    if fmt == "e4m3":
        words = by_word.astype(ml_dtypes.float8_e4m3fn).view(np.uint8)
    else:
        c = by_word.astype(ml_dtypes.float4_e2m1fn).view(np.uint8) & 0xF
        words = c[..., 0::2] | (c[..., 1::2] << 4)
    return np.ascontiguousarray(words), np.ascontiguousarray(byte.astype(np.uint8).reshape(k // 512, 16, n))


def unpack_weight(words, scales, fmt):
    g, p, n, _ = words.shape
    if fmt == "e4m3":
        vals = np.ascontiguousarray(words).view(ml_dtypes.float8_e4m3fn).astype(np.float64)
    else:
        nib = np.empty((g, p, n, 4), np.uint8)
        nib[..., 0::2] = words & 0xF
        nib[..., 1::2] = words >> 4
        vals = E2M1[nib]
    vals = vals * np.repeat(np.exp2(scales.astype(np.float64) - 127.0), 8, axis=1)[..., None]
    return vals.transpose(0, 1, 3, 2).reshape(g * 512, n)


N, F, U, G, P = 512, 2048, 512, 5, 3
C = G + P
T = G + 2 * P + 1
LO, HI = -1.0, 1.0
LN_EPS = 0.001
FMT = "e4m3"


def b_splines(x, grid):
    xe = x[..., None]
    bases = np.where((xe >= grid[..., :-1]) & (xe < grid[..., 1:]), 1.0, 0.0)
    for k in range(1, P + 1):
        left = (xe - grid[..., :-(k + 1)]) / (grid[..., k:-1] - grid[..., :-(k + 1)])
        right = (grid[..., k + 1:] - xe) / (grid[..., k + 1:] - grid[..., 1:-k])
        bases = left * bases[..., :-1] + right * bases[..., 1:]
    return bases.reshape(x.shape[0], -1)


def setup_inputs():
    t = mx_kscale(F)
    h = (HI - LO) / G
    knots = np.linspace(LO - P * h, LO + (G + P) * h, T)
    grid = knots[None, None, :] + (np.random.random_sample((1, F, T)) - 0.5) * 0.25 * h
    x = bf(np.random.standard_normal((N, F)) * 0.1 + np.random.standard_normal((N, 1)) * 0.1)
    ln_gamma = bf((1.0 + 0.1 * np.random.standard_normal(F)) * t)
    ln_beta = bf(0.1 * np.random.standard_normal(F) * t)
    base_weight_words, base_weight_scales = pack_weight(np.random.standard_normal((F, U)) / np.sqrt(F) / t[:, None], FMT)
    base_bias = bf(0.25 * np.random.standard_normal(U))
    spline_weight_words, spline_weight_scales = pack_weight(np.random.standard_normal((F * C, U)) / np.sqrt(F), FMT)
    return {
        "x": x,
        "ln_gamma": ln_gamma,
        "ln_beta": ln_beta,
        "base_weight_words": base_weight_words,
        "base_weight_scales": base_weight_scales,
        "base_bias": base_bias,
        "spline_weight_words": spline_weight_words,
        "spline_weight_scales": spline_weight_scales,
        "grid": bf(grid * t[None, :, None]),
    }


def reference(x, ln_gamma, ln_beta, base_weight_words, base_weight_scales, base_bias, spline_weight_words, spline_weight_scales, grid):
    x = f64(x)
    mean = x.mean(-1, keepdims=True)
    var = x.var(-1, keepdims=True)
    xn = (x - mean) / np.sqrt(var + LN_EPS) * f64(ln_gamma) + f64(ln_beta)
    base_out = (mxq(np.maximum(xn, 0.0), 1, "e4m3") @ unpack_weight(base_weight_words, base_weight_scales, FMT)) + f64(base_bias)
    spline_out = mxq(b_splines(xn, f64(grid)), 1, "e4m3") @ unpack_weight(spline_weight_words, spline_weight_scales, FMT)
    return base_out + spline_out

@@ -1,0 +1,311 @@
+import concourse.mybir as mybir
+from concourse.masks import make_identity
+
+F32 = mybir.dt.float32
+BF16 = mybir.dt.bfloat16
+I32 = mybir.dt.int32
+U32 = mybir.dt.uint32
+U8 = mybir.dt.uint8
+FP8X4 = mybir.dt.float8_e4m3fn_x4
+ALU = mybir.AluOpType
+ACT = mybir.ActivationFunctionType
+
+P = 128
+ROWS = 512
+ROW_TILES = ROWS // P
+FEATURES = 2048
+UNITS = 512
+PACK = 4
+K_PASS = P * PACK
+BASES = 8
+HALF = 4
+LOCAL_KNOTS = 8
+BASE_PASSES = FEATURES // K_PASS
+GROUPS = FEATURES * BASES // K_PASS
+GROUP_FEATURES = K_PASS // BASES
+LN_EPS = 0.001
+
+FLOPS = 2 * ROWS * (FEATURES + FEATURES * BASES) * UNITS
+
+
+def refined_rsqrt(nc, pool, result, value, shape, label):
+    root = pool.tile(shape, F32, name=label + "_root")
+    nc.scalar.activation(out=root[:], in_=value, func=ACT.Sqrt)
+    guess = pool.tile(shape, F32, name=label + "_guess")
+    nc.vector.reciprocal(out=guess[:], in_=root[:])
+    step = pool.tile(shape, F32, name=label + "_step")
+    nc.vector.tensor_tensor(out=step[:], in0=value, in1=guess[:], op=ALU.mult)
+    nc.vector.tensor_tensor(out=step[:], in0=step[:], in1=guess[:], op=ALU.mult)
+    nc.vector.tensor_scalar(out=step[:], in0=step[:], scalar1=-0.5, scalar2=1.5, op0=ALU.mult, op1=ALU.add)
+    nc.vector.tensor_tensor(out=result, in0=guess[:], in1=step[:], op=ALU.mult)
+
+
+def tile_kanlinear_pa_k_kernel(
+    tc,
+    x,
+    ln_gamma,
+    ln_beta,
+    base_weight_words,
+    base_weight_scales,
+    base_bias,
+    spline_weight_words,
+    spline_weight_scales,
+    grid,
+    out,
+):
+    nc = tc.nc
+    with tc.tile_pool(name="keep", bufs=1) as keep, tc.tile_pool(name="weights", bufs=4) as weights, tc.psum_pool(
+        name="sums", bufs=1
+    ) as sums, tc.psum_pool(name="turned", bufs=2) as turned:
+        ident_f32 = keep.tile([P, P], F32)
+        make_identity(nc, ident_f32[:])
+        ident_bf16 = keep.tile([P, P], BF16)
+        make_identity(nc, ident_bf16[:])
+
+        scale_planes = keep.tile([P, BASE_PASSES + GROUPS, UNITS], U8, align_bytes=64)
+        nc.vector.memset(scale_planes[:].bitcast(I32), 0)
+
+        xn_twice = [keep.tile([P, 2 * FEATURES], F32, name="xn_twice%d" % r) for r in range(ROW_TILES)]
+        knots = keep.tile([P, GROUPS, LOCAL_KNOTS], F32)
+        slope = keep.tile([P, GROUPS, LOCAL_KNOTS], F32)
+        shift = keep.tile([P, GROUPS, LOCAL_KNOTS], F32)
+        left_weight = keep.tile([P, GROUPS, HALF], F32)
+        right_weight = keep.tile([P, GROUPS, HALF], F32)
+        bias_rows = keep.tile([P, UNITS], BF16)
+        acc = [sums.tile([P, UNITS], F32, name="acc%d" % r) for r in range(ROW_TILES)]
+
+        with tc.tile_pool(name="head", bufs=1) as head, tc.tile_pool(name="head2", bufs=2) as head2:
+            x_rows = [head.tile([P, FEATURES], BF16, name="x_rows%d" % r) for r in range(ROW_TILES)]
+            for r in range(ROW_TILES):
+                nc.sync.dma_start(out=x_rows[r][:], in_=x[r * P : (r + 1) * P, :])
+            gamma_rows = head.tile([P, FEATURES], BF16)
+            nc.scalar.dma_start(out=gamma_rows[:], in_=ln_gamma.partition_broadcast(P))
+            beta_rows = head.tile([P, FEATURES], BF16)
+            nc.scalar.dma_start(out=beta_rows[:], in_=ln_beta.partition_broadcast(P))
+            knots_bf16 = head.tile([P, GROUPS, LOCAL_KNOTS], BF16)
+            grid_by_group = grid[0].rearrange("(g f) i -> f g i", f=GROUP_FEATURES)
+            for h in range(2):
+                nc.scalar.dma_start(
+                    out=knots_bf16[h:P:2, :, :], in_=grid_by_group[:, :, HALF * h : HALF * h + LOCAL_KNOTS]
+                )
+            nc.scalar.dma_start(out=bias_rows[:], in_=base_bias.partition_broadcast(P))
+            for q in range(4):
+                nc.sync.dma_start(
+                    out=scale_planes[32 * q : 32 * q + 4, 0:BASE_PASSES, :].bitcast(I32),
+                    in_=base_weight_scales[:, 4 * q : 4 * q + 4, :].rearrange("g r n -> r g n").bitcast(I32),
+                )
+                nc.sync.dma_start(
+                    out=scale_planes[32 * q : 32 * q + 4, BASE_PASSES:, :].bitcast(I32),
+                    in_=spline_weight_scales[:, 4 * q : 4 * q + 4, :].rearrange("g r n -> r g n").bitcast(I32),
+                )
+
+            nc.gpsimd.tensor_copy(out=knots[:], in_=knots_bf16[:])
+            gap = {}
+            for span in (1, 2, 3, 4):
+                count = LOCAL_KNOTS - span
+                gap[span] = head.tile([P, GROUPS, count], F32, name="gap%d" % span)
+                nc.gpsimd.tensor_tensor(
+                    out=gap[span][:], in0=knots[:, :, span:LOCAL_KNOTS], in1=knots[:, :, 0:count], op=ALU.subtract
+                )
+            rise = head.tile([P, GROUPS, 5], F32)
+            nc.gpsimd.tensor_tensor(out=rise[:], in0=gap[1][:, :, 0:5], in1=gap[2][:, :, 0:5], op=ALU.mult)
+            nc.gpsimd.tensor_tensor(out=rise[:], in0=rise[:], in1=gap[3][:, :, 0:5], op=ALU.mult)
+            fall = head.tile([P, GROUPS, 5], F32)
+            nc.gpsimd.tensor_tensor(out=fall[:], in0=gap[1][:, :, 2:7], in1=gap[2][:, :, 1:6], op=ALU.mult)
+            nc.gpsimd.tensor_tensor(out=fall[:], in0=fall[:], in1=gap[3][:, :, 0:5], op=ALU.mult)
+            volume = head.tile([P, GROUPS, LOCAL_KNOTS], F32)
+            nc.gpsimd.tensor_copy(out=volume[:, :, 0:HALF], in_=rise[:, :, 0:HALF])
+            nc.gpsimd.tensor_copy(out=volume[:, :, HALF:LOCAL_KNOTS], in_=fall[:, :, 1:5])
+            refined_rsqrt(nc, head, slope[:], volume[:], [P, GROUPS, LOCAL_KNOTS], "slope")
+            nc.vector.scalar_tensor_tensor(
+                out=shift[:], in0=slope[:], scalar=-1.0, in1=knots[:], op0=ALU.mult, op1=ALU.mult
+            )
+            for weight, sign, first, outer in ((left_weight, 1.0, 1, rise[:, :, 1:5]), (right_weight, -1.0, 3, fall[:, :, 0:4])):
+                edge = 0 if first == 1 else 3
+                top = head.tile([P, GROUPS, HALF], F32, name="top%d" % first)
+                nc.gpsimd.tensor_tensor(out=top[:], in0=gap[4][:], in1=volume[:, :, first : first + HALF], op=ALU.mult)
+                bottom = head.tile([P, GROUPS, HALF], F32, name="bottom%d" % first)
+                nc.gpsimd.tensor_tensor(out=bottom[:], in0=gap[1][:, :, edge : edge + HALF], in1=outer, op=ALU.mult)
+                nc.vector.reciprocal(out=bottom[:], in_=bottom[:])
+                nc.vector.scalar_tensor_tensor(
+                    out=weight[:], in0=top[:], scalar=sign, in1=bottom[:], op0=ALU.mult, op1=ALU.mult
+                )
+
+            moments = head.tile([P, ROW_TILES, 2], F32)
+            for r in range(ROW_TILES):
+                chunks = head2.tile([P, 4, 6], F32, name="chunks")
+                for c in range(4):
+                    nc.vector.bn_stats(out=chunks[:, c, :], in_=x_rows[r][:, c * 512 : (c + 1) * 512])
+                nc.vector.bn_aggr(out=moments[:, r, :], in_=chunks[:].rearrange("p c s -> p (c s)"))
+            spread = head.tile([P, ROW_TILES], F32)
+            nc.vector.tensor_scalar_add(out=spread[:], in0=moments[:, :, 1], scalar1=LN_EPS)
+            rstd = head.tile([P, ROW_TILES], F32)
+            refined_rsqrt(nc, head, rstd[:], spread[:], [P, ROW_TILES], "rstd")
+            relu_rows = []
+            for r in range(ROW_TILES):
+                centred = head2.tile([P, FEATURES], F32, name="centred")
+                nc.vector.scalar_tensor_tensor(
+                    out=centred[:],
+                    in0=x_rows[r][:],
+                    scalar=moments[:, r, 0:1],
+                    in1=gamma_rows[:],
+                    op0=ALU.subtract,
+                    op1=ALU.mult,
+                )
+                nc.vector.scalar_tensor_tensor(
+                    out=xn_twice[r][:].rearrange("n (f h) -> n f h", h=2),
+                    in0=centred[:].unsqueeze(2).to_broadcast([P, FEATURES, 2]),
+                    scalar=rstd[:, r : r + 1],
+                    in1=beta_rows[:].unsqueeze(2).to_broadcast([P, FEATURES, 2]),
+                    op0=ALU.mult,
+                    op1=ALU.add,
+                )
+                relu_row = head.tile([P, FEATURES], BF16, name="relu_rows%d" % r)
+                nc.scalar.activation(
+                    out=relu_row[:].rearrange("n (g t p) -> n g t p", g=BASE_PASSES, t=PACK),
+                    in_=xn_twice[r][:].rearrange("n (g p t h) -> n g t p h", g=BASE_PASSES, p=P, t=PACK, h=2)[
+                        :, :, :, :, 0
+                    ],
+                    func=ACT.Relu,
+                )
+                relu_rows.append(relu_row)
+
+            for g in range(BASE_PASSES):
+                w_words = weights.tile([P, PACK * UNITS], U8, name="w_words", align_bytes=64)
+                nc.sync.dma_start(
+                    out=w_words[:].bitcast(I32), in_=base_weight_words[g].rearrange("p n t -> p (n t)").bitcast(I32)
+                )
+                grouped = head2.tile([P, ROWS, PACK], BF16, name="grouped", align_bytes=64)
+                for pair in range(2):
+                    flipped = turned.tile([P, PACK, 2 * P], BF16, name="flipped", tag="for_scalar")
+                    for t in range(PACK):
+                        for b in range(2):
+                            nc.tensor.transpose(
+                                flipped[:, t, b * P : (b + 1) * P],
+                                relu_rows[2 * pair + b][:, g * K_PASS + t * P : g * K_PASS + (t + 1) * P],
+                                ident_bf16[:],
+                            )
+                    nc.scalar.copy(
+                        out=grouped[:, pair * 2 * P : (pair + 1) * 2 * P, :], in_=flipped[:].rearrange("p t n -> p n t")
+                    )
+                a_words = head2.tile([P, ROWS], U32, name="a_words", align_bytes=64)
+                a_scales = head2.tile([P, ROWS], U8, name="a_scales", align_bytes=64)
+                nc.vector.quantize_mx(
+                    out=a_words[:].bitcast(FP8X4), scales=a_scales[:], in_=grouped[:].rearrange("p n t -> p (n t)")
+                )
+                for r in range(ROW_TILES):
+                    nc.tensor.matmul_mx(
+                        out=acc[r][:],
+                        lhsT=a_words[:, r * P : (r + 1) * P].bitcast(FP8X4),
+                        lhsT_scale=a_scales[:, r * P : (r + 1) * P],
+                        rhs=w_words[:].bitcast(FP8X4),
+                        rhs_scale=scale_planes[:, g, :],
+                        start=(g == 0),
+                        stop=False,
+                    )
+
+        with tc.tile_pool(name="squares", bufs=LOCAL_KNOTS) as squares, tc.tile_pool(name="work", bufs=2) as work:
+
+            def load_weights(g):
+                w_words = weights.tile([P, PACK * UNITS], U8, name="w_words", align_bytes=64)
+                nc.sync.dma_start(
+                    out=w_words[:].bitcast(I32), in_=spline_weight_words[g].rearrange("p n t -> p (n t)").bitcast(I32)
+                )
+                return w_words
+
+            def turn(g):
+                v_scalar = turned.tile([P, ROWS], F32, name="v_scalar", tag="for_scalar")
+                v_vector = turned.tile([P, ROWS], F32, name="v_vector", tag="for_vector")
+                for bank in (v_scalar, v_vector):
+                    for r in range(ROW_TILES):
+                        nc.tensor.transpose(
+                            bank[:, r * P : (r + 1) * P], xn_twice[r][:, g * P : (g + 1) * P], ident_f32[:]
+                        )
+                return v_scalar, v_vector
+
+            def cube(g, v_scalar, v_vector):
+                cubes = work.tile([P, LOCAL_KNOTS, ROWS], F32, name="cubes")
+                for i in range(LOCAL_KNOTS):
+                    square = squares.tile([P, ROWS], F32, name="square")
+                    nc.scalar.activation(
+                        out=square[:],
+                        in_=v_scalar[:],
+                        func=ACT.Square,
+                        scale=slope[:, g, i : i + 1],
+                        bias=shift[:, g, i : i + 1],
+                    )
+                    nc.vector.scalar_tensor_tensor(
+                        out=cubes[:, i, :],
+                        in0=v_vector[:],
+                        scalar=knots[:, g, i : i + 1],
+                        in1=square[:],
+                        op0=ALU.subtract,
+                        op1=ALU.mult,
+                    )
+                inner = work.tile([P, 2 * HALF, ROWS], F32, name="inner")
+                for t in range(HALF):
+                    nc.scalar.activation(
+                        out=inner[:, t, :], in_=cubes[:, t + 1, :], func=ACT.Relu, scale=left_weight[:, g, t : t + 1]
+                    )
+                for t in range(HALF):
+                    nc.scalar.activation(
+                        out=inner[:, HALF + t, :],
+                        in_=cubes[:, t + 3, :],
+                        func=ACT.Relu,
+                        scale=right_weight[:, g, t : t + 1],
+                    )
+                return cubes, inner
+
+            def finish(g, cubes, inner, w_words):
+                left = work.tile([P, HALF, ROWS], F32, name="left")
+                nc.vector.tensor_tensor(out=left[:], in0=cubes[:, 0:HALF, :], in1=inner[:, 0:HALF, :], op=ALU.subtract)
+                right = work.tile([P, HALF, ROWS], F32, name="right")
+                nc.vector.scalar_tensor_tensor(
+                    out=right[:],
+                    in0=cubes[:, HALF:, :],
+                    scalar=-1.0,
+                    in1=inner[:, HALF:, :],
+                    op0=ALU.mult,
+                    op1=ALU.subtract,
+                )
+                basis = work.tile([P, ROWS, HALF], BF16, name="basis", align_bytes=64)
+                nc.vector.scalar_tensor_tensor(
+                    out=basis[:],
+                    in0=left[:].rearrange("p t n -> p n t"),
+                    scalar=0.0,
+                    in1=right[:].rearrange("p t n -> p n t"),
+                    op0=ALU.max,
+                    op1=ALU.max,
+                )
+                b_words = work.tile([P, ROWS], U32, name="b_words", align_bytes=64)
+                b_scales = work.tile([P, ROWS], U8, name="b_scales", align_bytes=64)
+                nc.vector.quantize_mx(
+                    out=b_words[:].bitcast(FP8X4), scales=b_scales[:], in_=basis[:].rearrange("p n t -> p (n t)")
+                )
+                for r in range(ROW_TILES):
+                    nc.tensor.matmul_mx(
+                        out=acc[r][:],
+                        lhsT=b_words[:, r * P : (r + 1) * P].bitcast(FP8X4),
+                        lhsT_scale=b_scales[:, r * P : (r + 1) * P],
+                        rhs=w_words[:].bitcast(FP8X4),
+                        rhs_scale=scale_planes[:, BASE_PASSES + g, :],
+                        start=False,
+                        stop=(g == GROUPS - 1),
+                    )
+
+            with tc.manual_schedule():
+                w_of = {0: load_weights(0), 1: load_weights(1)}
+                v_of = {0: turn(0), 1: turn(1)}
+                made = {0: cube(0, v_of[0][0], v_of[0][1])}
+                for g in range(GROUPS):
+                    if g + 2 < GROUPS:
+                        w_of[g + 2] = load_weights(g + 2)
+                        v_of[g + 2] = turn(g + 2)
+                    if g + 1 < GROUPS:
+                        made[g + 1] = cube(g + 1, v_of[g + 1][0], v_of[g + 1][1])
+                    finish(g, made[g][0], made[g][1], w_of[g])
+
+                for r in range(ROW_TILES):
+                    result = work.tile([P, UNITS], F32, name="result")
+                    nc.vector.tensor_tensor(out=result[:], in0=acc[r][:], in1=bias_rows[:], op=ALU.add)
+                    nc.sync.dma_start(out=out[r * P : (r + 1) * P, :], in_=result[:])

@@ -258,7 +258,7 @@ def tile_kanlinear_pa_k_kernel(
 
             def finish(g, cubes, inner, w_words):
                 left = work.tile([P, HALF, ROWS], F32, name="left")
-                nc.vector.tensor_tensor(out=left[:], in0=cubes[:, 0:HALF, :], in1=inner[:, 0:HALF, :], op=ALU.subtract)
+                nc.gpsimd.tensor_tensor(out=left[:], in0=cubes[:, 0:HALF, :], in1=inner[:, 0:HALF, :], op=ALU.subtract)
                 right = work.tile([P, HALF, ROWS], F32, name="right")
                 nc.vector.scalar_tensor_tensor(
                     out=right[:],

@@ -256,10 +256,10 @@ def tile_kanlinear_pa_k_kernel(
                     )
                 return cubes, inner
 
-            def finish(g, cubes, inner, w_words):
-                left = work.tile([P, HALF, ROWS], F32, name="left")
-                nc.gpsimd.tensor_tensor(out=left[:], in0=cubes[:, 0:HALF, :], in1=inner[:, 0:HALF, :], op=ALU.subtract)
-                right = work.tile([P, HALF, ROWS], F32, name="right")
+            def merge(g, cubes, inner):
+                left = work.tile([P, HALF, ROWS], BF16, name="left")
+                nc.vector.tensor_tensor(out=left[:], in0=cubes[:, 0:HALF, :], in1=inner[:, 0:HALF, :], op=ALU.subtract)
+                right = work.tile([P, HALF, ROWS], BF16, name="right")
                 nc.vector.scalar_tensor_tensor(
                     out=right[:],
                     in0=cubes[:, HALF:, :],
@@ -268,15 +268,21 @@ def tile_kanlinear_pa_k_kernel(
                     op0=ALU.mult,
                     op1=ALU.subtract,
                 )
+                return left, right
+
+            def regroup(left, right):
+                nc.vector.tensor_tensor(out=left[:], in0=left[:], in1=right[:], op=ALU.max)
                 basis = work.tile([P, ROWS, HALF], BF16, name="basis", align_bytes=64)
-                nc.vector.scalar_tensor_tensor(
-                    out=basis[:],
-                    in0=left[:].rearrange("p t n -> p n t"),
-                    scalar=0.0,
-                    in1=right[:].rearrange("p t n -> p n t"),
+                nc.vector.tensor_scalar(
+                    out=basis[:].rearrange("p (c i) t -> p c t i", i=4),
+                    in0=left[:].rearrange("p t (c i) -> p c t i", i=4),
+                    scalar1=0.0,
+                    scalar2=None,
                     op0=ALU.max,
-                    op1=ALU.max,
                 )
+                return basis
+
+            def multiply(g, basis, w_words):
                 b_words = work.tile([P, ROWS], U32, name="b_words", align_bytes=64)
                 b_scales = work.tile([P, ROWS], U8, name="b_scales", align_bytes=64)
                 nc.vector.quantize_mx(
@@ -297,13 +303,18 @@ def tile_kanlinear_pa_k_kernel(
                 w_of = {0: load_weights(0), 1: load_weights(1)}
                 v_of = {0: turn(0), 1: turn(1)}
                 made = {0: cube(0, v_of[0][0], v_of[0][1])}
+                basis_of = {}
                 for g in range(GROUPS):
                     if g + 2 < GROUPS:
                         w_of[g + 2] = load_weights(g + 2)
                         v_of[g + 2] = turn(g + 2)
                     if g + 1 < GROUPS:
                         made[g + 1] = cube(g + 1, v_of[g + 1][0], v_of[g + 1][1])
-                    finish(g, made[g][0], made[g][1], w_of[g])
+                    halves = merge(g, made[g][0], made[g][1])
+                    if g > 0:
+                        multiply(g - 1, basis_of[g - 1], w_of[g - 1])
+                    basis_of[g] = regroup(halves[0], halves[1])
+                multiply(GROUPS - 1, basis_of[GROUPS - 1], w_of[GROUPS - 1])
 
                 for r in range(ROW_TILES):
                     result = work.tile([P, UNITS], F32, name="result")

@@ -204,7 +204,7 @@ def tile_kanlinear_pa_k_kernel(
                         stop=False,
                     )
 
-        with tc.tile_pool(name="squares", bufs=LOCAL_KNOTS) as squares, tc.tile_pool(name="work", bufs=2) as work:
+        with tc.tile_pool(name="squares", bufs=LOCAL_KNOTS) as square_pool, tc.tile_pool(name="work", bufs=2) as work:
 
             def load_weights(g):
                 w_words = weights.tile([P, PACK * UNITS], U8, name="w_words", align_bytes=64)
@@ -223,25 +223,34 @@ def tile_kanlinear_pa_k_kernel(
                         )
                 return v_scalar, v_vector
 
-            def cube(g, v_scalar, v_vector):
-                cubes = work.tile([P, LOCAL_KNOTS, ROWS], F32, name="cubes")
+            def square(g, v_scalar):
+                squares = []
                 for i in range(LOCAL_KNOTS):
-                    square = squares.tile([P, ROWS], F32, name="square")
+                    one = square_pool.tile([P, ROWS], F32, name="one")
                     nc.scalar.activation(
-                        out=square[:],
+                        out=one[:],
                         in_=v_scalar[:],
                         func=ACT.Square,
                         scale=slope[:, g, i : i + 1],
                         bias=shift[:, g, i : i + 1],
                     )
+                    squares.append(one)
+                return squares
+
+            def cube(g, v_vector, squares):
+                cubes = work.tile([P, LOCAL_KNOTS, ROWS], F32, name="cubes")
+                for i in range(LOCAL_KNOTS):
                     nc.vector.scalar_tensor_tensor(
                         out=cubes[:, i, :],
                         in0=v_vector[:],
                         scalar=knots[:, g, i : i + 1],
-                        in1=square[:],
+                        in1=squares[i][:],
                         op0=ALU.subtract,
                         op1=ALU.mult,
                     )
+                return cubes
+
+            def cut(g, cubes):
                 inner = work.tile([P, 2 * HALF, ROWS], F32, name="inner")
                 for t in range(HALF):
                     nc.scalar.activation(
@@ -254,9 +263,9 @@ def tile_kanlinear_pa_k_kernel(
                         func=ACT.Relu,
                         scale=right_weight[:, g, t : t + 1],
                     )
-                return cubes, inner
+                return inner
 
-            def merge(g, cubes, inner):
+            def merge(cubes, inner):
                 left = work.tile([P, HALF, ROWS], BF16, name="left")
                 nc.vector.tensor_tensor(out=left[:], in0=cubes[:, 0:HALF, :], in1=inner[:, 0:HALF, :], op=ALU.subtract)
                 right = work.tile([P, HALF, ROWS], BF16, name="right")
@@ -273,12 +282,10 @@ def tile_kanlinear_pa_k_kernel(
             def regroup(left, right):
                 nc.vector.tensor_tensor(out=left[:], in0=left[:], in1=right[:], op=ALU.max)
                 basis = work.tile([P, ROWS, HALF], BF16, name="basis", align_bytes=64)
-                nc.vector.tensor_scalar(
+                nc.scalar.activation(
                     out=basis[:].rearrange("p (c i) t -> p c t i", i=4),
-                    in0=left[:].rearrange("p t (c i) -> p c t i", i=4),
-                    scalar1=0.0,
-                    scalar2=None,
-                    op0=ALU.max,
+                    in_=left[:].rearrange("p t (c i) -> p c t i", i=4),
+                    func=ACT.Relu,
                 )
                 return basis
 
@@ -302,15 +309,21 @@ def tile_kanlinear_pa_k_kernel(
             with tc.manual_schedule():
                 w_of = {0: load_weights(0), 1: load_weights(1)}
                 v_of = {0: turn(0), 1: turn(1)}
-                made = {0: cube(0, v_of[0][0], v_of[0][1])}
+                squares_of = {0: square(0, v_of[0][0])}
+                cubes_of = {0: cube(0, v_of[0][1], squares_of[0])}
+                inner_of = {0: cut(0, cubes_of[0])}
+                squares_of[1] = square(1, v_of[1][0])
                 basis_of = {}
                 for g in range(GROUPS):
                     if g + 2 < GROUPS:
                         w_of[g + 2] = load_weights(g + 2)
                         v_of[g + 2] = turn(g + 2)
                     if g + 1 < GROUPS:
-                        made[g + 1] = cube(g + 1, v_of[g + 1][0], v_of[g + 1][1])
-                    halves = merge(g, made[g][0], made[g][1])
+                        cubes_of[g + 1] = cube(g + 1, v_of[g + 1][1], squares_of[g + 1])
+                        inner_of[g + 1] = cut(g + 1, cubes_of[g + 1])
+                    if g + 2 < GROUPS:
+                        squares_of[g + 2] = square(g + 2, v_of[g + 2][0])
+                    halves = merge(cubes_of[g], inner_of[g])
                     if g > 0:
                         multiply(g - 1, basis_of[g - 1], w_of[g - 1])
                     basis_of[g] = regroup(halves[0], halves[1])

@@ -204,7 +204,7 @@ def tile_kanlinear_pa_k_kernel(
                         stop=False,
                     )
 
-        with tc.tile_pool(name="squares", bufs=LOCAL_KNOTS) as square_pool, tc.tile_pool(name="work", bufs=2) as work:
+        with tc.tile_pool(name="squares", bufs=2 * LOCAL_KNOTS) as square_pool, tc.tile_pool(name="work", bufs=2) as work:
 
             def load_weights(g):
                 w_words = weights.tile([P, PACK * UNITS], U8, name="w_words", align_bytes=64)
@@ -254,39 +254,52 @@ def tile_kanlinear_pa_k_kernel(
                 inner = work.tile([P, 2 * HALF, ROWS], F32, name="inner")
                 for t in range(HALF):
                     nc.scalar.activation(
-                        out=inner[:, t, :], in_=cubes[:, t + 1, :], func=ACT.Relu, scale=left_weight[:, g, t : t + 1]
-                    )
-                for t in range(HALF):
-                    nc.scalar.activation(
                         out=inner[:, HALF + t, :],
                         in_=cubes[:, t + 3, :],
                         func=ACT.Relu,
                         scale=right_weight[:, g, t : t + 1],
                     )
+                for t in range(HALF):
+                    nc.scalar.activation(
+                        out=inner[:, t, :], in_=cubes[:, t + 1, :], func=ACT.Relu, scale=left_weight[:, g, t : t + 1]
+                    )
                 return inner
 
-            def merge(cubes, inner):
-                left = work.tile([P, HALF, ROWS], BF16, name="left")
-                nc.vector.tensor_tensor(out=left[:], in0=cubes[:, 0:HALF, :], in1=inner[:, 0:HALF, :], op=ALU.subtract)
-                right = work.tile([P, HALF, ROWS], BF16, name="right")
-                nc.vector.scalar_tensor_tensor(
-                    out=right[:],
-                    in0=cubes[:, HALF:, :],
-                    scalar=-1.0,
-                    in1=inner[:, HALF:, :],
-                    op0=ALU.mult,
-                    op1=ALU.subtract,
-                )
-                return left, right
+            def planes(tile_slice):
+                return tile_slice.rearrange("p t (c i) -> p c t i", i=4)
 
-            def regroup(left, right):
-                nc.vector.tensor_tensor(out=left[:], in0=left[:], in1=right[:], op=ALU.max)
-                basis = work.tile([P, ROWS, HALF], BF16, name="basis", align_bytes=64)
-                nc.scalar.activation(
-                    out=basis[:].rearrange("p (c i) t -> p c t i", i=4),
-                    in_=left[:].rearrange("p t (c i) -> p c t i", i=4),
-                    func=ACT.Relu,
+            def words(tile_slice):
+                return tile_slice.rearrange("p (c i) t -> p c t i", i=4)
+
+            def merge_left(cubes, inner):
+                left = work.tile([P, ROWS, HALF], BF16, name="left", align_bytes=64)
+                nc.gpsimd.tensor_tensor(
+                    out=words(left[:]), in0=planes(inner[:, 0:HALF, :]), in1=planes(cubes[:, 0:HALF, :]), op=ALU.subtract
                 )
+                return left
+
+            def merge_right(cubes, inner):
+                right = work.tile([P, ROWS, HALF], BF16, name="right", align_bytes=64)
+                nc.vector.tensor_tensor(
+                    out=words(right[:]), in0=planes(cubes[:, HALF:, :]), in1=planes(inner[:, HALF:, :]), op=ALU.add
+                )
+                return right
+
+            def pick(left, right):
+                for half in range(2):
+                    rows = slice(half * ROWS // 2, (half + 1) * ROWS // 2)
+                    nc.vector.tensor_tensor(out=right[:, rows, :], in0=left[:, rows, :], in1=right[:, rows, :], op=ALU.min)
+                basis = work.tile([P, ROWS, HALF], BF16, name="basis", align_bytes=64)
+                for half in range(2):
+                    rows = slice(half * ROWS // 2, (half + 1) * ROWS // 2)
+                    nc.vector.tensor_scalar(
+                        out=basis[:, rows, :],
+                        in0=right[:, rows, :],
+                        scalar1=-1.0,
+                        scalar2=0.0,
+                        op0=ALU.mult,
+                        op1=ALU.max,
+                    )
                 return basis
 
             def multiply(g, basis, w_words):
@@ -311,22 +324,22 @@ def tile_kanlinear_pa_k_kernel(
                 v_of = {0: turn(0), 1: turn(1)}
                 squares_of = {0: square(0, v_of[0][0])}
                 cubes_of = {0: cube(0, v_of[0][1], squares_of[0])}
-                inner_of = {0: cut(0, cubes_of[0])}
                 squares_of[1] = square(1, v_of[1][0])
+                inner_of = {0: cut(0, cubes_of[0])}
                 basis_of = {}
                 for g in range(GROUPS):
+                    left = merge_left(cubes_of[g], inner_of[g])
                     if g + 2 < GROUPS:
                         w_of[g + 2] = load_weights(g + 2)
                         v_of[g + 2] = turn(g + 2)
+                        squares_of[g + 2] = square(g + 2, v_of[g + 2][0])
                     if g + 1 < GROUPS:
                         cubes_of[g + 1] = cube(g + 1, v_of[g + 1][1], squares_of[g + 1])
                         inner_of[g + 1] = cut(g + 1, cubes_of[g + 1])
-                    if g + 2 < GROUPS:
-                        squares_of[g + 2] = square(g + 2, v_of[g + 2][0])
-                    halves = merge(cubes_of[g], inner_of[g])
+                    right = merge_right(cubes_of[g], inner_of[g])
                     if g > 0:
                         multiply(g - 1, basis_of[g - 1], w_of[g - 1])
-                    basis_of[g] = regroup(halves[0], halves[1])
+                    basis_of[g] = pick(left, right)
                 multiply(GROUPS - 1, basis_of[GROUPS - 1], w_of[GROUPS - 1])
 
                 for r in range(ROW_TILES):

@@ -54,7 +54,9 @@ def tile_kanlinear_pa_k_kernel(
     out,
 ):
     nc = tc.nc
-    with tc.tile_pool(name="keep", bufs=1) as keep, tc.tile_pool(name="weights", bufs=4) as weights, tc.psum_pool(
+    with tc.tile_pool(name="keep", bufs=1) as keep, tc.tile_pool(name="weights", bufs=4) as weights, tc.tile_pool(
+        name="squares", bufs=LOCAL_KNOTS + LOCAL_KNOTS // 2
+    ) as square_pool, tc.psum_pool(
         name="sums", bufs=1
     ) as sums, tc.psum_pool(name="turned", bufs=2) as turned:
         ident_f32 = keep.tile([P, P], F32)
@@ -65,13 +67,14 @@ def tile_kanlinear_pa_k_kernel(
         scale_planes = keep.tile([P, BASE_PASSES + GROUPS, UNITS], U8, align_bytes=64)
         nc.vector.memset(scale_planes[:].bitcast(I32), 0)
 
-        xn_twice = [keep.tile([P, 2 * FEATURES], F32, name="xn_twice%d" % r) for r in range(ROW_TILES)]
+        y_twice = [keep.tile([P, 2 * FEATURES], F32, name="y_twice%d" % r) for r in range(ROW_TILES)]
         knots = keep.tile([P, GROUPS, LOCAL_KNOTS], F32)
         slope = keep.tile([P, GROUPS, LOCAL_KNOTS], F32)
         shift = keep.tile([P, GROUPS, LOCAL_KNOTS], F32)
         left_weight = keep.tile([P, GROUPS, HALF], F32)
         right_weight = keep.tile([P, GROUPS, HALF], F32)
         bias_rows = keep.tile([P, UNITS], BF16)
+        beta_of_base = keep.tile([P, BASE_PASSES, PACK], BF16)
         acc = [sums.tile([P, UNITS], F32, name="acc%d" % r) for r in range(ROW_TILES)]
 
         with tc.tile_pool(name="head", bufs=1) as head, tc.tile_pool(name="head2", bufs=2) as head2:
@@ -80,14 +83,18 @@ def tile_kanlinear_pa_k_kernel(
                 nc.sync.dma_start(out=x_rows[r][:], in_=x[r * P : (r + 1) * P, :])
             gamma_rows = head.tile([P, FEATURES], BF16)
             nc.scalar.dma_start(out=gamma_rows[:], in_=ln_gamma.partition_broadcast(P))
-            beta_rows = head.tile([P, FEATURES], BF16)
-            nc.scalar.dma_start(out=beta_rows[:], in_=ln_beta.partition_broadcast(P))
+            beta_by_group = head.tile([P, GROUP_FEATURES], BF16)
+            nc.vector.memset(beta_by_group[:], 0.0)
+            nc.scalar.dma_start(out=beta_by_group[0:GROUPS, :], in_=ln_beta.rearrange("(g f) -> g f", f=GROUP_FEATURES))
             knots_bf16 = head.tile([P, GROUPS, LOCAL_KNOTS], BF16)
             grid_by_group = grid[0].rearrange("(g f) i -> f g i", f=GROUP_FEATURES)
             for h in range(2):
                 nc.scalar.dma_start(
                     out=knots_bf16[h:P:2, :, :], in_=grid_by_group[:, :, HALF * h : HALF * h + LOCAL_KNOTS]
                 )
+            nc.scalar.dma_start(
+                out=beta_of_base[:], in_=ln_beta.rearrange("(g p t) -> p g t", g=BASE_PASSES, t=PACK)
+            )
             nc.scalar.dma_start(out=bias_rows[:], in_=base_bias.partition_broadcast(P))
             for q in range(4):
                 nc.sync.dma_start(
@@ -99,13 +106,29 @@ def tile_kanlinear_pa_k_kernel(
                     in_=spline_weight_scales[:, 4 * q : 4 * q + 4, :].rearrange("g r n -> r g n").bitcast(I32),
                 )
 
-            nc.gpsimd.tensor_copy(out=knots[:], in_=knots_bf16[:])
+            beta_twice = head.tile([P, P], BF16)
+            nc.vector.tensor_copy(
+                out=beta_twice[:].rearrange("g (f h) -> g f h", h=2),
+                in_=beta_by_group[:].unsqueeze(2).to_broadcast([P, GROUP_FEATURES, 2]),
+            )
+            beta_turned = turned.tile([P, P], BF16, name="beta_turned", tag="for_scalar")
+            nc.tensor.transpose(beta_turned[:], beta_twice[:], ident_bf16[:])
+            beta_column = head.tile([P, GROUPS], F32)
+            nc.vector.tensor_copy(out=beta_column[:], in_=beta_turned[:, 0:GROUPS])
+            plain_knots = head.tile([P, GROUPS, LOCAL_KNOTS], F32)
+            nc.gpsimd.tensor_copy(out=plain_knots[:], in_=knots_bf16[:])
+            nc.gpsimd.tensor_tensor(
+                out=knots[:],
+                in0=plain_knots[:],
+                in1=beta_column[:].unsqueeze(2).to_broadcast([P, GROUPS, LOCAL_KNOTS]),
+                op=ALU.subtract,
+            )
             gap = {}
             for span in (1, 2, 3, 4):
                 count = LOCAL_KNOTS - span
                 gap[span] = head.tile([P, GROUPS, count], F32, name="gap%d" % span)
                 nc.gpsimd.tensor_tensor(
-                    out=gap[span][:], in0=knots[:, :, span:LOCAL_KNOTS], in1=knots[:, :, 0:count], op=ALU.subtract
+                    out=gap[span][:], in0=plain_knots[:, :, span:LOCAL_KNOTS], in1=plain_knots[:, :, 0:count], op=ALU.subtract
                 )
             rise = head.tile([P, GROUPS, 5], F32)
             nc.gpsimd.tensor_tensor(out=rise[:], in0=gap[1][:, :, 0:5], in1=gap[2][:, :, 0:5], op=ALU.mult)
@@ -131,80 +154,33 @@ def tile_kanlinear_pa_k_kernel(
                     out=weight[:], in0=top[:], scalar=sign, in1=bottom[:], op0=ALU.mult, op1=ALU.mult
                 )
 
-            moments = head.tile([P, ROW_TILES, 2], F32)
             for r in range(ROW_TILES):
                 chunks = head2.tile([P, 4, 6], F32, name="chunks")
                 for c in range(4):
                     nc.vector.bn_stats(out=chunks[:, c, :], in_=x_rows[r][:, c * 512 : (c + 1) * 512])
-                nc.vector.bn_aggr(out=moments[:, r, :], in_=chunks[:].rearrange("p c s -> p (c s)"))
-            spread = head.tile([P, ROW_TILES], F32)
-            nc.vector.tensor_scalar_add(out=spread[:], in0=moments[:, :, 1], scalar1=LN_EPS)
-            rstd = head.tile([P, ROW_TILES], F32)
-            refined_rsqrt(nc, head, rstd[:], spread[:], [P, ROW_TILES], "rstd")
-            relu_rows = []
-            for r in range(ROW_TILES):
+                moments = head2.tile([P, 2], F32, name="moments")
+                nc.vector.bn_aggr(out=moments[:], in_=chunks[:].rearrange("p c s -> p (c s)"))
+                spread = head2.tile([P, 1], F32, name="spread")
+                nc.vector.tensor_scalar_add(out=spread[:], in0=moments[:, 1:2], scalar1=LN_EPS)
+                rstd = head2.tile([P, 1], F32, name="rstd")
+                refined_rsqrt(nc, head2, rstd[:], spread[:], [P, 1], "rstd")
                 centred = head2.tile([P, FEATURES], F32, name="centred")
                 nc.vector.scalar_tensor_tensor(
                     out=centred[:],
                     in0=x_rows[r][:],
-                    scalar=moments[:, r, 0:1],
+                    scalar=moments[:, 0:1],
                     in1=gamma_rows[:],
                     op0=ALU.subtract,
                     op1=ALU.mult,
                 )
-                nc.vector.scalar_tensor_tensor(
-                    out=xn_twice[r][:].rearrange("n (f h) -> n f h", h=2),
-                    in0=centred[:].unsqueeze(2).to_broadcast([P, FEATURES, 2]),
-                    scalar=rstd[:, r : r + 1],
-                    in1=beta_rows[:].unsqueeze(2).to_broadcast([P, FEATURES, 2]),
-                    op0=ALU.mult,
-                    op1=ALU.add,
-                )
-                relu_row = head.tile([P, FEATURES], BF16, name="relu_rows%d" % r)
-                nc.scalar.activation(
-                    out=relu_row[:].rearrange("n (g t p) -> n g t p", g=BASE_PASSES, t=PACK),
-                    in_=xn_twice[r][:].rearrange("n (g p t h) -> n g t p h", g=BASE_PASSES, p=P, t=PACK, h=2)[
-                        :, :, :, :, 0
-                    ],
-                    func=ACT.Relu,
-                )
-                relu_rows.append(relu_row)
+                twice = y_twice[r][:].rearrange("n (f h) -> n f h", h=2)
+                once = centred[:].unsqueeze(2).to_broadcast([P, FEATURES, 2])
+                if r < 2:
+                    nc.scalar.activation(out=twice, in_=once, func=ACT.Copy, scale=rstd[:])
+                else:
+                    nc.vector.tensor_scalar_mul(out=twice, in0=once, scalar1=rstd[:])
 
-            for g in range(BASE_PASSES):
-                w_words = weights.tile([P, PACK * UNITS], U8, name="w_words", align_bytes=64)
-                nc.sync.dma_start(
-                    out=w_words[:].bitcast(I32), in_=base_weight_words[g].rearrange("p n t -> p (n t)").bitcast(I32)
-                )
-                grouped = head2.tile([P, ROWS, PACK], BF16, name="grouped", align_bytes=64)
-                for pair in range(2):
-                    flipped = turned.tile([P, PACK, 2 * P], BF16, name="flipped", tag="for_scalar")
-                    for t in range(PACK):
-                        for b in range(2):
-                            nc.tensor.transpose(
-                                flipped[:, t, b * P : (b + 1) * P],
-                                relu_rows[2 * pair + b][:, g * K_PASS + t * P : g * K_PASS + (t + 1) * P],
-                                ident_bf16[:],
-                            )
-                    nc.scalar.copy(
-                        out=grouped[:, pair * 2 * P : (pair + 1) * 2 * P, :], in_=flipped[:].rearrange("p t n -> p n t")
-                    )
-                a_words = head2.tile([P, ROWS], U32, name="a_words", align_bytes=64)
-                a_scales = head2.tile([P, ROWS], U8, name="a_scales", align_bytes=64)
-                nc.vector.quantize_mx(
-                    out=a_words[:].bitcast(FP8X4), scales=a_scales[:], in_=grouped[:].rearrange("p n t -> p (n t)")
-                )
-                for r in range(ROW_TILES):
-                    nc.tensor.matmul_mx(
-                        out=acc[r][:],
-                        lhsT=a_words[:, r * P : (r + 1) * P].bitcast(FP8X4),
-                        lhsT_scale=a_scales[:, r * P : (r + 1) * P],
-                        rhs=w_words[:].bitcast(FP8X4),
-                        rhs_scale=scale_planes[:, g, :],
-                        start=(g == 0),
-                        stop=False,
-                    )
-
-        with tc.tile_pool(name="squares", bufs=2 * LOCAL_KNOTS) as square_pool, tc.tile_pool(name="work", bufs=2) as work:
+        with tc.tile_pool(name="work", bufs=2, reuse_waits="tile") as work:
 
             def load_weights(g):
                 w_words = weights.tile([P, PACK * UNITS], U8, name="w_words", align_bytes=64)
@@ -219,7 +195,7 @@ def tile_kanlinear_pa_k_kernel(
                 for bank in (v_scalar, v_vector):
                     for r in range(ROW_TILES):
                         nc.tensor.transpose(
-                            bank[:, r * P : (r + 1) * P], xn_twice[r][:, g * P : (g + 1) * P], ident_f32[:]
+                            bank[:, r * P : (r + 1) * P], y_twice[r][:, g * P : (g + 1) * P], ident_f32[:]
                         )
                 return v_scalar, v_vector
 
@@ -271,9 +247,9 @@ def tile_kanlinear_pa_k_kernel(
             def words(tile_slice):
                 return tile_slice.rearrange("p (c i) t -> p c t i", i=4)
 
-            def merge_left(cubes, inner):
+            def merge_left(engine, cubes, inner):
                 left = work.tile([P, ROWS, HALF], BF16, name="left", align_bytes=64)
-                nc.gpsimd.tensor_tensor(
+                engine.tensor_tensor(
                     out=words(left[:]), in0=planes(inner[:, 0:HALF, :]), in1=planes(cubes[:, 0:HALF, :]), op=ALU.subtract
                 )
                 return left
@@ -315,8 +291,43 @@ def tile_kanlinear_pa_k_kernel(
                         lhsT_scale=b_scales[:, r * P : (r + 1) * P],
                         rhs=w_words[:].bitcast(FP8X4),
                         rhs_scale=scale_planes[:, BASE_PASSES + g, :],
-                        start=False,
+                        start=(g == 0),
                         stop=(g == GROUPS - 1),
+                    )
+
+            def relu_step(g, t, relu_planes):
+                y_base = turned.tile([P, ROWS], F32, name="y_base", tag="for_scalar")
+                for r in range(ROW_TILES):
+                    features = y_twice[r][:].rearrange("n (g p t h) -> n g t h p", g=BASE_PASSES, p=P, t=PACK, h=2)
+                    nc.tensor.transpose(y_base[:, r * P : (r + 1) * P], features[:, g, t, 0, :], ident_f32[:])
+                nc.scalar.activation(
+                    out=relu_planes[:, t, :], in_=y_base[:], func=ACT.Relu, bias=beta_of_base[:, g, t : t + 1]
+                )
+
+            def relu_group(relu_planes):
+                grouped = work.tile([P, ROWS, PACK], BF16, name="grouped", align_bytes=64, bufs=1)
+                nc.vector.tensor_copy(out=words(grouped[:]), in_=planes(relu_planes[:]))
+                return grouped
+
+            def relu_multiply(g, grouped):
+                w_words = weights.tile([P, PACK * UNITS], U8, name="w_words", align_bytes=64)
+                nc.sync.dma_start(
+                    out=w_words[:].bitcast(I32), in_=base_weight_words[g].rearrange("p n t -> p (n t)").bitcast(I32)
+                )
+                a_words = work.tile([P, ROWS], U32, name="a_words", align_bytes=64, bufs=1)
+                a_scales = work.tile([P, ROWS], U8, name="a_scales", align_bytes=64, bufs=1)
+                nc.vector.quantize_mx(
+                    out=a_words[:].bitcast(FP8X4), scales=a_scales[:], in_=grouped[:].rearrange("p n t -> p (n t)")
+                )
+                for r in range(ROW_TILES):
+                    nc.tensor.matmul_mx(
+                        out=acc[r][:],
+                        lhsT=a_words[:, r * P : (r + 1) * P].bitcast(FP8X4),
+                        lhsT_scale=a_scales[:, r * P : (r + 1) * P],
+                        rhs=w_words[:].bitcast(FP8X4),
+                        rhs_scale=scale_planes[:, g, :],
+                        start=False,
+                        stop=False,
                     )
 
             with tc.manual_schedule():
@@ -327,8 +338,9 @@ def tile_kanlinear_pa_k_kernel(
                 squares_of[1] = square(1, v_of[1][0])
                 inner_of = {0: cut(0, cubes_of[0])}
                 basis_of = {}
+                relu_of = {}
                 for g in range(GROUPS):
-                    left = merge_left(cubes_of[g], inner_of[g])
+                    left = merge_left(nc.gpsimd if g + 1 < GROUPS else nc.vector, cubes_of[g], inner_of[g])
                     if g + 2 < GROUPS:
                         w_of[g + 2] = load_weights(g + 2)
                         v_of[g + 2] = turn(g + 2)
@@ -340,6 +352,15 @@ def tile_kanlinear_pa_k_kernel(
                     if g > 0:
                         multiply(g - 1, basis_of[g - 1], w_of[g - 1])
                     basis_of[g] = pick(left, right)
+                    step = g - 4
+                    if step >= PACK and step % PACK == 0 and step <= BASE_PASSES * PACK:
+                        grouped_relu = relu_group(relu_of[step // PACK - 1])
+                    if step >= PACK and step % PACK == 1 and step <= BASE_PASSES * PACK + 1:
+                        relu_multiply(step // PACK - 1, grouped_relu)
+                    if 0 <= step < BASE_PASSES * PACK:
+                        if step % PACK == 0:
+                            relu_of[step // PACK] = work.tile([P, PACK, ROWS], BF16, name="relu_planes")
+                        relu_step(step // PACK, step % PACK, relu_of[step // PACK])
                 multiply(GROUPS - 1, basis_of[GROUPS - 1], w_of[GROUPS - 1])
 
                 for r in range(ROW_TILES):

@@ -248,29 +248,24 @@ def tile_kanlinear_pa_k_kernel(
                 return tile_slice.rearrange("p (c i) t -> p c t i", i=4)
 
             def merge_left(engine, cubes, inner):
-                left = work.tile([P, ROWS, HALF], BF16, name="left", align_bytes=64)
-                engine.tensor_tensor(
-                    out=words(left[:]), in0=planes(inner[:, 0:HALF, :]), in1=planes(cubes[:, 0:HALF, :]), op=ALU.subtract
-                )
+                left = work.tile([P, HALF, ROWS], BF16, name="left")
+                engine.tensor_tensor(out=left[:], in0=inner[:, 0:HALF, :], in1=cubes[:, 0:HALF, :], op=ALU.subtract)
                 return left
 
             def merge_right(cubes, inner):
-                right = work.tile([P, ROWS, HALF], BF16, name="right", align_bytes=64)
-                nc.vector.tensor_tensor(
-                    out=words(right[:]), in0=planes(cubes[:, HALF:, :]), in1=planes(inner[:, HALF:, :]), op=ALU.add
-                )
+                right = work.tile([P, HALF, ROWS], BF16, name="right")
+                nc.vector.tensor_tensor(out=right[:], in0=cubes[:, HALF:, :], in1=inner[:, HALF:, :], op=ALU.add)
                 return right
 
             def pick(left, right):
-                for half in range(2):
-                    rows = slice(half * ROWS // 2, (half + 1) * ROWS // 2)
-                    nc.vector.tensor_tensor(out=right[:, rows, :], in0=left[:, rows, :], in1=right[:, rows, :], op=ALU.min)
+                pieces = [slice(half * ROWS // 2, (half + 1) * ROWS // 2) for half in range(2)]
+                for rows in pieces:
+                    nc.vector.tensor_tensor(out=right[:, :, rows], in0=left[:, :, rows], in1=right[:, :, rows], op=ALU.min)
                 basis = work.tile([P, ROWS, HALF], BF16, name="basis", align_bytes=64)
-                for half in range(2):
-                    rows = slice(half * ROWS // 2, (half + 1) * ROWS // 2)
+                for rows in pieces:
                     nc.vector.tensor_scalar(
-                        out=basis[:, rows, :],
-                        in0=right[:, rows, :],
+                        out=words(basis[:, rows, :]),
+                        in0=planes(right[:, :, rows]),
                         scalar1=-1.0,
                         scalar2=0.0,
                         op0=ALU.mult,

@@ -230,14 +230,14 @@ def tile_kanlinear_pa_k_kernel(
                 inner = work.tile([P, 2 * HALF, ROWS], F32, name="inner")
                 for t in range(HALF):
                     nc.scalar.activation(
+                        out=inner[:, t, :], in_=cubes[:, t + 1, :], func=ACT.Relu, scale=left_weight[:, g, t : t + 1]
+                    )
+                for t in range(HALF):
+                    nc.scalar.activation(
                         out=inner[:, HALF + t, :],
                         in_=cubes[:, t + 3, :],
                         func=ACT.Relu,
                         scale=right_weight[:, g, t : t + 1],
-                    )
-                for t in range(HALF):
-                    nc.scalar.activation(
-                        out=inner[:, t, :], in_=cubes[:, t + 1, :], func=ACT.Relu, scale=left_weight[:, g, t : t + 1]
                     )
                 return inner
 
@@ -248,7 +248,7 @@ def tile_kanlinear_pa_k_kernel(
                 return tile_slice.rearrange("p (c i) t -> p c t i", i=4)
 
             def merge_left(engine, cubes, inner):
-                left = work.tile([P, HALF, ROWS], BF16, name="left")
+                left = work.tile([P, HALF, ROWS], BF16, name="left", bufs=1)
                 engine.tensor_tensor(out=left[:], in0=inner[:, 0:HALF, :], in1=cubes[:, 0:HALF, :], op=ALU.subtract)
                 return left
 
@@ -260,12 +260,12 @@ def tile_kanlinear_pa_k_kernel(
             def pick(left, right):
                 pieces = [slice(half * ROWS // 2, (half + 1) * ROWS // 2) for half in range(2)]
                 for rows in pieces:
-                    nc.vector.tensor_tensor(out=right[:, :, rows], in0=left[:, :, rows], in1=right[:, :, rows], op=ALU.min)
+                    nc.vector.tensor_tensor(out=left[:, :, rows], in0=left[:, :, rows], in1=right[:, :, rows], op=ALU.min)
                 basis = work.tile([P, ROWS, HALF], BF16, name="basis", align_bytes=64)
                 for rows in pieces:
                     nc.vector.tensor_scalar(
                         out=words(basis[:, rows, :]),
-                        in0=planes(right[:, :, rows]),
+                        in0=planes(left[:, :, rows]),
                         scalar1=-1.0,
                         scalar2=0.0,
                         op0=ALU.mult,

@@ -18,26 +18,24 @@ UNITS = 512
 PACK = 4
 K_PASS = P * PACK
 BASES = 8
+KNOTS = 12
 HALF = 4
 LOCAL_KNOTS = 8
 BASE_PASSES = FEATURES // K_PASS
 GROUPS = FEATURES * BASES // K_PASS
 GROUP_FEATURES = K_PASS // BASES
+BANK = 512
 LN_EPS = 0.001
 
 FLOPS = 2 * ROWS * (FEATURES + FEATURES * BASES) * UNITS
 
 
-def refined_rsqrt(nc, pool, result, value, shape, label):
-    root = pool.tile(shape, F32, name=label + "_root")
-    nc.scalar.activation(out=root[:], in_=value, func=ACT.Sqrt)
-    guess = pool.tile(shape, F32, name=label + "_guess")
-    nc.vector.reciprocal(out=guess[:], in_=root[:])
+def refine_rsqrt(engine, pool, result, value, guess, shape, label):
     step = pool.tile(shape, F32, name=label + "_step")
-    nc.vector.tensor_tensor(out=step[:], in0=value, in1=guess[:], op=ALU.mult)
-    nc.vector.tensor_tensor(out=step[:], in0=step[:], in1=guess[:], op=ALU.mult)
-    nc.vector.tensor_scalar(out=step[:], in0=step[:], scalar1=-0.5, scalar2=1.5, op0=ALU.mult, op1=ALU.add)
-    nc.vector.tensor_tensor(out=result, in0=guess[:], in1=step[:], op=ALU.mult)
+    engine.tensor_tensor(out=step[:], in0=value, in1=guess, op=ALU.mult)
+    engine.tensor_tensor(out=step[:], in0=step[:], in1=guess, op=ALU.mult)
+    engine.tensor_scalar(out=step[:], in0=step[:], scalar1=-0.5, scalar2=1.5, op0=ALU.mult, op1=ALU.add)
+    engine.tensor_tensor(out=result, in0=guess, in1=step[:], op=ALU.mult)
 
 
 def tile_kanlinear_pa_k_kernel(
@@ -56,73 +54,125 @@ def tile_kanlinear_pa_k_kernel(
     nc = tc.nc
     with tc.tile_pool(name="keep", bufs=1) as keep, tc.tile_pool(name="weights", bufs=4) as weights, tc.tile_pool(
         name="squares", bufs=LOCAL_KNOTS + LOCAL_KNOTS // 2
-    ) as square_pool, tc.psum_pool(
-        name="sums", bufs=1
-    ) as sums, tc.psum_pool(name="turned", bufs=2) as turned:
+    ) as square_pool, tc.psum_pool(name="sums", bufs=1) as sums, tc.psum_pool(name="turned", bufs=2) as turned:
         ident_f32 = keep.tile([P, P], F32)
-        make_identity(nc, ident_f32[:])
         ident_bf16 = keep.tile([P, P], BF16)
-        make_identity(nc, ident_bf16[:])
-
         scale_planes = keep.tile([P, BASE_PASSES + GROUPS, UNITS], U8, align_bytes=64)
-        nc.vector.memset(scale_planes[:].bitcast(I32), 0)
-
         y_twice = [keep.tile([P, 2 * FEATURES], F32, name="y_twice%d" % r) for r in range(ROW_TILES)]
-        knots = keep.tile([P, GROUPS, LOCAL_KNOTS], F32)
+        minus_knots = keep.tile([P, GROUPS, LOCAL_KNOTS], F32)
         slope = keep.tile([P, GROUPS, LOCAL_KNOTS], F32)
         shift = keep.tile([P, GROUPS, LOCAL_KNOTS], F32)
-        left_weight = keep.tile([P, GROUPS, HALF], F32)
-        right_weight = keep.tile([P, GROUPS, HALF], F32)
+        cut_weight = keep.tile([P, GROUPS, 2 * HALF], F32)
         bias_rows = keep.tile([P, UNITS], BF16)
         beta_of_base = keep.tile([P, BASE_PASSES, PACK], BF16)
         acc = [sums.tile([P, UNITS], F32, name="acc%d" % r) for r in range(ROW_TILES)]
 
-        with tc.tile_pool(name="head", bufs=1) as head, tc.tile_pool(name="head2", bufs=2) as head2:
+        with tc.tile_pool(name="head", bufs=1) as head, tc.tile_pool(name="head2", bufs=2) as head2, tc.manual_schedule():
             x_rows = [head.tile([P, FEATURES], BF16, name="x_rows%d" % r) for r in range(ROW_TILES)]
-            for r in range(ROW_TILES):
+            gamma_row = head.tile([P, FEATURES], BF16)
+            group_rows = head.tile([P, GROUP_FEATURES * KNOTS], BF16)
+            beta_rows = head.tile([P, GROUP_FEATURES], BF16)
+            nc.sync.dma_start(out=x_rows[0][:], in_=x[0:P, :])
+            nc.vector.memset(group_rows[:], 0.0)
+            nc.scalar.dma_start(out=group_rows[0:GROUPS, :], in_=grid[0].rearrange("(g f) i -> g (f i)", f=GROUP_FEATURES))
+            nc.vector.memset(beta_rows[:], 0.0)
+            nc.scalar.dma_start(out=beta_rows[0:GROUPS, :], in_=ln_beta.rearrange("(g f) -> g f", f=GROUP_FEATURES))
+            nc.vector.memset(gamma_row[:], 0.0)
+            nc.scalar.dma_start(out=gamma_row[0:1, :], in_=ln_gamma.unsqueeze(0))
+            for r in range(1, ROW_TILES):
                 nc.sync.dma_start(out=x_rows[r][:], in_=x[r * P : (r + 1) * P, :])
-            gamma_rows = head.tile([P, FEATURES], BF16)
-            nc.scalar.dma_start(out=gamma_rows[:], in_=ln_gamma.partition_broadcast(P))
-            beta_by_group = head.tile([P, GROUP_FEATURES], BF16)
-            nc.vector.memset(beta_by_group[:], 0.0)
-            nc.scalar.dma_start(out=beta_by_group[0:GROUPS, :], in_=ln_beta.rearrange("(g f) -> g f", f=GROUP_FEATURES))
-            knots_bf16 = head.tile([P, GROUPS, LOCAL_KNOTS], BF16)
-            grid_by_group = grid[0].rearrange("(g f) i -> f g i", f=GROUP_FEATURES)
-            for h in range(2):
-                nc.scalar.dma_start(
-                    out=knots_bf16[h:P:2, :, :], in_=grid_by_group[:, :, HALF * h : HALF * h + LOCAL_KNOTS]
-                )
-            nc.scalar.dma_start(
-                out=beta_of_base[:], in_=ln_beta.rearrange("(g p t) -> p g t", g=BASE_PASSES, t=PACK)
-            )
-            nc.scalar.dma_start(out=bias_rows[:], in_=base_bias.partition_broadcast(P))
-            for q in range(4):
-                nc.sync.dma_start(
-                    out=scale_planes[32 * q : 32 * q + 4, 0:BASE_PASSES, :].bitcast(I32),
-                    in_=base_weight_scales[:, 4 * q : 4 * q + 4, :].rearrange("g r n -> r g n").bitcast(I32),
-                )
-                nc.sync.dma_start(
-                    out=scale_planes[32 * q : 32 * q + 4, BASE_PASSES:, :].bitcast(I32),
-                    in_=spline_weight_scales[:, 4 * q : 4 * q + 4, :].rearrange("g r n -> r g n").bitcast(I32),
-                )
+            first = head.tile([P, 1], F32)
+            nc.vector.memset(first[:], 1.0)
+            nc.scalar.activation(out=first[:], in_=first[:], func=ACT.Abs_reciprocal_sqrt)
+            ones = head.tile([P, P], BF16)
+            nc.gpsimd.memset(ones[:], 1.0)
+            make_identity(nc, ident_bf16[:])
+            make_identity(nc, ident_f32[:])
 
-            beta_twice = head.tile([P, P], BF16)
+            spread_knots = head.tile([P, LOCAL_KNOTS, P], BF16)
+            for h in range(2):
+                nc.vector.tensor_copy(
+                    out=spread_knots[:].rearrange("g i (f h) -> g h f i", h=2)[:, h, :, :],
+                    in_=group_rows[:].rearrange("g (f i) -> g f i", i=KNOTS)[:, :, HALF * h : HALF * h + LOCAL_KNOTS],
+                )
+            spread_beta = head.tile([P, P], BF16)
             nc.vector.tensor_copy(
-                out=beta_twice[:].rearrange("g (f h) -> g f h", h=2),
-                in_=beta_by_group[:].unsqueeze(2).to_broadcast([P, GROUP_FEATURES, 2]),
+                out=spread_beta[:].rearrange("g (f h) -> g f h", h=2),
+                in_=beta_rows[:].unsqueeze(2).to_broadcast([P, GROUP_FEATURES, 2]),
             )
-            beta_turned = turned.tile([P, P], BF16, name="beta_turned", tag="for_scalar")
-            nc.tensor.transpose(beta_turned[:], beta_twice[:], ident_bf16[:])
-            beta_column = head.tile([P, GROUPS], F32)
-            nc.vector.tensor_copy(out=beta_column[:], in_=beta_turned[:, 0:GROUPS])
+            turned_knots = acc[0][:].bitcast(BF16).rearrange("p (i g) -> p i g", i=LOCAL_KNOTS)
+            for i in range(LOCAL_KNOTS):
+                nc.tensor.transpose(turned_knots[:, i, :], spread_knots[:, i, :], ident_bf16[:])
+            turned_beta = acc[1][:].bitcast(BF16)[:, 0:P]
+            nc.tensor.transpose(turned_beta, spread_beta[:], ident_bf16[:])
+
+            gamma_banks = []
+            for c in range(FEATURES // BANK):
+                bank = turned.tile([P, BANK], F32, name="gamma_bank", tag="for_scalar" if c % 2 == 0 else "for_vector")
+                nc.tensor.matmul(
+                    out=bank[:], lhsT=ones[:], rhs=gamma_row[:, c * BANK : (c + 1) * BANK], start=True, stop=True
+                )
+                gamma_banks.append(bank)
+
+            minus_mean = head.tile([P, 1], F32)
+            squared = head.tile([P, 1], F32)
+            unused = head.tile([P, FEATURES], BF16)
+            nc.scalar.activation(
+                out=unused[:], in_=x_rows[0][:], func=ACT.Copy, scale=-1.0 / FEATURES, accum_out=minus_mean[:]
+            )
+            nc.scalar.activation(
+                out=unused[:], in_=x_rows[0][:], func=ACT.Square, bias=minus_mean[:], accum_out=squared[:]
+            )
+            moments = head.tile([P, ROW_TILES, 2], F32)
+            spread = head.tile([P, ROW_TILES], F32)
+            guess = head.tile([P, ROW_TILES], F32)
+            rstd = head.tile([P, ROW_TILES], F32)
+
+            def statistics(r):
+                chunks = head2.tile([P, 4, 6], F32, name="chunks")
+                for c in range(4):
+                    nc.vector.bn_stats(out=chunks[:, c, :], in_=x_rows[r][:, c * 512 : (c + 1) * 512])
+                nc.vector.bn_aggr(out=moments[:, r, :], in_=chunks[:].rearrange("p c s -> p (c s)"))
+
+            def centre(r):
+                centred = head.tile([P, FEATURES], F32, name="centred%d" % r)
+                for c in range(FEATURES // BANK):
+                    columns = slice(c * BANK, (c + 1) * BANK)
+                    nc.vector.scalar_tensor_tensor(
+                        out=centred[:, columns],
+                        in0=x_rows[r][:, columns],
+                        scalar=minus_mean[:] if r == 0 else moments[:, r, 0:1],
+                        in1=gamma_banks[c][:],
+                        op0=ALU.add if r == 0 else ALU.subtract,
+                        op1=ALU.mult,
+                    )
+                return centred
+
+            def double(engine_is_scalar, r, centred):
+                twice = y_twice[r][:].rearrange("n (f h) -> n f h", h=2)
+                once = centred[:].unsqueeze(2).to_broadcast([P, FEATURES, 2])
+                if engine_is_scalar:
+                    nc.scalar.activation(out=twice, in_=once, func=ACT.Copy, scale=rstd[:, r : r + 1])
+                else:
+                    nc.vector.tensor_scalar_mul(out=twice, in0=once, scalar1=rstd[:, r : r + 1])
+
+            statistics(1)
             plain_knots = head.tile([P, GROUPS, LOCAL_KNOTS], F32)
-            nc.gpsimd.tensor_copy(out=plain_knots[:], in_=knots_bf16[:])
-            nc.gpsimd.tensor_tensor(
-                out=knots[:],
-                in0=plain_knots[:],
-                in1=beta_column[:].unsqueeze(2).to_broadcast([P, GROUPS, LOCAL_KNOTS]),
-                op=ALU.subtract,
+            nc.vector.tensor_copy(out=plain_knots[:], in_=turned_knots[:, :, 0:GROUPS].rearrange("p i g -> p g i"))
+            beta_column = head.tile([P, GROUPS], F32)
+            nc.vector.tensor_copy(out=beta_column[:], in_=turned_beta[:, 0:GROUPS])
+            statistics(2)
+            statistics(3)
+            nc.vector.tensor_scalar(
+                out=spread[:, 0:1], in0=squared[:], scalar1=1.0 / FEATURES, scalar2=LN_EPS, op0=ALU.mult, op1=ALU.add
             )
+            nc.vector.tensor_scalar_add(out=spread[:, 1:], in0=moments[:, 1:, 1], scalar1=LN_EPS)
+            nc.scalar.activation(out=guess[:], in_=spread[:], func=ACT.Abs_reciprocal_sqrt)
+            centred = {0: centre(0)}
+            refine_rsqrt(nc.vector, head, rstd[:], spread[:], guess[:], [P, ROW_TILES], "rstd")
+            for r in range(1, ROW_TILES):
+                centred[r] = centre(r)
+
             gap = {}
             for span in (1, 2, 3, 4):
                 count = LOCAL_KNOTS - span
@@ -137,57 +187,62 @@ def tile_kanlinear_pa_k_kernel(
             nc.gpsimd.tensor_tensor(out=fall[:], in0=gap[1][:, :, 2:7], in1=gap[2][:, :, 1:6], op=ALU.mult)
             nc.gpsimd.tensor_tensor(out=fall[:], in0=fall[:], in1=gap[3][:, :, 0:5], op=ALU.mult)
             volume = head.tile([P, GROUPS, LOCAL_KNOTS], F32)
-            nc.gpsimd.tensor_copy(out=volume[:, :, 0:HALF], in_=rise[:, :, 0:HALF])
-            nc.gpsimd.tensor_copy(out=volume[:, :, HALF:LOCAL_KNOTS], in_=fall[:, :, 1:5])
-            refined_rsqrt(nc, head, slope[:], volume[:], [P, GROUPS, LOCAL_KNOTS], "slope")
-            nc.vector.scalar_tensor_tensor(
-                out=shift[:], in0=slope[:], scalar=-1.0, in1=knots[:], op0=ALU.mult, op1=ALU.mult
+            nc.scalar.copy(out=volume[:, :, 0:HALF], in_=rise[:, :, 0:HALF])
+            nc.scalar.copy(out=volume[:, :, HALF:LOCAL_KNOTS], in_=fall[:, :, 1:5])
+            slope_guess = head.tile([P, GROUPS, LOCAL_KNOTS], F32)
+            nc.scalar.activation(out=slope_guess[:], in_=volume[:], func=ACT.Abs_reciprocal_sqrt)
+            refine_rsqrt(
+                nc.gpsimd, head, slope[:], volume[:], slope_guess[:], [P, GROUPS, LOCAL_KNOTS], "slope"
             )
-            for weight, sign, first, outer in ((left_weight, 1.0, 1, rise[:, :, 1:5]), (right_weight, -1.0, 3, fall[:, :, 0:4])):
-                edge = 0 if first == 1 else 3
-                top = head.tile([P, GROUPS, HALF], F32, name="top%d" % first)
-                nc.gpsimd.tensor_tensor(out=top[:], in0=gap[4][:], in1=volume[:, :, first : first + HALF], op=ALU.mult)
-                bottom = head.tile([P, GROUPS, HALF], F32, name="bottom%d" % first)
-                nc.gpsimd.tensor_tensor(out=bottom[:], in0=gap[1][:, :, edge : edge + HALF], in1=outer, op=ALU.mult)
-                nc.vector.reciprocal(out=bottom[:], in_=bottom[:])
-                nc.vector.scalar_tensor_tensor(
-                    out=weight[:], in0=top[:], scalar=sign, in1=bottom[:], op0=ALU.mult, op1=ALU.mult
+            nc.gpsimd.tensor_tensor(
+                out=minus_knots[:],
+                in0=beta_column[:].unsqueeze(2).to_broadcast([P, GROUPS, LOCAL_KNOTS]),
+                in1=plain_knots[:],
+                op=ALU.subtract,
+            )
+            nc.gpsimd.tensor_tensor(out=shift[:], in0=slope[:], in1=minus_knots[:], op=ALU.mult)
+            top = head.tile([P, GROUPS, 2 * HALF], F32)
+            bottom = head.tile([P, GROUPS, 2 * HALF], F32)
+            for side, first_knot, edge, outer in ((0, 1, 0, rise[:, :, 1:5]), (1, 3, 3, fall[:, :, 0:4])):
+                part = slice(side * HALF, (side + 1) * HALF)
+                nc.gpsimd.tensor_tensor(out=bottom[:, :, part], in0=gap[1][:, :, edge : edge + HALF], in1=outer, op=ALU.mult)
+                nc.gpsimd.tensor_tensor(
+                    out=top[:, :, part], in0=gap[4][:], in1=volume[:, :, first_knot : first_knot + HALF], op=ALU.mult
                 )
-
-            for r in range(ROW_TILES):
-                chunks = head2.tile([P, 4, 6], F32, name="chunks")
-                for c in range(4):
-                    nc.vector.bn_stats(out=chunks[:, c, :], in_=x_rows[r][:, c * 512 : (c + 1) * 512])
-                moments = head2.tile([P, 2], F32, name="moments")
-                nc.vector.bn_aggr(out=moments[:], in_=chunks[:].rearrange("p c s -> p (c s)"))
-                spread = head2.tile([P, 1], F32, name="spread")
-                nc.vector.tensor_scalar_add(out=spread[:], in0=moments[:, 1:2], scalar1=LN_EPS)
-                rstd = head2.tile([P, 1], F32, name="rstd")
-                refined_rsqrt(nc, head2, rstd[:], spread[:], [P, 1], "rstd")
-                centred = head2.tile([P, FEATURES], F32, name="centred")
-                nc.vector.scalar_tensor_tensor(
-                    out=centred[:],
-                    in0=x_rows[r][:],
-                    scalar=moments[:, 0:1],
-                    in1=gamma_rows[:],
-                    op0=ALU.subtract,
-                    op1=ALU.mult,
-                )
-                twice = y_twice[r][:].rearrange("n (f h) -> n f h", h=2)
-                once = centred[:].unsqueeze(2).to_broadcast([P, FEATURES, 2])
-                if r < 2:
-                    nc.scalar.activation(out=twice, in_=once, func=ACT.Copy, scale=rstd[:])
-                else:
-                    nc.vector.tensor_scalar_mul(out=twice, in0=once, scalar1=rstd[:])
+            nc.gpsimd.tensor_scalar(
+                out=top[:, :, HALF:], in0=top[:, :, HALF:], scalar1=-1.0, scalar2=0.0, op0=ALU.mult, op1=ALU.add
+            )
+            double(True, 0, centred[0])
+            double(False, 2, centred[2])
+            double(True, 1, centred[1])
+            double(False, 3, centred[3])
+            nc.vector.reciprocal(out=bottom[:], in_=bottom[:])
+            nc.gpsimd.tensor_tensor(out=cut_weight[:], in0=top[:], in1=bottom[:], op=ALU.mult)
+            nc.gpsimd.memset(scale_planes[:].bitcast(I32), 0)
+            nc.scalar.dma_start(
+                out=beta_of_base[:], in_=ln_beta.rearrange("(g p t) -> p g t", g=BASE_PASSES, t=PACK)
+            )
+            nc.scalar.dma_start(out=bias_rows[:], in_=base_bias.partition_broadcast(P))
 
         with tc.tile_pool(name="work", bufs=2, reuse_waits="tile") as work:
 
-            def load_weights(g):
+            def load_weights(words_of_pass):
                 w_words = weights.tile([P, PACK * UNITS], U8, name="w_words", align_bytes=64)
                 nc.sync.dma_start(
-                    out=w_words[:].bitcast(I32), in_=spline_weight_words[g].rearrange("p n t -> p (n t)").bitcast(I32)
+                    out=w_words[:].bitcast(I32), in_=words_of_pass.rearrange("p n t -> p (n t)").bitcast(I32)
                 )
                 return w_words
+
+            def load_scales():
+                for q in range(4):
+                    nc.sync.dma_start(
+                        out=scale_planes[32 * q : 32 * q + 4, 0:BASE_PASSES, :].bitcast(I32),
+                        in_=base_weight_scales[:, 4 * q : 4 * q + 4, :].rearrange("g r n -> r g n").bitcast(I32),
+                    )
+                    nc.sync.dma_start(
+                        out=scale_planes[32 * q : 32 * q + 4, BASE_PASSES:, :].bitcast(I32),
+                        in_=spline_weight_scales[:, 4 * q : 4 * q + 4, :].rearrange("g r n -> r g n").bitcast(I32),
+                    )
 
             def turn(g):
                 v_scalar = turned.tile([P, ROWS], F32, name="v_scalar", tag="for_scalar")
@@ -219,26 +274,24 @@ def tile_kanlinear_pa_k_kernel(
                     nc.vector.scalar_tensor_tensor(
                         out=cubes[:, i, :],
                         in0=v_vector[:],
-                        scalar=knots[:, g, i : i + 1],
+                        scalar=minus_knots[:, g, i : i + 1],
                         in1=squares[i][:],
-                        op0=ALU.subtract,
+                        op0=ALU.add,
                         op1=ALU.mult,
                     )
                 return cubes
 
-            def cut(g, cubes):
+            def cut(g, cubes, on_vector):
                 inner = work.tile([P, 2 * HALF, ROWS], F32, name="inner")
-                for t in range(HALF):
-                    nc.scalar.activation(
-                        out=inner[:, t, :], in_=cubes[:, t + 1, :], func=ACT.Relu, scale=left_weight[:, g, t : t + 1]
-                    )
-                for t in range(HALF):
-                    nc.scalar.activation(
-                        out=inner[:, HALF + t, :],
-                        in_=cubes[:, t + 3, :],
-                        func=ACT.Relu,
-                        scale=right_weight[:, g, t : t + 1],
-                    )
+                for j in range(2 * HALF):
+                    source = cubes[:, j + 1 if j < HALF else j - 1, :]
+                    weight = cut_weight[:, g, j : j + 1]
+                    if j in on_vector:
+                        nc.vector.tensor_scalar(
+                            out=inner[:, j, :], in0=source, scalar1=weight, scalar2=0.0, op0=ALU.mult, op1=ALU.max
+                        )
+                    else:
+                        nc.scalar.activation(out=inner[:, j, :], in_=source, func=ACT.Relu, scale=weight)
                 return inner
 
             def planes(tile_slice):
@@ -257,38 +310,46 @@ def tile_kanlinear_pa_k_kernel(
                 nc.vector.tensor_tensor(out=right[:], in0=cubes[:, HALF:, :], in1=inner[:, HALF:, :], op=ALU.add)
                 return right
 
-            def pick(left, right):
+            def pick(left, right, last):
                 pieces = [slice(half * ROWS // 2, (half + 1) * ROWS // 2) for half in range(2)]
                 for rows in pieces:
                     nc.vector.tensor_tensor(out=left[:, :, rows], in0=left[:, :, rows], in1=right[:, :, rows], op=ALU.min)
                 basis = work.tile([P, ROWS, HALF], BF16, name="basis", align_bytes=64)
                 for rows in pieces:
-                    nc.vector.tensor_scalar(
-                        out=words(basis[:, rows, :]),
-                        in0=planes(left[:, :, rows]),
-                        scalar1=-1.0,
-                        scalar2=0.0,
-                        op0=ALU.mult,
-                        op1=ALU.max,
-                    )
+                    if last and rows.start == 0:
+                        nc.scalar.activation(
+                            out=words(basis[:, rows, :]), in_=planes(left[:, :, rows]), func=ACT.Relu, scale=-1.0
+                        )
+                    else:
+                        nc.vector.tensor_scalar(
+                            out=words(basis[:, rows, :]),
+                            in0=planes(left[:, :, rows]),
+                            scalar1=-1.0,
+                            scalar2=0.0,
+                            op0=ALU.mult,
+                            op1=ALU.max,
+                        )
                 return basis
 
-            def multiply(g, basis, w_words):
-                b_words = work.tile([P, ROWS], U32, name="b_words", align_bytes=64)
-                b_scales = work.tile([P, ROWS], U8, name="b_scales", align_bytes=64)
+            def multiply(values, w_words, scale_row, start, stop):
+                codes = work.tile([P, ROWS], U32, name="codes", align_bytes=64)
+                scales = work.tile([P, ROWS], U8, name="scales", align_bytes=64)
                 nc.vector.quantize_mx(
-                    out=b_words[:].bitcast(FP8X4), scales=b_scales[:], in_=basis[:].rearrange("p n t -> p (n t)")
+                    out=codes[:].bitcast(FP8X4), scales=scales[:], in_=values[:].rearrange("p n t -> p (n t)")
                 )
                 for r in range(ROW_TILES):
                     nc.tensor.matmul_mx(
                         out=acc[r][:],
-                        lhsT=b_words[:, r * P : (r + 1) * P].bitcast(FP8X4),
-                        lhsT_scale=b_scales[:, r * P : (r + 1) * P],
+                        lhsT=codes[:, r * P : (r + 1) * P].bitcast(FP8X4),
+                        lhsT_scale=scales[:, r * P : (r + 1) * P],
                         rhs=w_words[:].bitcast(FP8X4),
-                        rhs_scale=scale_planes[:, BASE_PASSES + g, :],
-                        start=(g == 0),
-                        stop=(g == GROUPS - 1),
+                        rhs_scale=scale_planes[:, scale_row, :],
+                        start=start,
+                        stop=stop,
                     )
+
+            def multiply_bases(g, basis, w_words):
+                multiply(basis, w_words, BASE_PASSES + g, g == 0, g == GROUPS - 1)
 
             def relu_step(g, t, relu_planes):
                 y_base = turned.tile([P, ROWS], F32, name="y_base", tag="for_scalar")
@@ -304,59 +365,46 @@ def tile_kanlinear_pa_k_kernel(
                 nc.vector.tensor_copy(out=words(grouped[:]), in_=planes(relu_planes[:]))
                 return grouped
 
-            def relu_multiply(g, grouped):
-                w_words = weights.tile([P, PACK * UNITS], U8, name="w_words", align_bytes=64)
-                nc.sync.dma_start(
-                    out=w_words[:].bitcast(I32), in_=base_weight_words[g].rearrange("p n t -> p (n t)").bitcast(I32)
-                )
-                a_words = work.tile([P, ROWS], U32, name="a_words", align_bytes=64, bufs=1)
-                a_scales = work.tile([P, ROWS], U8, name="a_scales", align_bytes=64, bufs=1)
-                nc.vector.quantize_mx(
-                    out=a_words[:].bitcast(FP8X4), scales=a_scales[:], in_=grouped[:].rearrange("p n t -> p (n t)")
-                )
-                for r in range(ROW_TILES):
-                    nc.tensor.matmul_mx(
-                        out=acc[r][:],
-                        lhsT=a_words[:, r * P : (r + 1) * P].bitcast(FP8X4),
-                        lhsT_scale=a_scales[:, r * P : (r + 1) * P],
-                        rhs=w_words[:].bitcast(FP8X4),
-                        rhs_scale=scale_planes[:, g, :],
-                        start=False,
-                        stop=False,
-                    )
-
             with tc.manual_schedule():
-                w_of = {0: load_weights(0), 1: load_weights(1)}
+                w_of = {0: load_weights(spline_weight_words[0]), 1: load_weights(spline_weight_words[1])}
+                load_scales()
                 v_of = {0: turn(0), 1: turn(1)}
-                squares_of = {0: square(0, v_of[0][0])}
+                squares_of = {0: square(0, v_of[0][0]), 1: square(1, v_of[1][0])}
                 cubes_of = {0: cube(0, v_of[0][1], squares_of[0])}
-                squares_of[1] = square(1, v_of[1][0])
-                inner_of = {0: cut(0, cubes_of[0])}
+                inner_of = {0: cut(0, cubes_of[0], range(2 * HALF))}
                 basis_of = {}
                 relu_of = {}
                 for g in range(GROUPS):
-                    left = merge_left(nc.gpsimd if g + 1 < GROUPS else nc.vector, cubes_of[g], inner_of[g])
+                    last = g == GROUPS - 1
+                    if not last:
+                        left = merge_left(nc.gpsimd, cubes_of[g], inner_of[g])
                     if g + 2 < GROUPS:
-                        w_of[g + 2] = load_weights(g + 2)
+                        w_of[g + 2] = load_weights(spline_weight_words[g + 2])
                         v_of[g + 2] = turn(g + 2)
                         squares_of[g + 2] = square(g + 2, v_of[g + 2][0])
                     if g + 1 < GROUPS:
                         cubes_of[g + 1] = cube(g + 1, v_of[g + 1][1], squares_of[g + 1])
-                        inner_of[g + 1] = cut(g + 1, cubes_of[g + 1])
+                    if g + 2 < GROUPS:
+                        inner_of[g + 1] = cut(g + 1, cubes_of[g + 1], ())
                     right = merge_right(cubes_of[g], inner_of[g])
                     if g > 0:
-                        multiply(g - 1, basis_of[g - 1], w_of[g - 1])
-                    basis_of[g] = pick(left, right)
+                        multiply_bases(g - 1, basis_of[g - 1], w_of[g - 1])
                     step = g - 4
-                    if step >= PACK and step % PACK == 0 and step <= BASE_PASSES * PACK:
-                        grouped_relu = relu_group(relu_of[step // PACK - 1])
-                    if step >= PACK and step % PACK == 1 and step <= BASE_PASSES * PACK + 1:
-                        relu_multiply(step // PACK - 1, grouped_relu)
+                    if PACK <= step <= BASE_PASSES * PACK and step % PACK == 0:
+                        relu_values = relu_group(relu_of[step // PACK - 1])
+                    if PACK < step <= BASE_PASSES * PACK + 1 and step % PACK == 1:
+                        branch = step // PACK - 1
+                        multiply(relu_values, load_weights(base_weight_words[branch]), branch, False, False)
                     if 0 <= step < BASE_PASSES * PACK:
                         if step % PACK == 0:
                             relu_of[step // PACK] = work.tile([P, PACK, ROWS], BF16, name="relu_planes")
                         relu_step(step // PACK, step % PACK, relu_of[step // PACK])
-                multiply(GROUPS - 1, basis_of[GROUPS - 1], w_of[GROUPS - 1])
+                    if last:
+                        left = merge_left(nc.vector, cubes_of[g], inner_of[g])
+                    basis_of[g] = pick(left, right, last)
+                    if g + 2 == GROUPS:
+                        inner_of[g + 1] = cut(g + 1, cubes_of[g + 1], range(HALF, 2 * HALF))
+                multiply_bases(GROUPS - 1, basis_of[GROUPS - 1], w_of[GROUPS - 1])
 
                 for r in range(ROW_TILES):
                     result = work.tile([P, UNITS], F32, name="result")

@@ -20,11 +20,12 @@ K_PASS = P * PACK
 BASES = 8
 KNOTS = 12
 HALF = 4
-LOCAL_KNOTS = 8
+SETS = FEATURES // P
 BASE_PASSES = FEATURES // K_PASS
 GROUPS = FEATURES * BASES // K_PASS
-GROUP_FEATURES = K_PASS // BASES
 BANK = 512
+WORD_BYTES = PACK * UNITS
+GPSIMD_LEFTS = 6
 LN_EPS = 0.001
 
 FLOPS = 2 * ROWS * (FEATURES + FEATURES * BASES) * UNITS
@@ -52,17 +53,19 @@ def tile_kanlinear_pa_k_kernel(
     out,
 ):
     nc = tc.nc
-    with tc.tile_pool(name="keep", bufs=1) as keep, tc.tile_pool(name="weights", bufs=4) as weights, tc.tile_pool(
-        name="squares", bufs=LOCAL_KNOTS + LOCAL_KNOTS // 2
-    ) as square_pool, tc.psum_pool(name="sums", bufs=1) as sums, tc.psum_pool(name="turned", bufs=2) as turned:
+    with tc.tile_pool(name="keep", bufs=1) as keep, tc.tile_pool(name="squares", bufs=14) as square_pool, tc.tile_pool(
+        name="weights", bufs=5
+    ) as weights, tc.psum_pool(
+        name="sums", bufs=1
+    ) as sums, tc.psum_pool(name="turned", bufs=2) as turned:
         ident_f32 = keep.tile([P, P], F32)
         ident_bf16 = keep.tile([P, P], BF16)
         scale_planes = keep.tile([P, BASE_PASSES + GROUPS, UNITS], U8, align_bytes=64)
-        y_twice = [keep.tile([P, 2 * FEATURES], F32, name="y_twice%d" % r) for r in range(ROW_TILES)]
-        minus_knots = keep.tile([P, GROUPS, LOCAL_KNOTS], F32)
-        slope = keep.tile([P, GROUPS, LOCAL_KNOTS], F32)
-        shift = keep.tile([P, GROUPS, LOCAL_KNOTS], F32)
-        cut_weight = keep.tile([P, GROUPS, 2 * HALF], F32)
+        y_rows = [keep.tile([P, FEATURES], F32, name="y_rows%d" % r) for r in range(ROW_TILES)]
+        minus_knots = keep.tile([P, SETS, KNOTS], F32)
+        slope = keep.tile([P, SETS, KNOTS], F32)
+        shift = keep.tile([P, SETS, KNOTS], F32)
+        weight = keep.tile([P, SETS, 2 * BASES + HALF], F32)
         bias_rows = keep.tile([P, UNITS], BF16)
         beta_of_base = keep.tile([P, BASE_PASSES, PACK], BF16)
         acc = [sums.tile([P, UNITS], F32, name="acc%d" % r) for r in range(ROW_TILES)]
@@ -70,13 +73,13 @@ def tile_kanlinear_pa_k_kernel(
         with tc.tile_pool(name="head", bufs=1) as head, tc.tile_pool(name="head2", bufs=2) as head2, tc.manual_schedule():
             x_rows = [head.tile([P, FEATURES], BF16, name="x_rows%d" % r) for r in range(ROW_TILES)]
             gamma_row = head.tile([P, FEATURES], BF16)
-            group_rows = head.tile([P, GROUP_FEATURES * KNOTS], BF16)
-            beta_rows = head.tile([P, GROUP_FEATURES], BF16)
+            set_rows = head.tile([P, P * KNOTS], BF16)
+            beta_rows = head.tile([P, P], BF16)
             nc.sync.dma_start(out=x_rows[0][:], in_=x[0:P, :])
-            nc.vector.memset(group_rows[:], 0.0)
-            nc.scalar.dma_start(out=group_rows[0:GROUPS, :], in_=grid[0].rearrange("(g f) i -> g (f i)", f=GROUP_FEATURES))
+            nc.vector.memset(set_rows[:], 0.0)
+            nc.scalar.dma_start(out=set_rows[0:SETS, :], in_=grid[0].rearrange("(s f) i -> s (f i)", f=P))
             nc.vector.memset(beta_rows[:], 0.0)
-            nc.scalar.dma_start(out=beta_rows[0:GROUPS, :], in_=ln_beta.rearrange("(g f) -> g f", f=GROUP_FEATURES))
+            nc.scalar.dma_start(out=beta_rows[0:SETS, :], in_=ln_beta.rearrange("(s f) -> s f", f=P))
             nc.vector.memset(gamma_row[:], 0.0)
             nc.scalar.dma_start(out=gamma_row[0:1, :], in_=ln_gamma.unsqueeze(0))
             for r in range(1, ROW_TILES):
@@ -88,23 +91,16 @@ def tile_kanlinear_pa_k_kernel(
             nc.gpsimd.memset(ones[:], 1.0)
             make_identity(nc, ident_bf16[:])
             make_identity(nc, ident_f32[:])
+            nc.gpsimd.memset(scale_planes[:].bitcast(I32), 0)
 
-            spread_knots = head.tile([P, LOCAL_KNOTS, P], BF16)
-            for h in range(2):
-                nc.vector.tensor_copy(
-                    out=spread_knots[:].rearrange("g i (f h) -> g h f i", h=2)[:, h, :, :],
-                    in_=group_rows[:].rearrange("g (f i) -> g f i", i=KNOTS)[:, :, HALF * h : HALF * h + LOCAL_KNOTS],
+            turned_knots = acc[0][:].bitcast(BF16).rearrange("p (i s) -> p i s", s=P)
+            turned_late = acc[1][:].bitcast(BF16).rearrange("p (i s) -> p i s", s=P)
+            by_knot = set_rows[:].rearrange("s (f i) -> s i f", i=KNOTS)
+            for i in range(KNOTS):
+                nc.tensor.transpose(
+                    turned_knots[:, i, :] if i < 8 else turned_late[:, i - 8, :], by_knot[:, i, :], ident_bf16[:]
                 )
-            spread_beta = head.tile([P, P], BF16)
-            nc.vector.tensor_copy(
-                out=spread_beta[:].rearrange("g (f h) -> g f h", h=2),
-                in_=beta_rows[:].unsqueeze(2).to_broadcast([P, GROUP_FEATURES, 2]),
-            )
-            turned_knots = acc[0][:].bitcast(BF16).rearrange("p (i g) -> p i g", i=LOCAL_KNOTS)
-            for i in range(LOCAL_KNOTS):
-                nc.tensor.transpose(turned_knots[:, i, :], spread_knots[:, i, :], ident_bf16[:])
-            turned_beta = acc[1][:].bitcast(BF16)[:, 0:P]
-            nc.tensor.transpose(turned_beta, spread_beta[:], ident_bf16[:])
+            nc.tensor.transpose(turned_late[:, 4, :], beta_rows[:], ident_bf16[:])
 
             gamma_banks = []
             for c in range(FEATURES // BANK):
@@ -148,19 +144,12 @@ def tile_kanlinear_pa_k_kernel(
                     )
                 return centred
 
-            def double(engine_is_scalar, r, centred):
-                twice = y_twice[r][:].rearrange("n (f h) -> n f h", h=2)
-                once = centred[:].unsqueeze(2).to_broadcast([P, FEATURES, 2])
-                if engine_is_scalar:
-                    nc.scalar.activation(out=twice, in_=once, func=ACT.Copy, scale=rstd[:, r : r + 1])
-                else:
-                    nc.vector.tensor_scalar_mul(out=twice, in0=once, scalar1=rstd[:, r : r + 1])
-
             statistics(1)
-            plain_knots = head.tile([P, GROUPS, LOCAL_KNOTS], F32)
-            nc.vector.tensor_copy(out=plain_knots[:], in_=turned_knots[:, :, 0:GROUPS].rearrange("p i g -> p g i"))
-            beta_column = head.tile([P, GROUPS], F32)
-            nc.vector.tensor_copy(out=beta_column[:], in_=turned_beta[:, 0:GROUPS])
+            plain_knots = head.tile([P, SETS, KNOTS], F32)
+            nc.vector.tensor_copy(out=plain_knots[:, :, 0:8], in_=turned_knots[:, :, 0:SETS].rearrange("p i s -> p s i"))
+            nc.vector.tensor_copy(out=plain_knots[:, :, 8:], in_=turned_late[:, 0:4, 0:SETS].rearrange("p i s -> p s i"))
+            beta_column = head.tile([P, SETS], F32)
+            nc.vector.tensor_copy(out=beta_column[:], in_=turned_late[:, 4, 0:SETS])
             statistics(2)
             statistics(3)
             nc.vector.tensor_scalar(
@@ -175,63 +164,54 @@ def tile_kanlinear_pa_k_kernel(
 
             gap = {}
             for span in (1, 2, 3, 4):
-                count = LOCAL_KNOTS - span
-                gap[span] = head.tile([P, GROUPS, count], F32, name="gap%d" % span)
+                count = KNOTS - span
+                gap[span] = head.tile([P, SETS, count], F32, name="gap%d" % span)
                 nc.gpsimd.tensor_tensor(
-                    out=gap[span][:], in0=plain_knots[:, :, span:LOCAL_KNOTS], in1=plain_knots[:, :, 0:count], op=ALU.subtract
+                    out=gap[span][:], in0=plain_knots[:, :, span:], in1=plain_knots[:, :, 0:count], op=ALU.subtract
                 )
-            rise = head.tile([P, GROUPS, 5], F32)
-            nc.gpsimd.tensor_tensor(out=rise[:], in0=gap[1][:, :, 0:5], in1=gap[2][:, :, 0:5], op=ALU.mult)
-            nc.gpsimd.tensor_tensor(out=rise[:], in0=rise[:], in1=gap[3][:, :, 0:5], op=ALU.mult)
-            fall = head.tile([P, GROUPS, 5], F32)
-            nc.gpsimd.tensor_tensor(out=fall[:], in0=gap[1][:, :, 2:7], in1=gap[2][:, :, 1:6], op=ALU.mult)
-            nc.gpsimd.tensor_tensor(out=fall[:], in0=fall[:], in1=gap[3][:, :, 0:5], op=ALU.mult)
-            volume = head.tile([P, GROUPS, LOCAL_KNOTS], F32)
-            nc.scalar.copy(out=volume[:, :, 0:HALF], in_=rise[:, :, 0:HALF])
-            nc.scalar.copy(out=volume[:, :, HALF:LOCAL_KNOTS], in_=fall[:, :, 1:5])
-            slope_guess = head.tile([P, GROUPS, LOCAL_KNOTS], F32)
+            rise = head.tile([P, SETS, 9], F32)
+            nc.gpsimd.tensor_tensor(out=rise[:], in0=gap[1][:, :, 0:9], in1=gap[2][:, :, 0:9], op=ALU.mult)
+            nc.gpsimd.tensor_tensor(out=rise[:], in0=rise[:], in1=gap[3][:], op=ALU.mult)
+            fall = head.tile([P, SETS, 9], F32)
+            nc.gpsimd.tensor_tensor(out=fall[:], in0=gap[1][:, :, 2:11], in1=gap[2][:, :, 1:10], op=ALU.mult)
+            nc.gpsimd.tensor_tensor(out=fall[:], in0=fall[:], in1=gap[3][:], op=ALU.mult)
+            volume = head.tile([P, SETS, KNOTS], F32)
+            nc.scalar.copy(out=volume[:, :, 0:BASES], in_=rise[:, :, 0:BASES])
+            nc.scalar.copy(out=volume[:, :, BASES:], in_=fall[:, :, 5:9])
+            slope_guess = head.tile([P, SETS, KNOTS], F32)
             nc.scalar.activation(out=slope_guess[:], in_=volume[:], func=ACT.Abs_reciprocal_sqrt)
-            refine_rsqrt(
-                nc.gpsimd, head, slope[:], volume[:], slope_guess[:], [P, GROUPS, LOCAL_KNOTS], "slope"
-            )
+            refine_rsqrt(nc.gpsimd, head, slope[:], volume[:], slope_guess[:], [P, SETS, KNOTS], "slope")
             nc.gpsimd.tensor_tensor(
                 out=minus_knots[:],
-                in0=beta_column[:].unsqueeze(2).to_broadcast([P, GROUPS, LOCAL_KNOTS]),
+                in0=beta_column[:].unsqueeze(2).to_broadcast([P, SETS, KNOTS]),
                 in1=plain_knots[:],
                 op=ALU.subtract,
             )
             nc.gpsimd.tensor_tensor(out=shift[:], in0=slope[:], in1=minus_knots[:], op=ALU.mult)
-            top = head.tile([P, GROUPS, 2 * HALF], F32)
-            bottom = head.tile([P, GROUPS, 2 * HALF], F32)
-            for side, first_knot, edge, outer in ((0, 1, 0, rise[:, :, 1:5]), (1, 3, 3, fall[:, :, 0:4])):
-                part = slice(side * HALF, (side + 1) * HALF)
-                nc.gpsimd.tensor_tensor(out=bottom[:, :, part], in0=gap[1][:, :, edge : edge + HALF], in1=outer, op=ALU.mult)
-                nc.gpsimd.tensor_tensor(
-                    out=top[:, :, part], in0=gap[4][:], in1=volume[:, :, first_knot : first_knot + HALF], op=ALU.mult
-                )
+            top = head.tile([P, SETS, 2 * BASES + HALF], F32)
+            bottom = head.tile([P, SETS, 2 * BASES + HALF], F32)
+            lefts, rights, firsts = slice(0, BASES), slice(BASES, 2 * BASES), slice(2 * BASES, None)
+            nc.gpsimd.tensor_tensor(out=top[:, :, lefts], in0=gap[4][:], in1=volume[:, :, 1:9], op=ALU.mult)
+            nc.gpsimd.tensor_tensor(out=bottom[:, :, lefts], in0=gap[1][:, :, 0:8], in1=rise[:, :, 1:9], op=ALU.mult)
+            nc.gpsimd.tensor_tensor(out=top[:, :, rights], in0=gap[4][:], in1=volume[:, :, 3:11], op=ALU.mult)
             nc.gpsimd.tensor_scalar(
-                out=top[:, :, HALF:], in0=top[:, :, HALF:], scalar1=-1.0, scalar2=0.0, op0=ALU.mult, op1=ALU.add
+                out=top[:, :, rights], in0=top[:, :, rights], scalar1=-1.0, scalar2=0.0, op0=ALU.mult, op1=ALU.add
             )
-            double(True, 0, centred[0])
-            double(False, 2, centred[2])
-            double(True, 1, centred[1])
-            double(False, 3, centred[3])
+            nc.gpsimd.tensor_tensor(out=bottom[:, :, rights], in0=gap[1][:, :, 3:11], in1=fall[:, :, 0:8], op=ALU.mult)
+            nc.scalar.copy(out=top[:, :, firsts], in_=rise[:, :, 4:8])
+            nc.scalar.copy(out=bottom[:, :, firsts], in_=fall[:, :, 1:5])
+
+            for r in range(ROW_TILES - 1):
+                nc.scalar.activation(out=y_rows[r][:], in_=centred[r][:], func=ACT.Copy, scale=rstd[:, r : r + 1])
+            nc.vector.tensor_scalar_mul(out=y_rows[3][:], in0=centred[3][:], scalar1=rstd[:, 3:4])
             nc.vector.reciprocal(out=bottom[:], in_=bottom[:])
-            nc.gpsimd.tensor_tensor(out=cut_weight[:], in0=top[:], in1=bottom[:], op=ALU.mult)
-            nc.gpsimd.memset(scale_planes[:].bitcast(I32), 0)
+            nc.gpsimd.tensor_tensor(out=weight[:], in0=top[:], in1=bottom[:], op=ALU.mult)
             nc.scalar.dma_start(
                 out=beta_of_base[:], in_=ln_beta.rearrange("(g p t) -> p g t", g=BASE_PASSES, t=PACK)
             )
             nc.scalar.dma_start(out=bias_rows[:], in_=base_bias.partition_broadcast(P))
 
-        with tc.tile_pool(name="work", bufs=2, reuse_waits="tile") as work:
-
-            def load_weights(words_of_pass):
-                w_words = weights.tile([P, PACK * UNITS], U8, name="w_words", align_bytes=64)
-                nc.sync.dma_start(
-                    out=w_words[:].bitcast(I32), in_=words_of_pass.rearrange("p n t -> p (n t)").bitcast(I32)
-                )
-                return w_words
+        with tc.tile_pool(name="work", bufs=1, reuse_waits="tile") as work:
 
             def load_scales():
                 for q in range(4):
@@ -244,55 +224,110 @@ def tile_kanlinear_pa_k_kernel(
                         in_=spline_weight_scales[:, 4 * q : 4 * q + 4, :].rearrange("g r n -> r g n").bitcast(I32),
                     )
 
-            def turn(g):
-                v_scalar = turned.tile([P, ROWS], F32, name="v_scalar", tag="for_scalar")
-                v_vector = turned.tile([P, ROWS], F32, name="v_vector", tag="for_vector")
-                for bank in (v_scalar, v_vector):
-                    for r in range(ROW_TILES):
-                        nc.tensor.transpose(
-                            bank[:, r * P : (r + 1) * P], y_twice[r][:, g * P : (g + 1) * P], ident_f32[:]
-                        )
-                return v_scalar, v_vector
+            def load_weights(words_of_pass):
+                w_words = weights.tile([P, WORD_BYTES], U8, name="w_words", align_bytes=64)
+                nc.sync.dma_start(
+                    out=w_words[:].bitcast(I32), in_=words_of_pass.rearrange("p n t -> p (n t)").bitcast(I32)
+                )
+                return w_words
 
-            def square(g, v_scalar):
+            def turn(s):
+                banks = []
+                for tag in ("for_scalar", "for_vector"):
+                    bank = turned.tile([P, ROWS], F32, name="turned_y", tag=tag)
+                    for r in range(ROW_TILES):
+                        nc.tensor.transpose(bank[:, r * P : (r + 1) * P], y_rows[r][:, s * P : (s + 1) * P], ident_f32[:])
+                    banks.append(bank)
+                return banks
+
+            def square(s, y_scalar):
                 squares = []
-                for i in range(LOCAL_KNOTS):
+                for i in range(KNOTS):
                     one = square_pool.tile([P, ROWS], F32, name="one")
                     nc.scalar.activation(
                         out=one[:],
-                        in_=v_scalar[:],
+                        in_=y_scalar[:],
                         func=ACT.Square,
-                        scale=slope[:, g, i : i + 1],
-                        bias=shift[:, g, i : i + 1],
+                        scale=slope[:, s, i : i + 1],
+                        bias=shift[:, s, i : i + 1],
                     )
                     squares.append(one)
                 return squares
 
-            def cube(g, v_vector, squares):
-                cubes = work.tile([P, LOCAL_KNOTS, ROWS], F32, name="cubes")
-                for i in range(LOCAL_KNOTS):
+            def cube(s, y_vector, squares):
+                cubes = work.tile([P, KNOTS, ROWS], F32, name="cubes", bufs=2)
+                for i in range(KNOTS):
                     nc.vector.scalar_tensor_tensor(
                         out=cubes[:, i, :],
-                        in0=v_vector[:],
-                        scalar=minus_knots[:, g, i : i + 1],
+                        in0=y_vector[:],
+                        scalar=minus_knots[:, s, i : i + 1],
                         in1=squares[i][:],
                         op0=ALU.add,
                         op1=ALU.mult,
                     )
                 return cubes
 
-            def cut(g, cubes, on_vector):
-                inner = work.tile([P, 2 * HALF, ROWS], F32, name="inner")
-                for j in range(2 * HALF):
-                    source = cubes[:, j + 1 if j < HALF else j - 1, :]
-                    weight = cut_weight[:, g, j : j + 1]
-                    if j in on_vector:
-                        nc.vector.tensor_scalar(
-                            out=inner[:, j, :], in0=source, scalar1=weight, scalar2=0.0, op0=ALU.mult, op1=ALU.max
-                        )
-                    else:
-                        nc.scalar.activation(out=inner[:, j, :], in_=source, func=ACT.Relu, scale=weight)
-                return inner
+            def cut(s, cubes, on_vector):
+                pieces = {}
+                for name, first, count, first_knot in (
+                    ("left_early", 0, GPSIMD_LEFTS, 1),
+                    ("left_late", GPSIMD_LEFTS, BASES - GPSIMD_LEFTS, 1),
+                    ("right_early", BASES, HALF, 3 - BASES),
+                    ("right_late", BASES + HALF, HALF, 3 - BASES),
+                ):
+                    piece = work.tile([P, count, ROWS], F32, name=name)
+                    for j in range(first, first + count):
+                        source = cubes[:, j + first_knot, :]
+                        one_weight = weight[:, s, j : j + 1]
+                        if on_vector:
+                            nc.vector.tensor_scalar(
+                                out=piece[:, j - first, :],
+                                in0=source,
+                                scalar1=one_weight,
+                                scalar2=0.0,
+                                op0=ALU.mult,
+                                op1=ALU.max,
+                            )
+                        else:
+                            nc.scalar.activation(
+                                out=piece[:, j - first, :], in_=source, func=ACT.Relu, scale=one_weight
+                            )
+                    pieces[name] = piece
+                return pieces
+
+            def merge_left_early(engine, cubes, pieces):
+                left = work.tile([P, BASES, ROWS], BF16, name="left")
+                engine.tensor_tensor(
+                    out=left[:, 0:GPSIMD_LEFTS, :],
+                    in0=pieces["left_early"][:],
+                    in1=cubes[:, 0:GPSIMD_LEFTS, :],
+                    op=ALU.subtract,
+                )
+                return left
+
+            def merge_left_late(left, cubes, pieces):
+                nc.vector.tensor_tensor(
+                    out=left[:, GPSIMD_LEFTS:, :],
+                    in0=pieces["left_late"][:],
+                    in1=cubes[:, GPSIMD_LEFTS:BASES, :],
+                    op=ALU.subtract,
+                )
+
+            def merge_right(s, cubes, pieces):
+                right = work.tile([P, BASES, ROWS], BF16, name="right")
+                for j in range(HALF):
+                    nc.vector.scalar_tensor_tensor(
+                        out=right[:, j, :],
+                        in0=cubes[:, j + HALF, :],
+                        scalar=weight[:, s, 2 * BASES + j : 2 * BASES + j + 1],
+                        in1=pieces["right_early"][:, j, :],
+                        op0=ALU.mult,
+                        op1=ALU.add,
+                    )
+                nc.vector.tensor_tensor(
+                    out=right[:, HALF:, :], in0=cubes[:, BASES:, :], in1=pieces["right_late"][:], op=ALU.add
+                )
+                return right
 
             def planes(tile_slice):
                 return tile_slice.rearrange("p t (c i) -> p c t i", i=4)
@@ -300,40 +335,38 @@ def tile_kanlinear_pa_k_kernel(
             def words(tile_slice):
                 return tile_slice.rearrange("p (c i) t -> p c t i", i=4)
 
-            def merge_left(engine, cubes, inner):
-                left = work.tile([P, HALF, ROWS], BF16, name="left", bufs=1)
-                engine.tensor_tensor(out=left[:], in0=inner[:, 0:HALF, :], in1=cubes[:, 0:HALF, :], op=ALU.subtract)
-                return left
+            def pick(left, right):
+                for h in range(2):
+                    bases = slice(HALF * h, HALF * h + HALF)
+                    nc.vector.tensor_tensor(out=left[:, bases, :], in0=left[:, bases, :], in1=right[:, bases, :], op=ALU.min)
 
-            def merge_right(cubes, inner):
-                right = work.tile([P, HALF, ROWS], BF16, name="right")
-                nc.vector.tensor_tensor(out=right[:], in0=cubes[:, HALF:, :], in1=inner[:, HALF:, :], op=ALU.add)
-                return right
-
-            def pick(left, right, last):
-                pieces = [slice(half * ROWS // 2, (half + 1) * ROWS // 2) for half in range(2)]
-                for rows in pieces:
-                    nc.vector.tensor_tensor(out=left[:, :, rows], in0=left[:, :, rows], in1=right[:, :, rows], op=ALU.min)
-                basis = work.tile([P, ROWS, HALF], BF16, name="basis", align_bytes=64)
-                for rows in pieces:
-                    if last and rows.start == 0:
-                        nc.scalar.activation(
-                            out=words(basis[:, rows, :]), in_=planes(left[:, :, rows]), func=ACT.Relu, scale=-1.0
-                        )
-                    else:
-                        nc.vector.tensor_scalar(
-                            out=words(basis[:, rows, :]),
-                            in0=planes(left[:, :, rows]),
-                            scalar1=-1.0,
-                            scalar2=0.0,
-                            op0=ALU.mult,
-                            op1=ALU.max,
-                        )
+            def regroup(left, on_scalar):
+                basis = work.tile([P, 2, ROWS, HALF], BF16, name="basis", align_bytes=64, bufs=2)
+                for h in range(2):
+                    for part in range(2):
+                        rows = slice(part * ROWS // 2, (part + 1) * ROWS // 2)
+                        target = words(basis[:, h, rows, :])
+                        source = planes(left[:, HALF * h : HALF * h + HALF, rows])
+                        if (h, part) in on_scalar:
+                            nc.scalar.activation(out=target, in_=source, func=ACT.Relu, scale=-1.0)
+                        else:
+                            nc.vector.tensor_scalar(
+                                out=target, in0=source, scalar1=-1.0, scalar2=0.0, op0=ALU.mult, op1=ALU.max
+                            )
                 return basis
 
-            def multiply(values, w_words, scale_row, start, stop):
-                codes = work.tile([P, ROWS], U32, name="codes", align_bytes=64)
-                scales = work.tile([P, ROWS], U8, name="scales", align_bytes=64)
+            def pair_up(basis):
+                groups = []
+                for b in range(2):
+                    group = work.tile([P, ROWS, HALF], BF16, name="group", align_bytes=64, bufs=4)
+                    for h in range(2):
+                        nc.sync.dma_start(out=group[h:P:2, :, :], in_=basis[P // 2 * b : P // 2 * (b + 1), h, :, :])
+                    groups.append(group)
+                return groups
+
+            def multiply(values, w_words, scale_row):
+                codes = work.tile([P, ROWS], U32, name="codes", align_bytes=64, bufs=2)
+                scales = work.tile([P, ROWS], U8, name="scales", align_bytes=64, bufs=2)
                 nc.vector.quantize_mx(
                     out=codes[:].bitcast(FP8X4), scales=scales[:], in_=values[:].rearrange("p n t -> p (n t)")
                 )
@@ -344,69 +377,69 @@ def tile_kanlinear_pa_k_kernel(
                         lhsT_scale=scales[:, r * P : (r + 1) * P],
                         rhs=w_words[:].bitcast(FP8X4),
                         rhs_scale=scale_planes[:, scale_row, :],
-                        start=start,
-                        stop=stop,
+                        start=(scale_row == BASE_PASSES),
+                        stop=(scale_row == BASE_PASSES + GROUPS - 1),
                     )
 
-            def multiply_bases(g, basis, w_words):
-                multiply(basis, w_words, BASE_PASSES + g, g == 0, g == GROUPS - 1)
+            def multiply_set(s, groups):
+                for b in range(2):
+                    multiply(groups[b], w_of[2 * s + b], BASE_PASSES + 2 * s + b)
 
             def relu_step(g, t, relu_planes):
                 y_base = turned.tile([P, ROWS], F32, name="y_base", tag="for_scalar")
                 for r in range(ROW_TILES):
-                    features = y_twice[r][:].rearrange("n (g p t h) -> n g t h p", g=BASE_PASSES, p=P, t=PACK, h=2)
-                    nc.tensor.transpose(y_base[:, r * P : (r + 1) * P], features[:, g, t, 0, :], ident_f32[:])
+                    features = y_rows[r][:].rearrange("n (g p t) -> n g t p", g=BASE_PASSES, t=PACK)
+                    nc.tensor.transpose(y_base[:, r * P : (r + 1) * P], features[:, g, t, :], ident_f32[:])
                 nc.scalar.activation(
                     out=relu_planes[:, t, :], in_=y_base[:], func=ACT.Relu, bias=beta_of_base[:, g, t : t + 1]
                 )
 
             def relu_group(relu_planes):
-                grouped = work.tile([P, ROWS, PACK], BF16, name="grouped", align_bytes=64, bufs=1)
+                grouped = work.tile([P, ROWS, PACK], BF16, name="grouped", align_bytes=64)
                 nc.vector.tensor_copy(out=words(grouped[:]), in_=planes(relu_planes[:]))
                 return grouped
 
             with tc.manual_schedule():
-                w_of = {0: load_weights(spline_weight_words[0]), 1: load_weights(spline_weight_words[1])}
+                w_of = {g: load_weights(spline_weight_words[g]) for g in range(4)}
                 load_scales()
-                v_of = {0: turn(0), 1: turn(1)}
-                squares_of = {0: square(0, v_of[0][0]), 1: square(1, v_of[1][0])}
-                cubes_of = {0: cube(0, v_of[0][1], squares_of[0])}
-                inner_of = {0: cut(0, cubes_of[0], range(2 * HALF))}
-                basis_of = {}
-                relu_of = {}
-                for g in range(GROUPS):
-                    last = g == GROUPS - 1
+                y_of = {0: turn(0), 1: turn(1)}
+                squares_of = {0: square(0, y_of[0][0]), 1: square(1, y_of[1][0])}
+                cubes_of = {0: cube(0, y_of[0][1], squares_of[0])}
+                pieces_of = {0: cut(0, cubes_of[0], True)}
+                groups_of = {}
+                for s in range(SETS):
+                    last = s == SETS - 1
+                    left = merge_left_early(nc.vector if last else nc.gpsimd, cubes_of[s], pieces_of[s])
+                    if s + 2 < SETS:
+                        y_of[s + 2] = turn(s + 2)
+                        squares_of[s + 2] = square(s + 2, y_of[s + 2][0])
                     if not last:
-                        left = merge_left(nc.gpsimd, cubes_of[g], inner_of[g])
-                    if g + 2 < GROUPS:
-                        w_of[g + 2] = load_weights(spline_weight_words[g + 2])
-                        v_of[g + 2] = turn(g + 2)
-                        squares_of[g + 2] = square(g + 2, v_of[g + 2][0])
-                    if g + 1 < GROUPS:
-                        cubes_of[g + 1] = cube(g + 1, v_of[g + 1][1], squares_of[g + 1])
-                    if g + 2 < GROUPS:
-                        inner_of[g + 1] = cut(g + 1, cubes_of[g + 1], ())
-                    right = merge_right(cubes_of[g], inner_of[g])
-                    if g > 0:
-                        multiply_bases(g - 1, basis_of[g - 1], w_of[g - 1])
-                    step = g - 4
-                    if PACK <= step <= BASE_PASSES * PACK and step % PACK == 0:
-                        relu_values = relu_group(relu_of[step // PACK - 1])
-                    if PACK < step <= BASE_PASSES * PACK + 1 and step % PACK == 1:
+                        cubes_of[s + 1] = cube(s + 1, y_of[s + 1][1], squares_of[s + 1])
+                    merge_left_late(left, cubes_of[s], pieces_of[s])
+                    right = merge_right(s, cubes_of[s], pieces_of[s])
+                    if not last:
+                        pieces_of[s + 1] = cut(s + 1, cubes_of[s + 1], False)
+                    if s > 0:
+                        multiply_set(s - 1, groups_of[s - 1])
+                        if not last:
+                            for g in (2 * s + 2, 2 * s + 3):
+                                w_of[g] = load_weights(spline_weight_words[g])
+                    step = 2 * (s - 1)
+                    if s >= 3 and step <= BASE_PASSES * PACK and step % PACK == 0:
+                        relu_values = relu_group(relu_planes)
+                    if s >= 4 and step <= BASE_PASSES * PACK + 2 and step % PACK == 2:
                         branch = step // PACK - 1
-                        multiply(relu_values, load_weights(base_weight_words[branch]), branch, False, False)
-                    if 0 <= step < BASE_PASSES * PACK:
+                        multiply(relu_values, load_weights(base_weight_words[branch]), branch)
+                    if s >= 1 and step < BASE_PASSES * PACK:
                         if step % PACK == 0:
-                            relu_of[step // PACK] = work.tile([P, PACK, ROWS], BF16, name="relu_planes")
-                        relu_step(step // PACK, step % PACK, relu_of[step // PACK])
-                    if last:
-                        left = merge_left(nc.vector, cubes_of[g], inner_of[g])
-                    basis_of[g] = pick(left, right, last)
-                    if g + 2 == GROUPS:
-                        inner_of[g + 1] = cut(g + 1, cubes_of[g + 1], range(HALF, 2 * HALF))
-                multiply_bases(GROUPS - 1, basis_of[GROUPS - 1], w_of[GROUPS - 1])
+                            relu_planes = work.tile([P, PACK, ROWS], BF16, name="relu_planes")
+                        for one_step in (step, step + 1):
+                            relu_step(one_step // PACK, one_step % PACK, relu_planes)
+                    pick(left, right)
+                    groups_of[s] = pair_up(regroup(left, ((0, 0), (1, 0)) if last else ((0, 0),)))
+                multiply_set(SETS - 1, groups_of[SETS - 1])
 
                 for r in range(ROW_TILES):
-                    result = work.tile([P, UNITS], F32, name="result")
+                    result = work.tile([P, UNITS], F32, name="result", bufs=2)
                     nc.vector.tensor_tensor(out=result[:], in0=acc[r][:], in1=bias_rows[:], op=ALU.add)
                     nc.sync.dma_start(out=out[r * P : (r + 1) * P, :], in_=result[:])

@@ -53,7 +53,7 @@ def tile_kanlinear_pa_k_kernel(
     out,
 ):
     nc = tc.nc
-    with tc.tile_pool(name="keep", bufs=1) as keep, tc.tile_pool(name="squares", bufs=14) as square_pool, tc.tile_pool(
+    with tc.tile_pool(name="keep", bufs=1) as keep, tc.tile_pool(name="squares", bufs=KNOTS + 2) as square_pool, tc.tile_pool(
         name="weights", bufs=5
     ) as weights, tc.psum_pool(
         name="sums", bufs=1
@@ -75,18 +75,17 @@ def tile_kanlinear_pa_k_kernel(
             gamma_row = head.tile([P, FEATURES], BF16)
             set_rows = head.tile([P, P * KNOTS], BF16)
             beta_rows = head.tile([P, P], BF16)
-            nc.sync.dma_start(out=x_rows[0][:], in_=x[0:P, :])
+            for r in range(ROW_TILES):
+                nc.sync.dma_start(out=x_rows[r][:], in_=x[r * P : (r + 1) * P, :])
+            first = head.tile([P, 1], F32)
+            nc.vector.memset(first[:], 1.0)
+            nc.scalar.activation(out=first[:], in_=first[:], func=ACT.Abs_reciprocal_sqrt)
             nc.vector.memset(set_rows[:], 0.0)
             nc.scalar.dma_start(out=set_rows[0:SETS, :], in_=grid[0].rearrange("(s f) i -> s (f i)", f=P))
             nc.vector.memset(beta_rows[:], 0.0)
             nc.scalar.dma_start(out=beta_rows[0:SETS, :], in_=ln_beta.rearrange("(s f) -> s f", f=P))
             nc.vector.memset(gamma_row[:], 0.0)
             nc.scalar.dma_start(out=gamma_row[0:1, :], in_=ln_gamma.unsqueeze(0))
-            for r in range(1, ROW_TILES):
-                nc.sync.dma_start(out=x_rows[r][:], in_=x[r * P : (r + 1) * P, :])
-            first = head.tile([P, 1], F32)
-            nc.vector.memset(first[:], 1.0)
-            nc.scalar.activation(out=first[:], in_=first[:], func=ACT.Abs_reciprocal_sqrt)
             ones = head.tile([P, P], BF16)
             nc.gpsimd.memset(ones[:], 1.0)
             make_identity(nc, ident_bf16[:])
@@ -110,15 +109,17 @@ def tile_kanlinear_pa_k_kernel(
                 )
                 gamma_banks.append(bank)
 
-            minus_mean = head.tile([P, 1], F32)
-            squared = head.tile([P, 1], F32)
+            minus_mean = head.tile([P, 2], F32)
+            squared = head.tile([P, 2], F32)
             unused = head.tile([P, FEATURES], BF16)
-            nc.scalar.activation(
-                out=unused[:], in_=x_rows[0][:], func=ACT.Copy, scale=-1.0 / FEATURES, accum_out=minus_mean[:]
-            )
-            nc.scalar.activation(
-                out=unused[:], in_=x_rows[0][:], func=ACT.Square, bias=minus_mean[:], accum_out=squared[:]
-            )
+            for r in range(2):
+                column = slice(r, r + 1)
+                nc.scalar.activation(
+                    out=unused[:], in_=x_rows[r][:], func=ACT.Copy, scale=-1.0 / FEATURES, accum_out=minus_mean[:, column]
+                )
+                nc.scalar.activation(
+                    out=unused[:], in_=x_rows[r][:], func=ACT.Square, bias=minus_mean[:, column], accum_out=squared[:, column]
+                )
             moments = head.tile([P, ROW_TILES, 2], F32)
             spread = head.tile([P, ROW_TILES], F32)
             guess = head.tile([P, ROW_TILES], F32)
@@ -137,29 +138,29 @@ def tile_kanlinear_pa_k_kernel(
                     nc.vector.scalar_tensor_tensor(
                         out=centred[:, columns],
                         in0=x_rows[r][:, columns],
-                        scalar=minus_mean[:] if r == 0 else moments[:, r, 0:1],
+                        scalar=minus_mean[:, r : r + 1] if r < 2 else moments[:, r, 0:1],
                         in1=gamma_banks[c][:],
-                        op0=ALU.add if r == 0 else ALU.subtract,
+                        op0=ALU.add if r < 2 else ALU.subtract,
                         op1=ALU.mult,
                     )
                 return centred
 
-            statistics(1)
+            statistics(2)
             plain_knots = head.tile([P, SETS, KNOTS], F32)
             nc.vector.tensor_copy(out=plain_knots[:, :, 0:8], in_=turned_knots[:, :, 0:SETS].rearrange("p i s -> p s i"))
             nc.vector.tensor_copy(out=plain_knots[:, :, 8:], in_=turned_late[:, 0:4, 0:SETS].rearrange("p i s -> p s i"))
             beta_column = head.tile([P, SETS], F32)
             nc.vector.tensor_copy(out=beta_column[:], in_=turned_late[:, 4, 0:SETS])
-            statistics(2)
             statistics(3)
-            nc.vector.tensor_scalar(
-                out=spread[:, 0:1], in0=squared[:], scalar1=1.0 / FEATURES, scalar2=LN_EPS, op0=ALU.mult, op1=ALU.add
-            )
-            nc.vector.tensor_scalar_add(out=spread[:, 1:], in0=moments[:, 1:, 1], scalar1=LN_EPS)
-            nc.scalar.activation(out=guess[:], in_=spread[:], func=ACT.Abs_reciprocal_sqrt)
             centred = {0: centre(0)}
+            nc.vector.tensor_scalar(
+                out=spread[:, 0:2], in0=squared[:], scalar1=1.0 / FEATURES, scalar2=LN_EPS, op0=ALU.mult, op1=ALU.add
+            )
+            nc.vector.tensor_scalar_add(out=spread[:, 2:], in0=moments[:, 2:, 1], scalar1=LN_EPS)
+            nc.scalar.activation(out=guess[:], in_=spread[:], func=ACT.Abs_reciprocal_sqrt)
+            centred[1] = centre(1)
             refine_rsqrt(nc.vector, head, rstd[:], spread[:], guess[:], [P, ROW_TILES], "rstd")
-            for r in range(1, ROW_TILES):
+            for r in range(2, ROW_TILES):
                 centred[r] = centre(r)
 
             gap = {}
@@ -295,26 +296,18 @@ def tile_kanlinear_pa_k_kernel(
                     pieces[name] = piece
                 return pieces
 
-            def merge_left_early(engine, cubes, pieces):
-                left = work.tile([P, BASES, ROWS], BF16, name="left")
-                engine.tensor_tensor(
-                    out=left[:, 0:GPSIMD_LEFTS, :],
-                    in0=pieces["left_early"][:],
-                    in1=cubes[:, 0:GPSIMD_LEFTS, :],
-                    op=ALU.subtract,
-                )
-                return left
+            def merge_left(engine, left, cubes, pieces, bases):
+                for name, first in (("left_early", 0), ("left_late", GPSIMD_LEFTS)):
+                    own = slice(max(bases.start, first), min(bases.stop, first + pieces[name].shape[1]))
+                    if own.start < own.stop:
+                        engine.tensor_tensor(
+                            out=left[:, own, :],
+                            in0=pieces[name][:, own.start - first : own.stop - first, :],
+                            in1=cubes[:, own, :],
+                            op=ALU.subtract,
+                        )
 
-            def merge_left_late(left, cubes, pieces):
-                nc.vector.tensor_tensor(
-                    out=left[:, GPSIMD_LEFTS:, :],
-                    in0=pieces["left_late"][:],
-                    in1=cubes[:, GPSIMD_LEFTS:BASES, :],
-                    op=ALU.subtract,
-                )
-
-            def merge_right(s, cubes, pieces):
-                right = work.tile([P, BASES, ROWS], BF16, name="right")
+            def merge_right_early(s, right, cubes, pieces):
                 for j in range(HALF):
                     nc.vector.scalar_tensor_tensor(
                         out=right[:, j, :],
@@ -324,10 +317,11 @@ def tile_kanlinear_pa_k_kernel(
                         op0=ALU.mult,
                         op1=ALU.add,
                     )
+
+            def merge_right_late(right, cubes, pieces):
                 nc.vector.tensor_tensor(
                     out=right[:, HALF:, :], in0=cubes[:, BASES:, :], in1=pieces["right_late"][:], op=ALU.add
                 )
-                return right
 
             def planes(tile_slice):
                 return tile_slice.rearrange("p t (c i) -> p c t i", i=4)
@@ -335,42 +329,41 @@ def tile_kanlinear_pa_k_kernel(
             def words(tile_slice):
                 return tile_slice.rearrange("p (c i) t -> p c t i", i=4)
 
-            def pick(left, right):
-                for h in range(2):
-                    bases = slice(HALF * h, HALF * h + HALF)
-                    nc.vector.tensor_tensor(out=left[:, bases, :], in0=left[:, bases, :], in1=right[:, bases, :], op=ALU.min)
+            def pick(h, left, right):
+                bases = slice(HALF * h, HALF * h + HALF)
+                picked = (right, left)[h]
+                nc.vector.tensor_tensor(out=picked[:, bases, :], in0=left[:, bases, :], in1=right[:, bases, :], op=ALU.min)
+                return picked[:, bases, :]
 
-            def regroup(left, on_scalar):
-                basis = work.tile([P, 2, ROWS, HALF], BF16, name="basis", align_bytes=64, bufs=2)
-                for h in range(2):
-                    for part in range(2):
-                        rows = slice(part * ROWS // 2, (part + 1) * ROWS // 2)
-                        target = words(basis[:, h, rows, :])
-                        source = planes(left[:, HALF * h : HALF * h + HALF, rows])
-                        if (h, part) in on_scalar:
-                            nc.scalar.activation(out=target, in_=source, func=ACT.Relu, scale=-1.0)
-                        else:
-                            nc.vector.tensor_scalar(
-                                out=target, in0=source, scalar1=-1.0, scalar2=0.0, op0=ALU.mult, op1=ALU.max
-                            )
-                return basis
+            def regroup(picked, basis, h, rows, on_scalar):
+                target = words(basis[:, h, rows, :])
+                source = planes(picked[:, :, rows])
+                if on_scalar:
+                    nc.scalar.activation(out=target, in_=source, func=ACT.Relu, scale=-1.0)
+                else:
+                    nc.vector.tensor_scalar(
+                        out=target, in0=source, scalar1=-1.0, scalar2=0.0, op0=ALU.mult, op1=ALU.max
+                    )
 
-            def pair_up(basis):
-                groups = []
+            def pair_up(basis, groups, h, rows):
                 for b in range(2):
-                    group = work.tile([P, ROWS, HALF], BF16, name="group", align_bytes=64, bufs=4)
-                    for h in range(2):
-                        nc.sync.dma_start(out=group[h:P:2, :, :], in_=basis[P // 2 * b : P // 2 * (b + 1), h, :, :])
-                    groups.append(group)
-                return groups
+                    nc.sync.dma_start(
+                        out=groups[b][h:P:2, rows, :], in_=basis[P // 2 * b : P // 2 * (b + 1), h, rows, :]
+                    )
 
-            def multiply(values, w_words, scale_row):
+            def new_groups():
+                return [work.tile([P, ROWS, HALF], BF16, name="group", align_bytes=64, bufs=4) for b in range(2)]
+
+            def multiply(values, w_words, scale_row, row_tiles=range(ROW_TILES)):
+                rows = slice(row_tiles.start * P, row_tiles.stop * P)
                 codes = work.tile([P, ROWS], U32, name="codes", align_bytes=64, bufs=2)
                 scales = work.tile([P, ROWS], U8, name="scales", align_bytes=64, bufs=2)
                 nc.vector.quantize_mx(
-                    out=codes[:].bitcast(FP8X4), scales=scales[:], in_=values[:].rearrange("p n t -> p (n t)")
+                    out=codes[:, rows].bitcast(FP8X4),
+                    scales=scales[:, rows],
+                    in_=values[:, rows, :].rearrange("p n t -> p (n t)"),
                 )
-                for r in range(ROW_TILES):
+                for r in row_tiles:
                     nc.tensor.matmul_mx(
                         out=acc[r][:],
                         lhsT=codes[:, r * P : (r + 1) * P].bitcast(FP8X4),
@@ -381,9 +374,9 @@ def tile_kanlinear_pa_k_kernel(
                         stop=(scale_row == BASE_PASSES + GROUPS - 1),
                     )
 
-            def multiply_set(s, groups):
+            def multiply_set(s, groups, row_tiles=range(ROW_TILES)):
                 for b in range(2):
-                    multiply(groups[b], w_of[2 * s + b], BASE_PASSES + 2 * s + b)
+                    multiply(groups[b], w_of[2 * s + b], BASE_PASSES + 2 * s + b, row_tiles)
 
             def relu_step(g, t, relu_planes):
                 y_base = turned.tile([P, ROWS], F32, name="y_base", tag="for_scalar")
@@ -409,21 +402,24 @@ def tile_kanlinear_pa_k_kernel(
                 groups_of = {}
                 for s in range(SETS):
                     last = s == SETS - 1
-                    left = merge_left_early(nc.vector if last else nc.gpsimd, cubes_of[s], pieces_of[s])
+                    left = work.tile([P, BASES, ROWS], BF16, name="left")
+                    if not last:
+                        merge_left(nc.gpsimd, left, cubes_of[s], pieces_of[s], slice(0, GPSIMD_LEFTS))
                     if s + 2 < SETS:
                         y_of[s + 2] = turn(s + 2)
                         squares_of[s + 2] = square(s + 2, y_of[s + 2][0])
                     if not last:
                         cubes_of[s + 1] = cube(s + 1, y_of[s + 1][1], squares_of[s + 1])
-                    merge_left_late(left, cubes_of[s], pieces_of[s])
-                    right = merge_right(s, cubes_of[s], pieces_of[s])
+                    right = work.tile([P, BASES, ROWS], BF16, name="right")
                     if not last:
+                        merge_left(nc.vector, left, cubes_of[s], pieces_of[s], slice(GPSIMD_LEFTS, BASES))
+                        merge_right_early(s, right, cubes_of[s], pieces_of[s])
+                        merge_right_late(right, cubes_of[s], pieces_of[s])
                         pieces_of[s + 1] = cut(s + 1, cubes_of[s + 1], False)
-                    if s > 0:
+                    if 0 < s < SETS - 1:
                         multiply_set(s - 1, groups_of[s - 1])
-                        if not last:
-                            for g in (2 * s + 2, 2 * s + 3):
-                                w_of[g] = load_weights(spline_weight_words[g])
+                        for g in (2 * s + 2, 2 * s + 3):
+                            w_of[g] = load_weights(spline_weight_words[g])
                     step = 2 * (s - 1)
                     if s >= 3 and step <= BASE_PASSES * PACK and step % PACK == 0:
                         relu_values = relu_group(relu_planes)
@@ -435,9 +431,33 @@ def tile_kanlinear_pa_k_kernel(
                             relu_planes = work.tile([P, PACK, ROWS], BF16, name="relu_planes")
                         for one_step in (step, step + 1):
                             relu_step(one_step // PACK, one_step % PACK, relu_planes)
-                    pick(left, right)
-                    groups_of[s] = pair_up(regroup(left, ((0, 0), (1, 0)) if last else ((0, 0),)))
-                multiply_set(SETS - 1, groups_of[SETS - 1])
+                    basis = work.tile([P, 2, ROWS, HALF], BF16, name="basis", align_bytes=64, bufs=2)
+                    groups_of[s] = new_groups()
+                    if not last:
+                        low = pick(0, left, right)
+                        high = pick(1, left, right)
+                        share = ROWS // 2 if 1 <= s <= 8 else 3 * ROWS // 4
+                        regroup(low, basis, 0, slice(0, share), True)
+                        regroup(low, basis, 0, slice(share, ROWS), False)
+                        regroup(high, basis, 1, slice(0, ROWS), False)
+                        for h in range(2):
+                            pair_up(basis, groups_of[s], h, slice(0, ROWS))
+                halves = [slice(0, ROWS // 2), slice(ROWS // 2, ROWS)]
+                merge_left(nc.vector, left, cubes_of[SETS - 1], pieces_of[SETS - 1], slice(0, HALF))
+                merge_right_early(SETS - 1, right, cubes_of[SETS - 1], pieces_of[SETS - 1])
+                low = pick(0, left, right)
+                multiply_set(SETS - 2, groups_of[SETS - 2])
+                for rows in halves:
+                    regroup(low, basis, 0, rows, True)
+                    pair_up(basis, groups_of[SETS - 1], 0, rows)
+                merge_left(nc.vector, left, cubes_of[SETS - 1], pieces_of[SETS - 1], slice(HALF, BASES))
+                merge_right_late(right, cubes_of[SETS - 1], pieces_of[SETS - 1])
+                high = pick(1, left, right)
+                for rows, on_scalar in zip(halves, (False, True)):
+                    regroup(high, basis, 1, rows, on_scalar)
+                    pair_up(basis, groups_of[SETS - 1], 1, rows)
+                for row_tiles in (range(0, 2), range(2, ROW_TILES)):
+                    multiply_set(SETS - 1, groups_of[SETS - 1], row_tiles)
 
                 for r in range(ROW_TILES):
                     result = work.tile([P, UNITS], F32, name="result", bufs=2)

@@ -26,6 +26,7 @@ GROUPS = FEATURES * BASES // K_PASS
 BANK = 512
 WORD_BYTES = PACK * UNITS
 GPSIMD_LEFTS = 6
+RELU_ROUNDS = 14
 LN_EPS = 0.001
 
 FLOPS = 2 * ROWS * (FEATURES + FEATURES * BASES) * UNITS
@@ -53,7 +54,7 @@ def tile_kanlinear_pa_k_kernel(
     out,
 ):
     nc = tc.nc
-    with tc.tile_pool(name="keep", bufs=1) as keep, tc.tile_pool(name="squares", bufs=KNOTS + 2) as square_pool, tc.tile_pool(
+    with tc.tile_pool(name="keep", bufs=1) as keep, tc.tile_pool(name="squares", bufs=KNOTS + 1) as square_pool, tc.tile_pool(
         name="weights", bufs=5
     ) as weights, tc.psum_pool(
         name="sums", bufs=1
@@ -67,7 +68,8 @@ def tile_kanlinear_pa_k_kernel(
         shift = keep.tile([P, SETS, KNOTS], F32)
         weight = keep.tile([P, SETS, 2 * BASES + HALF], F32)
         bias_rows = keep.tile([P, UNITS], BF16)
-        beta_of_base = keep.tile([P, BASE_PASSES, PACK], BF16)
+        ones = keep.tile([P, P], BF16)
+        beta_row = keep.tile([P, FEATURES], BF16)
         acc = [sums.tile([P, UNITS], F32, name="acc%d" % r) for r in range(ROW_TILES)]
 
         with tc.tile_pool(name="head", bufs=1) as head, tc.tile_pool(name="head2", bufs=2) as head2, tc.manual_schedule():
@@ -75,7 +77,7 @@ def tile_kanlinear_pa_k_kernel(
             gamma_row = head.tile([P, FEATURES], BF16)
             set_rows = head.tile([P, P * KNOTS], BF16)
             beta_rows = head.tile([P, P], BF16)
-            for r in range(ROW_TILES):
+            for r in (0, 2, 1, 3):
                 nc.sync.dma_start(out=x_rows[r][:], in_=x[r * P : (r + 1) * P, :])
             first = head.tile([P, 1], F32)
             nc.vector.memset(first[:], 1.0)
@@ -86,7 +88,6 @@ def tile_kanlinear_pa_k_kernel(
             nc.scalar.dma_start(out=beta_rows[0:SETS, :], in_=ln_beta.rearrange("(s f) -> s f", f=P))
             nc.vector.memset(gamma_row[:], 0.0)
             nc.scalar.dma_start(out=gamma_row[0:1, :], in_=ln_gamma.unsqueeze(0))
-            ones = head.tile([P, P], BF16)
             nc.gpsimd.memset(ones[:], 1.0)
             make_identity(nc, ident_bf16[:])
             make_identity(nc, ident_f32[:])
@@ -160,8 +161,8 @@ def tile_kanlinear_pa_k_kernel(
             nc.scalar.activation(out=guess[:], in_=spread[:], func=ACT.Abs_reciprocal_sqrt)
             centred[1] = centre(1)
             refine_rsqrt(nc.vector, head, rstd[:], spread[:], guess[:], [P, ROW_TILES], "rstd")
-            for r in range(2, ROW_TILES):
-                centred[r] = centre(r)
+            centred[2] = centre(2)
+            centred[3] = centre(3)
 
             gap = {}
             for span in (1, 2, 3, 4):
@@ -202,14 +203,14 @@ def tile_kanlinear_pa_k_kernel(
             nc.scalar.copy(out=top[:, :, firsts], in_=rise[:, :, 4:8])
             nc.scalar.copy(out=bottom[:, :, firsts], in_=fall[:, :, 1:5])
 
-            for r in range(ROW_TILES - 1):
+            for r in range(2):
                 nc.scalar.activation(out=y_rows[r][:], in_=centred[r][:], func=ACT.Copy, scale=rstd[:, r : r + 1])
-            nc.vector.tensor_scalar_mul(out=y_rows[3][:], in0=centred[3][:], scalar1=rstd[:, 3:4])
+            for r in range(2, ROW_TILES):
+                nc.vector.tensor_scalar_mul(out=y_rows[r][:], in0=centred[r][:], scalar1=rstd[:, r : r + 1])
             nc.vector.reciprocal(out=bottom[:], in_=bottom[:])
             nc.gpsimd.tensor_tensor(out=weight[:], in0=top[:], in1=bottom[:], op=ALU.mult)
-            nc.scalar.dma_start(
-                out=beta_of_base[:], in_=ln_beta.rearrange("(g p t) -> p g t", g=BASE_PASSES, t=PACK)
-            )
+            nc.gpsimd.memset(beta_row[:].bitcast(I32), 0)
+            nc.scalar.dma_start(out=beta_row[0:1, :], in_=ln_beta.unsqueeze(0))
             nc.scalar.dma_start(out=bias_rows[:], in_=base_bias.partition_broadcast(P))
 
         with tc.tile_pool(name="work", bufs=1, reuse_waits="tile") as work:
@@ -296,31 +297,29 @@ def tile_kanlinear_pa_k_kernel(
                     pieces[name] = piece
                 return pieces
 
-            def merge_left(engine, left, cubes, pieces, bases):
+            def merge_left(engine, left, cubes, pieces, bases, rows=slice(0, ROWS)):
                 for name, first in (("left_early", 0), ("left_late", GPSIMD_LEFTS)):
                     own = slice(max(bases.start, first), min(bases.stop, first + pieces[name].shape[1]))
                     if own.start < own.stop:
                         engine.tensor_tensor(
-                            out=left[:, own, :],
-                            in0=pieces[name][:, own.start - first : own.stop - first, :],
-                            in1=cubes[:, own, :],
+                            out=left[:, own, rows],
+                            in0=pieces[name][:, own.start - first : own.stop - first, rows],
+                            in1=cubes[:, own, rows],
                             op=ALU.subtract,
                         )
 
-            def merge_right_early(s, right, cubes, pieces):
+            def merge_right(s, right, cubes, pieces, rows=slice(0, ROWS)):
                 for j in range(HALF):
                     nc.vector.scalar_tensor_tensor(
-                        out=right[:, j, :],
-                        in0=cubes[:, j + HALF, :],
+                        out=right[:, j, rows],
+                        in0=cubes[:, j + HALF, rows],
                         scalar=weight[:, s, 2 * BASES + j : 2 * BASES + j + 1],
-                        in1=pieces["right_early"][:, j, :],
+                        in1=pieces["right_early"][:, j, rows],
                         op0=ALU.mult,
                         op1=ALU.add,
                     )
-
-            def merge_right_late(right, cubes, pieces):
                 nc.vector.tensor_tensor(
-                    out=right[:, HALF:, :], in0=cubes[:, BASES:, :], in1=pieces["right_late"][:], op=ALU.add
+                    out=right[:, HALF:, rows], in0=cubes[:, BASES:, rows], in1=pieces["right_late"][:, :, rows], op=ALU.add
                 )
 
             def planes(tile_slice):
@@ -329,10 +328,12 @@ def tile_kanlinear_pa_k_kernel(
             def words(tile_slice):
                 return tile_slice.rearrange("p (c i) t -> p c t i", i=4)
 
-            def pick(h, left, right):
+            def pick(h, left, right, rows=slice(0, ROWS)):
                 bases = slice(HALF * h, HALF * h + HALF)
                 picked = (right, left)[h]
-                nc.vector.tensor_tensor(out=picked[:, bases, :], in0=left[:, bases, :], in1=right[:, bases, :], op=ALU.min)
+                nc.vector.tensor_tensor(
+                    out=picked[:, bases, rows], in0=left[:, bases, rows], in1=right[:, bases, rows], op=ALU.min
+                )
                 return picked[:, bases, :]
 
             def regroup(picked, basis, h, rows, on_scalar):
@@ -356,8 +357,8 @@ def tile_kanlinear_pa_k_kernel(
 
             def multiply(values, w_words, scale_row, row_tiles=range(ROW_TILES)):
                 rows = slice(row_tiles.start * P, row_tiles.stop * P)
-                codes = work.tile([P, ROWS], U32, name="codes", align_bytes=64, bufs=2)
-                scales = work.tile([P, ROWS], U8, name="scales", align_bytes=64, bufs=2)
+                codes = work.tile([P, ROWS], U32, name="codes", align_bytes=64, bufs=3)
+                scales = work.tile([P, ROWS], U8, name="scales", align_bytes=64, bufs=3)
                 nc.vector.quantize_mx(
                     out=codes[:, rows].bitcast(FP8X4),
                     scales=scales[:, rows],
@@ -378,19 +379,31 @@ def tile_kanlinear_pa_k_kernel(
                 for b in range(2):
                     multiply(groups[b], w_of[2 * s + b], BASE_PASSES + 2 * s + b, row_tiles)
 
-            def relu_step(g, t, relu_planes):
-                y_base = turned.tile([P, ROWS], F32, name="y_base", tag="for_scalar")
-                for r in range(ROW_TILES):
-                    features = y_rows[r][:].rearrange("n (g p t) -> n g t p", g=BASE_PASSES, t=PACK)
-                    nc.tensor.transpose(y_base[:, r * P : (r + 1) * P], features[:, g, t, :], ident_f32[:])
+            def relu_step(g, r, grouped):
+                xn = turned.tile([P, PACK, P], F32, name="xn", tag="for_scalar")
+                y_by_slot = y_rows[r][:].rearrange("n (g p t) -> n g t p", g=BASE_PASSES, t=PACK)
+                beta_by_slot = beta_row[:].rearrange("n (g p t) -> n g t p", g=BASE_PASSES, t=PACK)
+                for t in range(PACK):
+                    nc.tensor.matmul(
+                        out=xn[:, t, :],
+                        lhsT=y_by_slot[:, g, t, :],
+                        rhs=ident_f32[:],
+                        is_transpose=True,
+                        start=True,
+                        stop=False,
+                    )
+                    nc.tensor.matmul(
+                        out=xn[:, t, :], lhsT=beta_by_slot[:, g, t, :], rhs=ones[:], start=False, stop=True
+                    )
                 nc.scalar.activation(
-                    out=relu_planes[:, t, :], in_=y_base[:], func=ACT.Relu, bias=beta_of_base[:, g, t : t + 1]
+                    out=grouped[:, r * P : (r + 1) * P, :], in_=xn[:].rearrange("p t n -> p n t"), func=ACT.Relu
                 )
 
-            def relu_group(relu_planes):
-                grouped = work.tile([P, ROWS, PACK], BF16, name="grouped", align_bytes=64)
-                nc.vector.tensor_copy(out=words(grouped[:]), in_=planes(relu_planes[:]))
-                return grouped
+            def store(row_tiles):
+                for r in row_tiles:
+                    result = work.tile([P, UNITS], F32, name="result", bufs=2)
+                    nc.vector.tensor_tensor(out=result[:], in0=acc[r][:], in1=bias_rows[:], op=ALU.add)
+                    nc.sync.dma_start(out=out[r * P : (r + 1) * P, :], in_=result[:])
 
             with tc.manual_schedule():
                 w_of = {g: load_weights(spline_weight_words[g]) for g in range(4)}
@@ -400,6 +413,7 @@ def tile_kanlinear_pa_k_kernel(
                 cubes_of = {0: cube(0, y_of[0][1], squares_of[0])}
                 pieces_of = {0: cut(0, cubes_of[0], True)}
                 groups_of = {}
+                relu_ready = []
                 for s in range(SETS):
                     last = s == SETS - 1
                     left = work.tile([P, BASES, ROWS], BF16, name="left")
@@ -413,53 +427,50 @@ def tile_kanlinear_pa_k_kernel(
                     right = work.tile([P, BASES, ROWS], BF16, name="right")
                     if not last:
                         merge_left(nc.vector, left, cubes_of[s], pieces_of[s], slice(GPSIMD_LEFTS, BASES))
-                        merge_right_early(s, right, cubes_of[s], pieces_of[s])
-                        merge_right_late(right, cubes_of[s], pieces_of[s])
+                        merge_right(s, right, cubes_of[s], pieces_of[s])
                         pieces_of[s + 1] = cut(s + 1, cubes_of[s + 1], False)
                     if 0 < s < SETS - 1:
+                        for values, branch in relu_ready:
+                            multiply(values, load_weights(base_weight_words[branch]), branch)
+                        relu_ready = []
                         multiply_set(s - 1, groups_of[s - 1])
                         for g in (2 * s + 2, 2 * s + 3):
                             w_of[g] = load_weights(spline_weight_words[g])
-                    step = 2 * (s - 1)
-                    if s >= 3 and step <= BASE_PASSES * PACK and step % PACK == 0:
-                        relu_values = relu_group(relu_planes)
-                    if s >= 4 and step <= BASE_PASSES * PACK + 2 and step % PACK == 2:
-                        branch = step // PACK - 1
-                        multiply(relu_values, load_weights(base_weight_words[branch]), branch)
-                    if s >= 1 and step < BASE_PASSES * PACK:
-                        if step % PACK == 0:
-                            relu_planes = work.tile([P, PACK, ROWS], BF16, name="relu_planes")
-                        for one_step in (step, step + 1):
-                            relu_step(one_step // PACK, one_step % PACK, relu_planes)
+                    if s < RELU_ROUNDS:
+                        steps = BASE_PASSES * ROW_TILES
+                        for step in range(steps * s // RELU_ROUNDS, steps * (s + 1) // RELU_ROUNDS):
+                            branch, r = step // ROW_TILES, step % ROW_TILES
+                            if r == 0:
+                                grouped = work.tile([P, ROWS, PACK], BF16, name="grouped", align_bytes=64)
+                            relu_step(branch, r, grouped)
+                            if r == ROW_TILES - 1:
+                                relu_ready.append((grouped, branch))
                     basis = work.tile([P, 2, ROWS, HALF], BF16, name="basis", align_bytes=64, bufs=2)
                     groups_of[s] = new_groups()
                     if not last:
                         low = pick(0, left, right)
                         high = pick(1, left, right)
-                        share = ROWS // 2 if 1 <= s <= 8 else 3 * ROWS // 4
-                        regroup(low, basis, 0, slice(0, share), True)
-                        regroup(low, basis, 0, slice(share, ROWS), False)
-                        regroup(high, basis, 1, slice(0, ROWS), False)
+                        if s + 2 < SETS:
+                            regroup(low, basis, 0, slice(0, ROWS // 2), True)
+                            regroup(low, basis, 0, slice(ROWS // 2, ROWS), False)
+                            regroup(high, basis, 1, slice(0, ROWS), False)
+                        else:
+                            regroup(low, basis, 0, slice(0, ROWS), True)
+                            regroup(high, basis, 1, slice(0, ROWS), False)
                         for h in range(2):
                             pair_up(basis, groups_of[s], h, slice(0, ROWS))
-                halves = [slice(0, ROWS // 2), slice(ROWS // 2, ROWS)]
-                merge_left(nc.vector, left, cubes_of[SETS - 1], pieces_of[SETS - 1], slice(0, HALF))
-                merge_right_early(SETS - 1, right, cubes_of[SETS - 1], pieces_of[SETS - 1])
-                low = pick(0, left, right)
-                multiply_set(SETS - 2, groups_of[SETS - 2])
-                for rows in halves:
-                    regroup(low, basis, 0, rows, True)
-                    pair_up(basis, groups_of[SETS - 1], 0, rows)
-                merge_left(nc.vector, left, cubes_of[SETS - 1], pieces_of[SETS - 1], slice(HALF, BASES))
-                merge_right_late(right, cubes_of[SETS - 1], pieces_of[SETS - 1])
-                high = pick(1, left, right)
-                for rows, on_scalar in zip(halves, (False, True)):
-                    regroup(high, basis, 1, rows, on_scalar)
-                    pair_up(basis, groups_of[SETS - 1], 1, rows)
+                s = SETS - 1
+                waiting = (s - 1, range(ROW_TILES))
                 for row_tiles in (range(0, 2), range(2, ROW_TILES)):
-                    multiply_set(SETS - 1, groups_of[SETS - 1], row_tiles)
-
-                for r in range(ROW_TILES):
-                    result = work.tile([P, UNITS], F32, name="result", bufs=2)
-                    nc.vector.tensor_tensor(out=result[:], in0=acc[r][:], in1=bias_rows[:], op=ALU.add)
-                    nc.sync.dma_start(out=out[r * P : (r + 1) * P, :], in_=result[:])
+                    rows = slice(row_tiles.start * P, row_tiles.stop * P)
+                    merge_left(nc.vector, left, cubes_of[s], pieces_of[s], slice(0, BASES), rows)
+                    merge_right(s, right, cubes_of[s], pieces_of[s], rows)
+                    multiply_set(waiting[0], groups_of[waiting[0]], waiting[1])
+                    waiting = (s, row_tiles)
+                    for h in range(2):
+                        on_scalar = h == 0 or row_tiles.stop < ROW_TILES
+                        regroup(pick(h, left, right, rows), basis, h, rows, on_scalar)
+                        pair_up(basis, groups_of[s], h, rows)
+                store(range(0, 2))
+                multiply_set(s, groups_of[s], waiting[1])
+                store(range(2, ROW_TILES))

@@ -25,6 +25,7 @@ BASE_PASSES = FEATURES // K_PASS
 GROUPS = FEATURES * BASES // K_PASS
 BANK = 512
 WORD_BYTES = PACK * UNITS
+RATIO_RIGHTS = (0, 1, 2, 4, 6)
 GPSIMD_LEFTS = 6
 RELU_ROUNDS = 14
 LN_EPS = 0.001
@@ -54,7 +55,7 @@ def tile_kanlinear_pa_k_kernel(
     out,
 ):
     nc = tc.nc
-    with tc.tile_pool(name="keep", bufs=1) as keep, tc.tile_pool(name="squares", bufs=KNOTS + 1) as square_pool, tc.tile_pool(
+    with tc.tile_pool(name="keep", bufs=1) as keep, tc.tile_pool(name="squares", bufs=KNOTS + 4) as square_pool, tc.tile_pool(
         name="weights", bufs=5
     ) as weights, tc.psum_pool(
         name="sums", bufs=1
@@ -63,12 +64,12 @@ def tile_kanlinear_pa_k_kernel(
         ident_bf16 = keep.tile([P, P], BF16)
         scale_planes = keep.tile([P, BASE_PASSES + GROUPS, UNITS], U8, align_bytes=64)
         y_rows = [keep.tile([P, FEATURES], F32, name="y_rows%d" % r) for r in range(ROW_TILES)]
-        minus_knots = keep.tile([P, SETS, KNOTS], F32)
+        knots = keep.tile([P, SETS, KNOTS], F32)
         slope = keep.tile([P, SETS, KNOTS], F32)
         shift = keep.tile([P, SETS, KNOTS], F32)
-        weight = keep.tile([P, SETS, 2 * BASES + HALF], F32)
+        weight = keep.tile([P, SETS, 3 * BASES + BASES - GPSIMD_LEFTS], F32)
         bias_rows = keep.tile([P, UNITS], BF16)
-        ones = keep.tile([P, P], BF16)
+        minus_ones = keep.tile([P, P], BF16)
         beta_row = keep.tile([P, FEATURES], BF16)
         acc = [sums.tile([P, UNITS], F32, name="acc%d" % r) for r in range(ROW_TILES)]
 
@@ -88,10 +89,13 @@ def tile_kanlinear_pa_k_kernel(
             nc.scalar.dma_start(out=beta_rows[0:SETS, :], in_=ln_beta.rearrange("(s f) -> s f", f=P))
             nc.vector.memset(gamma_row[:], 0.0)
             nc.scalar.dma_start(out=gamma_row[0:1, :], in_=ln_gamma.unsqueeze(0))
-            nc.gpsimd.memset(ones[:], 1.0)
+            nc.gpsimd.memset(minus_ones[:], -1.0)
             make_identity(nc, ident_bf16[:])
             make_identity(nc, ident_f32[:])
+            nc.gpsimd.memset(beta_row[:].bitcast(I32), 0)
             nc.gpsimd.memset(scale_planes[:].bitcast(I32), 0)
+            nc.sync.dma_start(out=beta_row[0:1, :], in_=ln_beta.unsqueeze(0))
+            nc.sync.dma_start(out=bias_rows[:], in_=base_bias.partition_broadcast(P))
 
             turned_knots = acc[0][:].bitcast(BF16).rearrange("p (i s) -> p i s", s=P)
             turned_late = acc[1][:].bitcast(BF16).rearrange("p (i s) -> p i s", s=P)
@@ -106,7 +110,7 @@ def tile_kanlinear_pa_k_kernel(
             for c in range(FEATURES // BANK):
                 bank = turned.tile([P, BANK], F32, name="gamma_bank", tag="for_scalar" if c % 2 == 0 else "for_vector")
                 nc.tensor.matmul(
-                    out=bank[:], lhsT=ones[:], rhs=gamma_row[:, c * BANK : (c + 1) * BANK], start=True, stop=True
+                    out=bank[:], lhsT=minus_ones[:], rhs=gamma_row[:, c * BANK : (c + 1) * BANK], start=True, stop=True
                 )
                 gamma_banks.append(bank)
 
@@ -154,6 +158,13 @@ def tile_kanlinear_pa_k_kernel(
             nc.vector.tensor_copy(out=beta_column[:], in_=turned_late[:, 4, 0:SETS])
             statistics(3)
             centred = {0: centre(0)}
+            gap = {span: head.tile([P, SETS, KNOTS - span], F32, name="gap%d" % span) for span in (1, 2, 3, 4)}
+            for span in gap:
+                nc.gpsimd.tensor_tensor(
+                    out=gap[span][:], in0=plain_knots[:, :, span:], in1=plain_knots[:, :, 0 : KNOTS - span], op=ALU.subtract
+                )
+            one_by_gap = head.tile([P, SETS, 3], F32)
+            nc.vector.reciprocal(out=one_by_gap[:], in_=gap[4][:, :, 3::2])
             nc.vector.tensor_scalar(
                 out=spread[:, 0:2], in0=squared[:], scalar1=1.0 / FEATURES, scalar2=LN_EPS, op0=ALU.mult, op1=ALU.add
             )
@@ -164,13 +175,6 @@ def tile_kanlinear_pa_k_kernel(
             centred[2] = centre(2)
             centred[3] = centre(3)
 
-            gap = {}
-            for span in (1, 2, 3, 4):
-                count = KNOTS - span
-                gap[span] = head.tile([P, SETS, count], F32, name="gap%d" % span)
-                nc.gpsimd.tensor_tensor(
-                    out=gap[span][:], in0=plain_knots[:, :, span:], in1=plain_knots[:, :, 0:count], op=ALU.subtract
-                )
             rise = head.tile([P, SETS, 9], F32)
             nc.gpsimd.tensor_tensor(out=rise[:], in0=gap[1][:, :, 0:9], in1=gap[2][:, :, 0:9], op=ALU.mult)
             nc.gpsimd.tensor_tensor(out=rise[:], in0=rise[:], in1=gap[3][:], op=ALU.mult)
@@ -178,40 +182,50 @@ def tile_kanlinear_pa_k_kernel(
             nc.gpsimd.tensor_tensor(out=fall[:], in0=gap[1][:, :, 2:11], in1=gap[2][:, :, 1:10], op=ALU.mult)
             nc.gpsimd.tensor_tensor(out=fall[:], in0=fall[:], in1=gap[3][:], op=ALU.mult)
             volume = head.tile([P, SETS, KNOTS], F32)
-            nc.scalar.copy(out=volume[:, :, 0:BASES], in_=rise[:, :, 0:BASES])
-            nc.scalar.copy(out=volume[:, :, BASES:], in_=fall[:, :, 5:9])
+            nc.scalar.copy(out=volume[:, :, 0:6], in_=rise[:, :, 0:6])
+            nc.scalar.copy(out=volume[:, :, 7::2], in_=fall[:, :, 4::2])
+            inner_volume = head.tile([P, SETS, 3], F32)
+            nc.gpsimd.tensor_tensor(out=inner_volume[:], in0=gap[1][:, :, 6::2], in1=fall[:, :, 3::2], op=ALU.mult)
+            nc.gpsimd.tensor_tensor(out=volume[:, :, 6::2], in0=inner_volume[:], in1=one_by_gap[:], op=ALU.mult)
             slope_guess = head.tile([P, SETS, KNOTS], F32)
             nc.scalar.activation(out=slope_guess[:], in_=volume[:], func=ACT.Abs_reciprocal_sqrt)
             refine_rsqrt(nc.gpsimd, head, slope[:], volume[:], slope_guess[:], [P, SETS, KNOTS], "slope")
             nc.gpsimd.tensor_tensor(
-                out=minus_knots[:],
-                in0=beta_column[:].unsqueeze(2).to_broadcast([P, SETS, KNOTS]),
-                in1=plain_knots[:],
+                out=knots[:],
+                in0=plain_knots[:],
+                in1=beta_column[:].unsqueeze(2).to_broadcast([P, SETS, KNOTS]),
                 op=ALU.subtract,
             )
-            nc.gpsimd.tensor_tensor(out=shift[:], in0=slope[:], in1=minus_knots[:], op=ALU.mult)
-            top = head.tile([P, SETS, 2 * BASES + HALF], F32)
-            bottom = head.tile([P, SETS, 2 * BASES + HALF], F32)
-            lefts, rights, firsts = slice(0, BASES), slice(BASES, 2 * BASES), slice(2 * BASES, None)
+            nc.gpsimd.tensor_tensor(out=shift[:], in0=slope[:], in1=knots[:], op=ALU.mult)
+            top = head.tile([P, SETS, 3 * BASES + BASES - GPSIMD_LEFTS], F32)
+            bottom = head.tile([P, SETS, 3 * BASES + BASES - GPSIMD_LEFTS], F32)
+            lefts, rights = slice(0, BASES), slice(BASES, 2 * BASES)
+            right_outers, left_outers = slice(2 * BASES, 3 * BASES), slice(3 * BASES, None)
             nc.gpsimd.tensor_tensor(out=top[:, :, lefts], in0=gap[4][:], in1=volume[:, :, 1:9], op=ALU.mult)
+            nc.gpsimd.tensor_scalar(
+                out=top[:, :, lefts], in0=top[:, :, lefts], scalar1=-1.0, scalar2=0.0, op0=ALU.mult, op1=ALU.add
+            )
             nc.gpsimd.tensor_tensor(out=bottom[:, :, lefts], in0=gap[1][:, :, 0:8], in1=rise[:, :, 1:9], op=ALU.mult)
             nc.gpsimd.tensor_tensor(out=top[:, :, rights], in0=gap[4][:], in1=volume[:, :, 3:11], op=ALU.mult)
-            nc.gpsimd.tensor_scalar(
-                out=top[:, :, rights], in0=top[:, :, rights], scalar1=-1.0, scalar2=0.0, op0=ALU.mult, op1=ALU.add
-            )
             nc.gpsimd.tensor_tensor(out=bottom[:, :, rights], in0=gap[1][:, :, 3:11], in1=fall[:, :, 0:8], op=ALU.mult)
-            nc.scalar.copy(out=top[:, :, firsts], in_=rise[:, :, 4:8])
-            nc.scalar.copy(out=bottom[:, :, firsts], in_=fall[:, :, 1:5])
+            nc.gpsimd.tensor_scalar(
+                out=top[:, :, right_outers], in0=volume[:, :, 4:], scalar1=-1.0, scalar2=0.0, op0=ALU.mult, op1=ALU.add
+            )
+            nc.scalar.copy(out=bottom[:, :, right_outers], in_=fall[:, :, 1:9])
+            nc.scalar.copy(out=top[:, :, left_outers], in_=volume[:, :, GPSIMD_LEFTS:BASES])
+            nc.scalar.copy(out=bottom[:, :, left_outers], in_=rise[:, :, GPSIMD_LEFTS:BASES])
 
             for r in range(2):
                 nc.scalar.activation(out=y_rows[r][:], in_=centred[r][:], func=ACT.Copy, scale=rstd[:, r : r + 1])
             for r in range(2, ROW_TILES):
                 nc.vector.tensor_scalar_mul(out=y_rows[r][:], in0=centred[r][:], scalar1=rstd[:, r : r + 1])
-            nc.vector.reciprocal(out=bottom[:], in_=bottom[:])
-            nc.gpsimd.tensor_tensor(out=weight[:], in0=top[:], in1=bottom[:], op=ALU.mult)
-            nc.gpsimd.memset(beta_row[:].bitcast(I32), 0)
-            nc.scalar.dma_start(out=beta_row[0:1, :], in_=ln_beta.unsqueeze(0))
-            nc.scalar.dma_start(out=bias_rows[:], in_=base_bias.partition_broadcast(P))
+            shape = [P, SETS, 3 * BASES + BASES - GPSIMD_LEFTS]
+            bottom_guess = head.tile(shape, F32)
+            nc.scalar.activation(out=bottom_guess[:], in_=bottom[:], func=ACT.Abs_reciprocal_sqrt)
+            inverse_root = head.tile(shape, F32)
+            refine_rsqrt(nc.gpsimd, head, inverse_root[:], bottom[:], bottom_guess[:], shape, "bottom")
+            nc.gpsimd.tensor_tensor(out=top[:], in0=top[:], in1=inverse_root[:], op=ALU.mult)
+            nc.gpsimd.tensor_tensor(out=weight[:], in0=top[:], in1=inverse_root[:], op=ALU.mult)
 
         with tc.tile_pool(name="work", bufs=1, reuse_waits="tile") as work:
 
@@ -262,65 +276,76 @@ def tile_kanlinear_pa_k_kernel(
                     nc.vector.scalar_tensor_tensor(
                         out=cubes[:, i, :],
                         in0=y_vector[:],
-                        scalar=minus_knots[:, s, i : i + 1],
+                        scalar=knots[:, s, i : i + 1],
                         in1=squares[i][:],
                         op0=ALU.add,
                         op1=ALU.mult,
                     )
                 return cubes
 
-            def cut(s, cubes, on_vector):
+            def cut(s, cubes, vector_lefts):
                 pieces = {}
-                for name, first, count, first_knot in (
-                    ("left_early", 0, GPSIMD_LEFTS, 1),
-                    ("left_late", GPSIMD_LEFTS, BASES - GPSIMD_LEFTS, 1),
-                    ("right_early", BASES, HALF, 3 - BASES),
-                    ("right_late", BASES + HALF, HALF, 3 - BASES),
+                for name, bases, first_knot, first_weight in (
+                    ("left_early", range(0, GPSIMD_LEFTS), 1, 0),
+                    ("left_late", range(GPSIMD_LEFTS, BASES), 1, 0),
+                    ("right_early", RATIO_RIGHTS[:3], 3, BASES),
+                    ("right_late", RATIO_RIGHTS[3:], 3, BASES),
                 ):
-                    piece = work.tile([P, count, ROWS], F32, name=name)
-                    for j in range(first, first + count):
+                    piece = work.tile([P, len(bases), ROWS], F32, name=name)
+                    for at, j in enumerate(bases):
                         source = cubes[:, j + first_knot, :]
-                        one_weight = weight[:, s, j : j + 1]
-                        if on_vector:
+                        one_weight = weight[:, s, first_weight + j : first_weight + j + 1]
+                        if vector_lefts and first_weight == 0:
                             nc.vector.tensor_scalar(
-                                out=piece[:, j - first, :],
-                                in0=source,
-                                scalar1=one_weight,
-                                scalar2=0.0,
-                                op0=ALU.mult,
-                                op1=ALU.max,
+                                out=piece[:, at, :], in0=source, scalar1=one_weight, scalar2=0.0, op0=ALU.mult, op1=ALU.max
                             )
                         else:
-                            nc.scalar.activation(
-                                out=piece[:, j - first, :], in_=source, func=ACT.Relu, scale=one_weight
-                            )
+                            nc.scalar.activation(out=piece[:, at, :], in_=source, func=ACT.Relu, scale=one_weight)
+                        pieces[first_weight + j] = piece[:, at, :]
                     pieces[name] = piece
                 return pieces
 
-            def merge_left(engine, left, cubes, pieces, bases, rows=slice(0, ROWS)):
-                for name, first in (("left_early", 0), ("left_late", GPSIMD_LEFTS)):
-                    own = slice(max(bases.start, first), min(bases.stop, first + pieces[name].shape[1]))
-                    if own.start < own.stop:
-                        engine.tensor_tensor(
-                            out=left[:, own, rows],
-                            in0=pieces[name][:, own.start - first : own.stop - first, rows],
-                            in1=cubes[:, own, rows],
-                            op=ALU.subtract,
-                        )
+            def merge_left_early(engine, left, cubes, pieces, rows=slice(0, ROWS)):
+                engine.tensor_tensor(
+                    out=left[:, 0:GPSIMD_LEFTS, rows],
+                    in0=pieces["left_early"][:, :, rows],
+                    in1=cubes[:, 0:GPSIMD_LEFTS, rows],
+                    op=ALU.add,
+                )
 
-            def merge_right(s, right, cubes, pieces, rows=slice(0, ROWS)):
-                for j in range(HALF):
+            def merge_left_late(s, left, cubes, pieces, rows=slice(0, ROWS)):
+                for j in range(GPSIMD_LEFTS, BASES):
+                    at = 3 * BASES + j - GPSIMD_LEFTS
                     nc.vector.scalar_tensor_tensor(
-                        out=right[:, j, rows],
-                        in0=cubes[:, j + HALF, rows],
-                        scalar=weight[:, s, 2 * BASES + j : 2 * BASES + j + 1],
-                        in1=pieces["right_early"][:, j, rows],
+                        out=left[:, j, rows],
+                        in0=cubes[:, j, rows],
+                        scalar=weight[:, s, at : at + 1],
+                        in1=pieces[j][:, rows],
                         op0=ALU.mult,
                         op1=ALU.add,
                     )
-                nc.vector.tensor_tensor(
-                    out=right[:, HALF:, rows], in0=cubes[:, BASES:, rows], in1=pieces["right_late"][:, :, rows], op=ALU.add
-                )
+
+            def merge_right(s, right, cubes, pieces, rows=slice(0, ROWS)):
+                for j in range(BASES):
+                    if j in RATIO_RIGHTS:
+                        at = 2 * BASES + j
+                        nc.vector.scalar_tensor_tensor(
+                            out=right[:, j, rows],
+                            in0=cubes[:, j + 4, rows],
+                            scalar=weight[:, s, at : at + 1],
+                            in1=pieces[BASES + j][:, rows],
+                            op0=ALU.mult,
+                            op1=ALU.add,
+                        )
+                    else:
+                        nc.vector.scalar_tensor_tensor(
+                            out=right[:, j, rows],
+                            in0=cubes[:, j + 3, rows],
+                            scalar=0.0,
+                            in1=cubes[:, j + 4, rows],
+                            op0=ALU.max,
+                            op1=ALU.subtract,
+                        )
 
             def planes(tile_slice):
                 return tile_slice.rearrange("p t (c i) -> p c t i", i=4)
@@ -375,17 +400,16 @@ def tile_kanlinear_pa_k_kernel(
                         stop=(scale_row == BASE_PASSES + GROUPS - 1),
                     )
 
-            def multiply_set(s, groups, row_tiles=range(ROW_TILES)):
-                for b in range(2):
-                    multiply(groups[b], w_of[2 * s + b], BASE_PASSES + 2 * s + b, row_tiles)
+            def multiply_group(g, values, row_tiles=range(ROW_TILES)):
+                multiply(values, w_of[g], BASE_PASSES + g, row_tiles)
 
             def relu_step(g, r, grouped):
-                xn = turned.tile([P, PACK, P], F32, name="xn", tag="for_scalar")
+                minus_xn = turned.tile([P, PACK, P], F32, name="minus_xn", tag="for_scalar")
                 y_by_slot = y_rows[r][:].rearrange("n (g p t) -> n g t p", g=BASE_PASSES, t=PACK)
                 beta_by_slot = beta_row[:].rearrange("n (g p t) -> n g t p", g=BASE_PASSES, t=PACK)
                 for t in range(PACK):
                     nc.tensor.matmul(
-                        out=xn[:, t, :],
+                        out=minus_xn[:, t, :],
                         lhsT=y_by_slot[:, g, t, :],
                         rhs=ident_f32[:],
                         is_transpose=True,
@@ -393,10 +417,10 @@ def tile_kanlinear_pa_k_kernel(
                         stop=False,
                     )
                     nc.tensor.matmul(
-                        out=xn[:, t, :], lhsT=beta_by_slot[:, g, t, :], rhs=ones[:], start=False, stop=True
+                        out=minus_xn[:, t, :], lhsT=beta_by_slot[:, g, t, :], rhs=minus_ones[:], start=False, stop=True
                     )
                 nc.scalar.activation(
-                    out=grouped[:, r * P : (r + 1) * P, :], in_=xn[:].rearrange("p t n -> p n t"), func=ACT.Relu
+                    out=grouped[:, r * P : (r + 1) * P, :], in_=minus_xn[:].rearrange("p t n -> p n t"), func=ACT.Relu, scale=-1.0
                 )
 
             def store(row_tiles):
@@ -418,7 +442,7 @@ def tile_kanlinear_pa_k_kernel(
                     last = s == SETS - 1
                     left = work.tile([P, BASES, ROWS], BF16, name="left")
                     if not last:
-                        merge_left(nc.gpsimd, left, cubes_of[s], pieces_of[s], slice(0, GPSIMD_LEFTS))
+                        merge_left_early(nc.gpsimd, left, cubes_of[s], pieces_of[s])
                     if s + 2 < SETS:
                         y_of[s + 2] = turn(s + 2)
                         squares_of[s + 2] = square(s + 2, y_of[s + 2][0])
@@ -426,16 +450,14 @@ def tile_kanlinear_pa_k_kernel(
                         cubes_of[s + 1] = cube(s + 1, y_of[s + 1][1], squares_of[s + 1])
                     right = work.tile([P, BASES, ROWS], BF16, name="right")
                     if not last:
-                        merge_left(nc.vector, left, cubes_of[s], pieces_of[s], slice(GPSIMD_LEFTS, BASES))
+                        merge_left_late(s, left, cubes_of[s], pieces_of[s])
                         merge_right(s, right, cubes_of[s], pieces_of[s])
                         pieces_of[s + 1] = cut(s + 1, cubes_of[s + 1], False)
                     if 0 < s < SETS - 1:
                         for values, branch in relu_ready:
                             multiply(values, load_weights(base_weight_words[branch]), branch)
                         relu_ready = []
-                        multiply_set(s - 1, groups_of[s - 1])
-                        for g in (2 * s + 2, 2 * s + 3):
-                            w_of[g] = load_weights(spline_weight_words[g])
+                        multiply_group(2 * s - 2, groups_of[s - 1][0])
                     if s < RELU_ROUNDS:
                         steps = BASE_PASSES * ROW_TILES
                         for step in range(steps * s // RELU_ROUNDS, steps * (s + 1) // RELU_ROUNDS):
@@ -450,27 +472,30 @@ def tile_kanlinear_pa_k_kernel(
                     if not last:
                         low = pick(0, left, right)
                         high = pick(1, left, right)
-                        if s + 2 < SETS:
-                            regroup(low, basis, 0, slice(0, ROWS // 2), True)
-                            regroup(low, basis, 0, slice(ROWS // 2, ROWS), False)
-                            regroup(high, basis, 1, slice(0, ROWS), False)
-                        else:
-                            regroup(low, basis, 0, slice(0, ROWS), True)
-                            regroup(high, basis, 1, slice(0, ROWS), False)
+                        if s > 0:
+                            multiply_group(2 * s - 1, groups_of[s - 1][1])
+                        regroup(low, basis, 0, slice(0, ROWS), True)
+                        regroup(high, basis, 1, slice(0, ROWS), False)
                         for h in range(2):
                             pair_up(basis, groups_of[s], h, slice(0, ROWS))
+                        if s > 0:
+                            for g in (2 * s + 2, 2 * s + 3):
+                                w_of[g] = load_weights(spline_weight_words[g])
                 s = SETS - 1
                 waiting = (s - 1, range(ROW_TILES))
                 for row_tiles in (range(0, 2), range(2, ROW_TILES)):
                     rows = slice(row_tiles.start * P, row_tiles.stop * P)
-                    merge_left(nc.vector, left, cubes_of[s], pieces_of[s], slice(0, BASES), rows)
+                    merge_left_early(nc.vector, left, cubes_of[s], pieces_of[s], rows)
+                    merge_left_late(s, left, cubes_of[s], pieces_of[s], rows)
                     merge_right(s, right, cubes_of[s], pieces_of[s], rows)
-                    multiply_set(waiting[0], groups_of[waiting[0]], waiting[1])
+                    for b in range(2):
+                        multiply_group(2 * waiting[0] + b, groups_of[waiting[0]][b], waiting[1])
                     waiting = (s, row_tiles)
                     for h in range(2):
                         on_scalar = h == 0 or row_tiles.stop < ROW_TILES
                         regroup(pick(h, left, right, rows), basis, h, rows, on_scalar)
                         pair_up(basis, groups_of[s], h, rows)
                 store(range(0, 2))
-                multiply_set(s, groups_of[s], waiting[1])
+                for b in range(2):
+                    multiply_group(2 * s + b, groups_of[s][b], waiting[1])
                 store(range(2, ROW_TILES))

import concourse.mybir as mybir
from concourse.masks import make_identity

F32 = mybir.dt.float32
BF16 = mybir.dt.bfloat16
I32 = mybir.dt.int32
U32 = mybir.dt.uint32
U8 = mybir.dt.uint8
FP8X4 = mybir.dt.float8_e4m3fn_x4
ALU = mybir.AluOpType
ACT = mybir.ActivationFunctionType

P = 128
ROWS = 512
ROW_TILES = ROWS // P
FEATURES = 2048
UNITS = 512
PACK = 4
K_PASS = P * PACK
BASES = 8
KNOTS = 12
HALF = 4
SETS = FEATURES // P
BASE_PASSES = FEATURES // K_PASS
GROUPS = FEATURES * BASES // K_PASS
BANK = 512
WORD_BYTES = PACK * UNITS
RATIO_RIGHTS = (0, 1, 2, 4, 6)
GPSIMD_LEFTS = 6
RELU_ROUNDS = 14
LN_EPS = 0.001

FLOPS = 2 * ROWS * (FEATURES + FEATURES * BASES) * UNITS


def refine_rsqrt(engine, pool, result, value, guess, shape, label):
    step = pool.tile(shape, F32, name=label + "_step")
    engine.tensor_tensor(out=step[:], in0=value, in1=guess, op=ALU.mult)
    engine.tensor_tensor(out=step[:], in0=step[:], in1=guess, op=ALU.mult)
    engine.tensor_scalar(out=step[:], in0=step[:], scalar1=-0.5, scalar2=1.5, op0=ALU.mult, op1=ALU.add)
    engine.tensor_tensor(out=result, in0=guess, in1=step[:], op=ALU.mult)


def tile_kanlinear_pa_k_kernel(
    tc,
    x,
    ln_gamma,
    ln_beta,
    base_weight_words,
    base_weight_scales,
    base_bias,
    spline_weight_words,
    spline_weight_scales,
    grid,
    out,
):
    nc = tc.nc
    with tc.tile_pool(name="keep", bufs=1) as keep, tc.tile_pool(name="squares", bufs=KNOTS + 4) as square_pool, tc.tile_pool(
        name="weights", bufs=5
    ) as weights, tc.psum_pool(
        name="sums", bufs=1
    ) as sums, tc.psum_pool(name="turned", bufs=2) as turned:
        ident_f32 = keep.tile([P, P], F32)
        ident_bf16 = keep.tile([P, P], BF16)
        scale_planes = keep.tile([P, BASE_PASSES + GROUPS, UNITS], U8, align_bytes=64)
        y_rows = [keep.tile([P, FEATURES], F32, name="y_rows%d" % r) for r in range(ROW_TILES)]
        knots = keep.tile([P, SETS, KNOTS], F32)
        slope = keep.tile([P, SETS, KNOTS], F32)
        shift = keep.tile([P, SETS, KNOTS], F32)
        weight = keep.tile([P, SETS, 3 * BASES + BASES - GPSIMD_LEFTS], F32)
        bias_rows = keep.tile([P, UNITS], BF16)
        minus_ones = keep.tile([P, P], BF16)
        beta_row = keep.tile([P, FEATURES], BF16)
        acc = [sums.tile([P, UNITS], F32, name="acc%d" % r) for r in range(ROW_TILES)]

        with tc.tile_pool(name="head", bufs=1) as head, tc.tile_pool(name="head2", bufs=2) as head2, tc.manual_schedule():
            x_rows = [head.tile([P, FEATURES], BF16, name="x_rows%d" % r) for r in range(ROW_TILES)]
            gamma_row = head.tile([P, FEATURES], BF16)
            set_rows = head.tile([P, P * KNOTS], BF16)
            beta_rows = head.tile([P, P], BF16)
            for r in (0, 2, 1, 3):
                nc.sync.dma_start(out=x_rows[r][:], in_=x[r * P : (r + 1) * P, :])
            first = head.tile([P, 1], F32)
            nc.vector.memset(first[:], 1.0)
            nc.scalar.activation(out=first[:], in_=first[:], func=ACT.Abs_reciprocal_sqrt)
            nc.vector.memset(set_rows[:], 0.0)
            nc.scalar.dma_start(out=set_rows[0:SETS, :], in_=grid[0].rearrange("(s f) i -> s (f i)", f=P))
            nc.vector.memset(beta_rows[:], 0.0)
            nc.scalar.dma_start(out=beta_rows[0:SETS, :], in_=ln_beta.rearrange("(s f) -> s f", f=P))
            nc.vector.memset(gamma_row[:], 0.0)
            nc.scalar.dma_start(out=gamma_row[0:1, :], in_=ln_gamma.unsqueeze(0))
            nc.gpsimd.memset(minus_ones[:], -1.0)
            make_identity(nc, ident_bf16[:])
            make_identity(nc, ident_f32[:])
            nc.gpsimd.memset(beta_row[:].bitcast(I32), 0)
            nc.gpsimd.memset(scale_planes[:].bitcast(I32), 0)
            nc.sync.dma_start(out=beta_row[0:1, :], in_=ln_beta.unsqueeze(0))
            nc.sync.dma_start(out=bias_rows[:], in_=base_bias.partition_broadcast(P))

            turned_knots = acc[0][:].bitcast(BF16).rearrange("p (i s) -> p i s", s=P)
            turned_late = acc[1][:].bitcast(BF16).rearrange("p (i s) -> p i s", s=P)
            by_knot = set_rows[:].rearrange("s (f i) -> s i f", i=KNOTS)
            for i in range(KNOTS):
                nc.tensor.transpose(
                    turned_knots[:, i, :] if i < 8 else turned_late[:, i - 8, :], by_knot[:, i, :], ident_bf16[:]
                )
            nc.tensor.transpose(turned_late[:, 4, :], beta_rows[:], ident_bf16[:])

            gamma_banks = []
            for c in range(FEATURES // BANK):
                bank = turned.tile([P, BANK], F32, name="gamma_bank", tag="for_scalar" if c % 2 == 0 else "for_vector")
                nc.tensor.matmul(
                    out=bank[:], lhsT=minus_ones[:], rhs=gamma_row[:, c * BANK : (c + 1) * BANK], start=True, stop=True
                )
                gamma_banks.append(bank)

            minus_mean = head.tile([P, 2], F32)
            squared = head.tile([P, 2], F32)
            unused = head.tile([P, FEATURES], BF16)
            for r in range(2):
                column = slice(r, r + 1)
                nc.scalar.activation(
                    out=unused[:], in_=x_rows[r][:], func=ACT.Copy, scale=-1.0 / FEATURES, accum_out=minus_mean[:, column]
                )
                nc.scalar.activation(
                    out=unused[:], in_=x_rows[r][:], func=ACT.Square, bias=minus_mean[:, column], accum_out=squared[:, column]
                )
            moments = head.tile([P, ROW_TILES, 2], F32)
            spread = head.tile([P, ROW_TILES], F32)
            guess = head.tile([P, ROW_TILES], F32)
            rstd = head.tile([P, ROW_TILES], F32)

            def statistics(r):
                chunks = head2.tile([P, 4, 6], F32, name="chunks")
                for c in range(4):
                    nc.vector.bn_stats(out=chunks[:, c, :], in_=x_rows[r][:, c * 512 : (c + 1) * 512])
                nc.vector.bn_aggr(out=moments[:, r, :], in_=chunks[:].rearrange("p c s -> p (c s)"))

            def centre(r):
                centred = head.tile([P, FEATURES], F32, name="centred%d" % r)
                for c in range(FEATURES // BANK):
                    columns = slice(c * BANK, (c + 1) * BANK)
                    nc.vector.scalar_tensor_tensor(
                        out=centred[:, columns],
                        in0=x_rows[r][:, columns],
                        scalar=minus_mean[:, r : r + 1] if r < 2 else moments[:, r, 0:1],
                        in1=gamma_banks[c][:],
                        op0=ALU.add if r < 2 else ALU.subtract,
                        op1=ALU.mult,
                    )
                return centred

            statistics(2)
            plain_knots = head.tile([P, SETS, KNOTS], F32)
            nc.vector.tensor_copy(out=plain_knots[:, :, 0:8], in_=turned_knots[:, :, 0:SETS].rearrange("p i s -> p s i"))
            nc.vector.tensor_copy(out=plain_knots[:, :, 8:], in_=turned_late[:, 0:4, 0:SETS].rearrange("p i s -> p s i"))
            beta_column = head.tile([P, SETS], F32)
            nc.vector.tensor_copy(out=beta_column[:], in_=turned_late[:, 4, 0:SETS])
            statistics(3)
            centred = {0: centre(0)}
            gap = {span: head.tile([P, SETS, KNOTS - span], F32, name="gap%d" % span) for span in (1, 2, 3, 4)}
            for span in gap:
                nc.gpsimd.tensor_tensor(
                    out=gap[span][:], in0=plain_knots[:, :, span:], in1=plain_knots[:, :, 0 : KNOTS - span], op=ALU.subtract
                )
            one_by_gap = head.tile([P, SETS, 3], F32)
            nc.vector.reciprocal(out=one_by_gap[:], in_=gap[4][:, :, 3::2])
            nc.vector.tensor_scalar(
                out=spread[:, 0:2], in0=squared[:], scalar1=1.0 / FEATURES, scalar2=LN_EPS, op0=ALU.mult, op1=ALU.add
            )
            nc.vector.tensor_scalar_add(out=spread[:, 2:], in0=moments[:, 2:, 1], scalar1=LN_EPS)
            nc.scalar.activation(out=guess[:], in_=spread[:], func=ACT.Abs_reciprocal_sqrt)
            centred[1] = centre(1)
            refine_rsqrt(nc.vector, head, rstd[:], spread[:], guess[:], [P, ROW_TILES], "rstd")
            centred[2] = centre(2)
            centred[3] = centre(3)

            rise = head.tile([P, SETS, 9], F32)
            nc.gpsimd.tensor_tensor(out=rise[:], in0=gap[1][:, :, 0:9], in1=gap[2][:, :, 0:9], op=ALU.mult)
            nc.gpsimd.tensor_tensor(out=rise[:], in0=rise[:], in1=gap[3][:], op=ALU.mult)
            fall = head.tile([P, SETS, 9], F32)
            nc.gpsimd.tensor_tensor(out=fall[:], in0=gap[1][:, :, 2:11], in1=gap[2][:, :, 1:10], op=ALU.mult)
            nc.gpsimd.tensor_tensor(out=fall[:], in0=fall[:], in1=gap[3][:], op=ALU.mult)
            volume = head.tile([P, SETS, KNOTS], F32)
            nc.scalar.copy(out=volume[:, :, 0:6], in_=rise[:, :, 0:6])
            nc.scalar.copy(out=volume[:, :, 7::2], in_=fall[:, :, 4::2])
            inner_volume = head.tile([P, SETS, 3], F32)
            nc.gpsimd.tensor_tensor(out=inner_volume[:], in0=gap[1][:, :, 6::2], in1=fall[:, :, 3::2], op=ALU.mult)
            nc.gpsimd.tensor_tensor(out=volume[:, :, 6::2], in0=inner_volume[:], in1=one_by_gap[:], op=ALU.mult)
            slope_guess = head.tile([P, SETS, KNOTS], F32)
            nc.scalar.activation(out=slope_guess[:], in_=volume[:], func=ACT.Abs_reciprocal_sqrt)
            refine_rsqrt(nc.gpsimd, head, slope[:], volume[:], slope_guess[:], [P, SETS, KNOTS], "slope")
            nc.gpsimd.tensor_tensor(
                out=knots[:],
                in0=plain_knots[:],
                in1=beta_column[:].unsqueeze(2).to_broadcast([P, SETS, KNOTS]),
                op=ALU.subtract,
            )
            nc.gpsimd.tensor_tensor(out=shift[:], in0=slope[:], in1=knots[:], op=ALU.mult)
            top = head.tile([P, SETS, 3 * BASES + BASES - GPSIMD_LEFTS], F32)
            bottom = head.tile([P, SETS, 3 * BASES + BASES - GPSIMD_LEFTS], F32)
            lefts, rights = slice(0, BASES), slice(BASES, 2 * BASES)
            right_outers, left_outers = slice(2 * BASES, 3 * BASES), slice(3 * BASES, None)
            nc.gpsimd.tensor_tensor(out=top[:, :, lefts], in0=gap[4][:], in1=volume[:, :, 1:9], op=ALU.mult)
            nc.gpsimd.tensor_scalar(
                out=top[:, :, lefts], in0=top[:, :, lefts], scalar1=-1.0, scalar2=0.0, op0=ALU.mult, op1=ALU.add
            )
            nc.gpsimd.tensor_tensor(out=bottom[:, :, lefts], in0=gap[1][:, :, 0:8], in1=rise[:, :, 1:9], op=ALU.mult)
            nc.gpsimd.tensor_tensor(out=top[:, :, rights], in0=gap[4][:], in1=volume[:, :, 3:11], op=ALU.mult)
            nc.gpsimd.tensor_tensor(out=bottom[:, :, rights], in0=gap[1][:, :, 3:11], in1=fall[:, :, 0:8], op=ALU.mult)
            nc.gpsimd.tensor_scalar(
                out=top[:, :, right_outers], in0=volume[:, :, 4:], scalar1=-1.0, scalar2=0.0, op0=ALU.mult, op1=ALU.add
            )
            nc.scalar.copy(out=bottom[:, :, right_outers], in_=fall[:, :, 1:9])
            nc.scalar.copy(out=top[:, :, left_outers], in_=volume[:, :, GPSIMD_LEFTS:BASES])
            nc.scalar.copy(out=bottom[:, :, left_outers], in_=rise[:, :, GPSIMD_LEFTS:BASES])

            for r in range(2):
                nc.scalar.activation(out=y_rows[r][:], in_=centred[r][:], func=ACT.Copy, scale=rstd[:, r : r + 1])
            for r in range(2, ROW_TILES):
                nc.vector.tensor_scalar_mul(out=y_rows[r][:], in0=centred[r][:], scalar1=rstd[:, r : r + 1])
            shape = [P, SETS, 3 * BASES + BASES - GPSIMD_LEFTS]
            bottom_guess = head.tile(shape, F32)
            nc.scalar.activation(out=bottom_guess[:], in_=bottom[:], func=ACT.Abs_reciprocal_sqrt)
            inverse_root = head.tile(shape, F32)
            refine_rsqrt(nc.gpsimd, head, inverse_root[:], bottom[:], bottom_guess[:], shape, "bottom")
            nc.gpsimd.tensor_tensor(out=top[:], in0=top[:], in1=inverse_root[:], op=ALU.mult)
            nc.gpsimd.tensor_tensor(out=weight[:], in0=top[:], in1=inverse_root[:], op=ALU.mult)

        with tc.tile_pool(name="work", bufs=1, reuse_waits="tile") as work:

            def load_scales():
                for q in range(4):
                    nc.sync.dma_start(
                        out=scale_planes[32 * q : 32 * q + 4, 0:BASE_PASSES, :].bitcast(I32),
                        in_=base_weight_scales[:, 4 * q : 4 * q + 4, :].rearrange("g r n -> r g n").bitcast(I32),
                    )
                    nc.sync.dma_start(
                        out=scale_planes[32 * q : 32 * q + 4, BASE_PASSES:, :].bitcast(I32),
                        in_=spline_weight_scales[:, 4 * q : 4 * q + 4, :].rearrange("g r n -> r g n").bitcast(I32),
                    )

            def load_weights(words_of_pass):
                w_words = weights.tile([P, WORD_BYTES], U8, name="w_words", align_bytes=64)
                nc.sync.dma_start(
                    out=w_words[:].bitcast(I32), in_=words_of_pass.rearrange("p n t -> p (n t)").bitcast(I32)
                )
                return w_words

            def turn(s):
                banks = []
                for tag in ("for_scalar", "for_vector"):
                    bank = turned.tile([P, ROWS], F32, name="turned_y", tag=tag)
                    for r in range(ROW_TILES):
                        nc.tensor.transpose(bank[:, r * P : (r + 1) * P], y_rows[r][:, s * P : (s + 1) * P], ident_f32[:])
                    banks.append(bank)
                return banks

            def square(s, y_scalar):
                squares = []
                for i in range(KNOTS):
                    one = square_pool.tile([P, ROWS], F32, name="one")
                    nc.scalar.activation(
                        out=one[:],
                        in_=y_scalar[:],
                        func=ACT.Square,
                        scale=slope[:, s, i : i + 1],
                        bias=shift[:, s, i : i + 1],
                    )
                    squares.append(one)
                return squares

            def cube(s, y_vector, squares):
                cubes = work.tile([P, KNOTS, ROWS], F32, name="cubes", bufs=2)
                for i in range(KNOTS):
                    nc.vector.scalar_tensor_tensor(
                        out=cubes[:, i, :],
                        in0=y_vector[:],
                        scalar=knots[:, s, i : i + 1],
                        in1=squares[i][:],
                        op0=ALU.add,
                        op1=ALU.mult,
                    )
                return cubes

            def cut(s, cubes, vector_lefts):
                pieces = {}
                for name, bases, first_knot, first_weight in (
                    ("left_early", range(0, GPSIMD_LEFTS), 1, 0),
                    ("left_late", range(GPSIMD_LEFTS, BASES), 1, 0),
                    ("right_early", RATIO_RIGHTS[:3], 3, BASES),
                    ("right_late", RATIO_RIGHTS[3:], 3, BASES),
                ):
                    piece = work.tile([P, len(bases), ROWS], F32, name=name)
                    for at, j in enumerate(bases):
                        source = cubes[:, j + first_knot, :]
                        one_weight = weight[:, s, first_weight + j : first_weight + j + 1]
                        if vector_lefts and first_weight == 0:
                            nc.vector.tensor_scalar(
                                out=piece[:, at, :], in0=source, scalar1=one_weight, scalar2=0.0, op0=ALU.mult, op1=ALU.max
                            )
                        else:
                            nc.scalar.activation(out=piece[:, at, :], in_=source, func=ACT.Relu, scale=one_weight)
                        pieces[first_weight + j] = piece[:, at, :]
                    pieces[name] = piece
                return pieces

            def merge_left_early(engine, left, cubes, pieces, rows=slice(0, ROWS)):
                engine.tensor_tensor(
                    out=left[:, 0:GPSIMD_LEFTS, rows],
                    in0=pieces["left_early"][:, :, rows],
                    in1=cubes[:, 0:GPSIMD_LEFTS, rows],
                    op=ALU.add,
                )

            def merge_left_late(s, left, cubes, pieces, rows=slice(0, ROWS)):
                for j in range(GPSIMD_LEFTS, BASES):
                    at = 3 * BASES + j - GPSIMD_LEFTS
                    nc.vector.scalar_tensor_tensor(
                        out=left[:, j, rows],
                        in0=cubes[:, j, rows],
                        scalar=weight[:, s, at : at + 1],
                        in1=pieces[j][:, rows],
                        op0=ALU.mult,
                        op1=ALU.add,
                    )

            def merge_right(s, right, cubes, pieces, rows=slice(0, ROWS)):
                for j in range(BASES):
                    if j in RATIO_RIGHTS:
                        at = 2 * BASES + j
                        nc.vector.scalar_tensor_tensor(
                            out=right[:, j, rows],
                            in0=cubes[:, j + 4, rows],
                            scalar=weight[:, s, at : at + 1],
                            in1=pieces[BASES + j][:, rows],
                            op0=ALU.mult,
                            op1=ALU.add,
                        )
                    else:
                        nc.vector.scalar_tensor_tensor(
                            out=right[:, j, rows],
                            in0=cubes[:, j + 3, rows],
                            scalar=0.0,
                            in1=cubes[:, j + 4, rows],
                            op0=ALU.max,
                            op1=ALU.subtract,
                        )

            def planes(tile_slice):
                return tile_slice.rearrange("p t (c i) -> p c t i", i=4)

            def words(tile_slice):
                return tile_slice.rearrange("p (c i) t -> p c t i", i=4)

            def pick(h, left, right, rows=slice(0, ROWS)):
                bases = slice(HALF * h, HALF * h + HALF)
                picked = (right, left)[h]
                nc.vector.tensor_tensor(
                    out=picked[:, bases, rows], in0=left[:, bases, rows], in1=right[:, bases, rows], op=ALU.min
                )
                return picked[:, bases, :]

            def regroup(picked, basis, h, rows, on_scalar):
                target = words(basis[:, h, rows, :])
                source = planes(picked[:, :, rows])
                if on_scalar:
                    nc.scalar.activation(out=target, in_=source, func=ACT.Relu, scale=-1.0)
                else:
                    nc.vector.tensor_scalar(
                        out=target, in0=source, scalar1=-1.0, scalar2=0.0, op0=ALU.mult, op1=ALU.max
                    )

            def pair_up(basis, groups, h, rows):
                for b in range(2):
                    nc.sync.dma_start(
                        out=groups[b][h:P:2, rows, :], in_=basis[P // 2 * b : P // 2 * (b + 1), h, rows, :]
                    )

            def new_groups():
                return [work.tile([P, ROWS, HALF], BF16, name="group", align_bytes=64, bufs=4) for b in range(2)]

            def multiply(values, w_words, scale_row, row_tiles=range(ROW_TILES)):
                rows = slice(row_tiles.start * P, row_tiles.stop * P)
                codes = work.tile([P, ROWS], U32, name="codes", align_bytes=64, bufs=3)
                scales = work.tile([P, ROWS], U8, name="scales", align_bytes=64, bufs=3)
                nc.vector.quantize_mx(
                    out=codes[:, rows].bitcast(FP8X4),
                    scales=scales[:, rows],
                    in_=values[:, rows, :].rearrange("p n t -> p (n t)"),
                )
                for r in row_tiles:
                    nc.tensor.matmul_mx(
                        out=acc[r][:],
                        lhsT=codes[:, r * P : (r + 1) * P].bitcast(FP8X4),
                        lhsT_scale=scales[:, r * P : (r + 1) * P],
                        rhs=w_words[:].bitcast(FP8X4),
                        rhs_scale=scale_planes[:, scale_row, :],
                        start=(scale_row == BASE_PASSES),
                        stop=(scale_row == BASE_PASSES + GROUPS - 1),
                    )

            def multiply_group(g, values, row_tiles=range(ROW_TILES)):
                multiply(values, w_of[g], BASE_PASSES + g, row_tiles)

            def relu_step(g, r, grouped):
                minus_xn = turned.tile([P, PACK, P], F32, name="minus_xn", tag="for_scalar")
                y_by_slot = y_rows[r][:].rearrange("n (g p t) -> n g t p", g=BASE_PASSES, t=PACK)
                beta_by_slot = beta_row[:].rearrange("n (g p t) -> n g t p", g=BASE_PASSES, t=PACK)
                for t in range(PACK):
                    nc.tensor.matmul(
                        out=minus_xn[:, t, :],
                        lhsT=y_by_slot[:, g, t, :],
                        rhs=ident_f32[:],
                        is_transpose=True,
                        start=True,
                        stop=False,
                    )
                    nc.tensor.matmul(
                        out=minus_xn[:, t, :], lhsT=beta_by_slot[:, g, t, :], rhs=minus_ones[:], start=False, stop=True
                    )
                nc.scalar.activation(
                    out=grouped[:, r * P : (r + 1) * P, :], in_=minus_xn[:].rearrange("p t n -> p n t"), func=ACT.Relu, scale=-1.0
                )

            def store(row_tiles):
                for r in row_tiles:
                    result = work.tile([P, UNITS], F32, name="result", bufs=2)
                    nc.vector.tensor_tensor(out=result[:], in0=acc[r][:], in1=bias_rows[:], op=ALU.add)
                    nc.sync.dma_start(out=out[r * P : (r + 1) * P, :], in_=result[:])

            with tc.manual_schedule():
                w_of = {g: load_weights(spline_weight_words[g]) for g in range(4)}
                load_scales()
                y_of = {0: turn(0), 1: turn(1)}
                squares_of = {0: square(0, y_of[0][0]), 1: square(1, y_of[1][0])}
                cubes_of = {0: cube(0, y_of[0][1], squares_of[0])}
                pieces_of = {0: cut(0, cubes_of[0], True)}
                groups_of = {}
                relu_ready = []
                for s in range(SETS):
                    last = s == SETS - 1
                    left = work.tile([P, BASES, ROWS], BF16, name="left")
                    if not last:
                        merge_left_early(nc.gpsimd, left, cubes_of[s], pieces_of[s])
                    if s + 2 < SETS:
                        y_of[s + 2] = turn(s + 2)
                        squares_of[s + 2] = square(s + 2, y_of[s + 2][0])
                    if not last:
                        cubes_of[s + 1] = cube(s + 1, y_of[s + 1][1], squares_of[s + 1])
                    right = work.tile([P, BASES, ROWS], BF16, name="right")
                    if not last:
                        merge_left_late(s, left, cubes_of[s], pieces_of[s])
                        merge_right(s, right, cubes_of[s], pieces_of[s])
                        pieces_of[s + 1] = cut(s + 1, cubes_of[s + 1], False)
                    if 0 < s < SETS - 1:
                        for values, branch in relu_ready:
                            multiply(values, load_weights(base_weight_words[branch]), branch)
                        relu_ready = []
                        multiply_group(2 * s - 2, groups_of[s - 1][0])
                    if s < RELU_ROUNDS:
                        steps = BASE_PASSES * ROW_TILES
                        for step in range(steps * s // RELU_ROUNDS, steps * (s + 1) // RELU_ROUNDS):
                            branch, r = step // ROW_TILES, step % ROW_TILES
                            if r == 0:
                                grouped = work.tile([P, ROWS, PACK], BF16, name="grouped", align_bytes=64)
                            relu_step(branch, r, grouped)
                            if r == ROW_TILES - 1:
                                relu_ready.append((grouped, branch))
                    basis = work.tile([P, 2, ROWS, HALF], BF16, name="basis", align_bytes=64, bufs=2)
                    groups_of[s] = new_groups()
                    if not last:
                        low = pick(0, left, right)
                        high = pick(1, left, right)
                        if s > 0:
                            multiply_group(2 * s - 1, groups_of[s - 1][1])
                        regroup(low, basis, 0, slice(0, ROWS), True)
                        regroup(high, basis, 1, slice(0, ROWS), False)
                        for h in range(2):
                            pair_up(basis, groups_of[s], h, slice(0, ROWS))
                        if s > 0:
                            for g in (2 * s + 2, 2 * s + 3):
                                w_of[g] = load_weights(spline_weight_words[g])
                s = SETS - 1
                waiting = (s - 1, range(ROW_TILES))
                for row_tiles in (range(0, 2), range(2, ROW_TILES)):
                    rows = slice(row_tiles.start * P, row_tiles.stop * P)
                    merge_left_early(nc.vector, left, cubes_of[s], pieces_of[s], rows)
                    merge_left_late(s, left, cubes_of[s], pieces_of[s], rows)
                    merge_right(s, right, cubes_of[s], pieces_of[s], rows)
                    for b in range(2):
                        multiply_group(2 * waiting[0] + b, groups_of[waiting[0]][b], waiting[1])
                    waiting = (s, row_tiles)
                    for h in range(2):
                        on_scalar = h == 0 or row_tiles.stop < ROW_TILES
                        regroup(pick(h, left, right, rows), basis, h, rows, on_scalar)
                        pair_up(basis, groups_of[s], h, rows)
                store(range(0, 2))
                for b in range(2):
                    multiply_group(2 * s + b, groups_of[s][b], waiting[1])
                store(range(2, ROW_TILES))
